import numpy as np
import ml_dtypes


def mxq(x, axis, fmt="e4m3"):
    dtype, down = {"e4m3": (ml_dtypes.float8_e4m3fn, 7), "e5m2": (ml_dtypes.float8_e5m2, 14)}[fmt]
    v = np.moveaxis(np.asarray(x, np.float32).astype(ml_dtypes.bfloat16).astype(np.float64), axis, -1)
    blocks = v.reshape(v.shape[:-1] + (-1, 32))
    amax = np.abs(blocks).max(-1, keepdims=True)
    byte = np.maximum(np.where(amax > 0, np.frexp(amax)[1] - 1 + 127, 0) - down, 1)
    scale = np.exp2(byte - 127.0)
    codes = (blocks / scale).astype(np.float32).astype(dtype).astype(np.float64)
    return np.moveaxis((codes * scale).reshape(v.shape), -1, axis)


WIDE = False


def mx_kscale(k):
    if not WIDE:
        return np.ones(k)
    levels = np.array([10, -10, 5, -5, 0])
    a = np.random.permutation(np.resize(levels, k // 512 * 4)).reshape(k // 512, 4)
    idx = np.arange(k)
    return np.exp2(a[idx // 512, idx % 128 // 32])


BF16 = ml_dtypes.bfloat16


def bf(x):
    return np.asarray(x, np.float32).astype(BF16)


def f64(x):
    return np.asarray(x).astype(np.float64)


B, S, D_MODEL, N_HEADS, QK_ROPE, QK_NOPE, KV_LORA, V_DIM = 2, 2048, 1024, 2, 128, 128, 512, 128
RMS_EPS = 1.1920928955078125e-07
ROPE_BASE = 10000.0


def apply_rope(r):
    freqs = 1.0 / (ROPE_BASE ** (np.arange(0, QK_ROPE, 2) / QK_ROPE))
    t = np.arange(S)[:, None] * freqs[None, :]
    cos = np.cos(t)[None, :, None, :]
    sin = np.sin(t)[None, :, None, :]
    r1 = r[..., 0::2]
    r2 = r[..., 1::2]
    return np.stack([r1 * cos - r2 * sin, r2 * cos + r1 * sin], axis=-1).reshape(r.shape)


def setup_inputs():
    s, t = mx_kscale(D_MODEL), mx_kscale(KV_LORA)
    return {"x": bf(np.random.standard_normal((B, S, D_MODEL)) * s),
            "Wkv_a": bf(np.random.standard_normal((D_MODEL, KV_LORA + QK_ROPE)) / np.sqrt(D_MODEL) / s[:, None]),
            "kv_norm_w": bf((1.0 + 0.1 * np.random.standard_normal(KV_LORA)) * t),
            "Wkv_b": bf(np.random.standard_normal((KV_LORA, N_HEADS * (QK_NOPE + V_DIM))) / np.sqrt(KV_LORA) / t[:, None])}


def reference(x, Wkv_a, kv_norm_w, Wkv_b):
    kv = mxq(f64(x), 2, "e4m3") @ mxq(f64(Wkv_a), 0, "e4m3")
    c_kv, k_rope = kv[..., :KV_LORA], kv[..., KV_LORA:]
    k_rope = apply_rope(k_rope.reshape(B, S, 1, QK_ROPE))
    c_kv = c_kv * (1.0 / np.sqrt(np.mean(c_kv * c_kv, axis=-1, keepdims=True) + RMS_EPS)) * f64(kv_norm_w)
    kv = (mxq(c_kv, 2, "e4m3") @ mxq(f64(Wkv_b), 0, "e4m3")).reshape(B, S, N_HEADS, QK_NOPE + V_DIM)
    return kv[..., :QK_NOPE], kv[..., QK_NOPE:], k_rope

@@ -1,0 +1,376 @@
+import math
+from contextlib import ExitStack
+
+import concourse.bass as bass
+import concourse.mybir as mybir
+import concourse.tile as tile
+from concourse.masks import make_identity
+
+F32 = mybir.dt.float32
+BF16 = mybir.dt.bfloat16
+I32 = mybir.dt.int32
+U32 = mybir.dt.uint32
+U8 = mybir.dt.uint8
+FP8X4 = mybir.dt.float8_e4m3fn_x4
+ALU = mybir.AluOpType
+ACT = mybir.ActivationFunctionType
+
+P = 128
+TOKENS = 4096
+D_MODEL = 1024
+LATENT = 512
+ROPE = 128
+KV_OUT = 512
+SEQ = 2048
+RMS_EPS = 1.1920928955078125e-07
+ROPE_BASE = 10000.0
+
+CHUNKS = 8
+PAIRS = 16
+X_EXTRA = 2
+ROPE_LAG = 2
+S_NCOPY = (5, 11)
+
+FLOPS = 2 * TOKENS * D_MODEL * (LATENT + ROPE) + 2 * TOKENS * LATENT * KV_OUT
+
+
+def tile_multiheadlatentattention_pa_t_kernel(tc, x, Wkv_a, kv_norm_w, Wkv_b, out_0, out_1, out_2):
+    nc = tc.nc
+    xv = x.rearrange("b s k -> (b s) k").rearrange("(c p j) k -> c p (j k)", p=P, j=4)
+    o0v = out_0.rearrange("b s h d -> (b s) (h d)").rearrange("(c p j) n -> c p j n", p=P, j=4)
+    o1v = out_1.rearrange("b s h d -> (b s) (h d)").rearrange("(c p j) n -> c p j n", p=P, j=4)
+    o2v = out_2.rearrange("b s h d -> (b s) (h d)").rearrange("(c p j) n -> c p (j n)", p=P, j=4)
+    wav = Wkv_a.rearrange("(a q e) n -> q a (e n)", a=4, q=P, e=2)
+    wbv = Wkv_b.rearrange("(t p) n -> p t n", t=4, p=P)
+
+    with ExitStack() as ctx:
+        const = ctx.enter_context(tc.tile_pool(name="const", bufs=1))
+        xgp = ctx.enter_context(tc.tile_pool(name="xgp", bufs=3))
+        small = ctx.enter_context(tc.tile_pool(name="small", bufs=4))
+        junkp = ctx.enter_context(tc.tile_pool(name="junkp", bufs=2))
+        nsp = ctx.enter_context(tc.tile_pool(name="nsp", bufs=3))
+        ngp = ctx.enter_context(tc.tile_pool(name="ngp", bufs=2))
+        ncp = ctx.enter_context(tc.tile_pool(name="ncp", bufs=3))
+        osp = ctx.enter_context(tc.tile_pool(name="osp", bufs=4))
+        rop = ctx.enter_context(tc.tile_pool(name="rop", bufs=2))
+        ps_xt = ctx.enter_context(tc.psum_pool(name="ps_xt", bufs=2))
+        ps_c = ctx.enter_context(tc.psum_pool(name="ps_c", bufs=3))
+        ps_nt = ctx.enter_context(tc.psum_pool(name="ps_nt", bufs=1))
+        ps_o = ctx.enter_context(tc.psum_pool(name="ps_o", bufs=1))
+        ps_r = ctx.enter_context(tc.psum_pool(name="ps_r", bufs=1))
+        ctx.enter_context(tc.manual_schedule())
+
+        x_sb = []
+        for c in range(CHUNKS):
+            x_sb.append(const.tile([P, 4096], BF16, name="x_sb%d" % c))
+        wa_raw = const.tile([P, 8, 640], BF16, name="wa_raw")
+        wb_raw = const.tile([P, 4, 512], BF16, name="wb_raw")
+        g_bf = const.tile([P, LATENT], BF16, name="g_bf")
+
+        def load_wa(g):
+            nc.sync.dma_start(
+                out=wa_raw[:, 4 * g : 4 * g + 4, :].rearrange("q (a e) n -> q a (e n)", a=2, e=2),
+                in_=wav[:, 2 * g : 2 * g + 2, :],
+            )
+
+        nc.scalar.dma_start(out=g_bf[:], in_=kv_norm_w.partition_broadcast(P))
+        load_wa(0)
+        nc.sync.dma_start(out=x_sb[0][:, 0:2048], in_=xv[0][:, 0:2048])
+        load_wa(1)
+        nc.sync.dma_start(out=x_sb[0][:, 2048:4096], in_=xv[0][:, 2048:4096])
+        nc.sync.dma_start(out=x_sb[1][:], in_=xv[1])
+        nc.sync.dma_start(out=wb_raw[:], in_=wbv)
+        for c in range(2, CHUNKS):
+            nc.sync.dma_start(out=x_sb[c][:], in_=xv[c])
+
+        pos_i = const.tile([P, 16], I32, name="pos_i")
+        nc.gpsimd.iota(pos_i[:], pattern=[[512, 4], [1, 4]], base=0, channel_multiplier=4)
+        ident_f = const.tile([P, P], F32, name="ident_f")
+        make_identity(nc, ident_f[:])
+        ident_b = const.tile([P, P], BF16, name="ident_b")
+        make_identity(nc, ident_b[:])
+        eps_t = const.tile([P, 1], F32, name="eps_t")
+        nc.vector.memset(eps_t[:], RMS_EPS)
+        warm = const.tile([P, 1], F32, name="warm")
+        nc.scalar.activation(out=warm[:], in_=eps_t[:], func=ACT.Sin)
+        mhalf = const.tile([P, 2], F32, name="mhalf")
+        nc.vector.memset(mhalf[:], -0.5)
+
+        pos_f = const.tile([P, 16], F32, name="pos_f")
+        nc.vector.tensor_copy(out=pos_f[:], in_=pos_i[:])
+        frq = const.tile([P, 64], F32, name="frq")
+        nc.vector.memset(frq[:, 0:1], 1.0)
+        nc.vector.tensor_scalar(out=frq[:, 0:1], in0=frq[:, 0:1], scalar1=1.0 / (2.0 * math.pi), scalar2=None, op0=ALU.mult)
+        ratio = ROPE_BASE ** (-1.0 / 64.0)
+        w = 1
+        while w < 64:
+            nc.vector.tensor_scalar(out=frq[:, w : 2 * w], in0=frq[:, 0:w], scalar1=ratio**w, scalar2=None, op0=ALU.mult)
+            w *= 2
+        turns = const.tile([P, 16, 64], F32, name="turns")
+        nc.vector.tensor_tensor(
+            out=turns[:],
+            in0=pos_f[:].unsqueeze(2).to_broadcast([P, 16, 64]),
+            in1=frq[:].unsqueeze(1).to_broadcast([P, 16, 64]),
+            op=ALU.mult,
+        )
+        whole = const.tile([P, 16, 64], I32, name="whole")
+        nc.vector.tensor_copy(out=whole[:], in_=turns[:])
+        sin_t = turns[:].rearrange("p a i -> p (a i)")
+        nc.vector.tensor_tensor(out=sin_t, in0=sin_t, in1=whole[:].rearrange("p a i -> p (a i)"), op=ALU.subtract)
+        cos_t = const.tile([P, 1024], F32, name="cos_t")
+
+        def tables_b():
+            nc.vector.tensor_scalar(out=cos_t[:], in0=sin_t, scalar1=0.25, scalar2=None, op0=ALU.add)
+            nc.vector.scalar_tensor_tensor(out=sin_t, in0=sin_t, scalar=0.5, in1=sin_t, op0=ALU.is_gt, op1=ALU.subtract)
+            nc.vector.scalar_tensor_tensor(out=cos_t[:], in0=cos_t[:], scalar=0.5, in1=cos_t[:], op0=ALU.is_gt, op1=ALU.subtract)
+
+        def rope_tables():
+            nc.scalar.activation(out=sin_t, in_=sin_t, func=ACT.Sin, scale=-2.0 * math.pi)
+            nc.scalar.activation(out=cos_t[:], in_=cos_t[:], func=ACT.Sin, scale=-2.0 * math.pi)
+
+        wag_c = const.tile([P, 2, 512, 4], BF16, name="wag_c", align_bytes=64)
+        wag_r = const.tile([P, 2, 128, 4], BF16, name="wag_r", align_bytes=64)
+        wac = const.tile([P, 2, 512], U32, name="wac", align_bytes=64)
+        was = const.tile([P, 2, 512], U8, name="was", align_bytes=64)
+        war = const.tile([P, 2, 128], U32, name="war", align_bytes=64)
+        wars = const.tile([P, 2, 128], U8, name="wars", align_bytes=64)
+        wbg = const.tile([P, 512, 4], BF16, name="wbg", align_bytes=64)
+        wbc = const.tile([P, 512], U32, name="wbc", align_bytes=64)
+        wbs = const.tile([P, 512], U8, name="wbs", align_bytes=64)
+
+        def wa_regroup(g):
+            nc.vector.tensor_copy(out=wag_c[:, g, :, :], in_=wa_raw[:, 4 * g : 4 * g + 4, 0:512].rearrange("q t n -> q n t"))
+
+        def wa_quant(g):
+            nc.vector.quantize_mx(
+                out=wac[:, g, :].bitcast(FP8X4), scales=was[:, g, :], in_=wag_c[:, g, :, :].rearrange("q n t -> q (n t)")
+            )
+
+        def war_regroup():
+            for g in range(2):
+                nc.scalar.copy(out=wag_r[:, g, :, :], in_=wa_raw[:, 4 * g : 4 * g + 4, 512:640].rearrange("q t n -> q n t"))
+
+        def war_quant():
+            for g in range(2):
+                nc.vector.quantize_mx(
+                    out=war[:, g, :].bitcast(FP8X4), scales=wars[:, g, :], in_=wag_r[:, g, :, :].rearrange("q n t -> q (n t)")
+                )
+
+        def wb_regroup():
+            src = wb_raw[:].rearrange("p t (h kv d) -> p kv h d t", h=2, kv=2, d=128)
+            for kv in range(2):
+                nc.scalar.copy(
+                    out=wbg[:, 256 * kv : 256 * kv + 256, :].rearrange("p (h d) t -> p h d t", h=2),
+                    in_=src[:, kv],
+                )
+
+        def wb_quant():
+            nc.vector.quantize_mx(out=wbc[:].bitcast(FP8X4), scales=wbs[:], in_=wbg[:].rearrange("p n t -> p (n t)"))
+
+        xg_t = {}
+        xc_t = {}
+        xs_t = {}
+        c_t = {}
+        ss_t = {}
+        sd_t = {}
+        n_t = {}
+        nt_t = {}
+        ng_t = {}
+        nc_t = {}
+        ns_t = {}
+        o_sb_t = {}
+        r_t = {}
+
+        def x_transpose(G):
+            x32 = x_sb[G // 2][:].bitcast(F32)
+            xg = xgp.tile([P, 2048], BF16, name="xg", align_bytes=64)
+            xg_t[G] = xg
+            xg32 = xg[:].bitcast(F32)
+            for i in range(2):
+                j = 2 * (G % 2) + i
+                xt = ps_xt.tile([P, 4, P], F32, name="xt")
+                for wd in range(4):
+                    col = 512 * j + 128 * wd
+                    nc.tensor.transpose(xt[:, wd, :], x32[:, col : col + 128], ident_f[:])
+                nc.scalar.copy(
+                    out=xg32[:, 512 * i : 512 * i + 512].rearrange("q (g m u) -> q g m u", g=2, m=P, u=2),
+                    in_=xt[:].rearrange("q (g u) m -> q g m u", g=2, u=2),
+                )
+
+        def x_quant(G):
+            xc = const.tile([P, 512], U32, name="xc%d" % G, align_bytes=64)
+            xs = const.tile([P, 512], U8, name="xs%d" % G, align_bytes=64)
+            xc_t[G] = xc
+            xs_t[G] = xs
+            nc.vector.quantize_mx(out=xc[:].bitcast(FP8X4), scales=xs[:], in_=xg_t[G][:])
+
+        def stage1(G, i):
+            if i == 0:
+                ss_new = small.tile([P, 2], F32, name="ss")
+                ss_t[G] = ss_new
+            c_ps = ps_c.tile([P, LATENT], F32, name="c_ps")
+            c_t[(G, i)] = c_ps
+            for g in range(2):
+                sl = slice(256 * i + 128 * g, 256 * i + 128 * g + 128)
+                nc.tensor.matmul_mx(
+                    out=c_ps[:],
+                    lhsT=xc_t[G][:, sl].bitcast(FP8X4),
+                    lhsT_scale=xs_t[G][:, sl],
+                    rhs=wac[:, g, :].bitcast(FP8X4),
+                    rhs_scale=was[:, g, :],
+                    start=(g == 0),
+                    stop=(g == 1),
+                )
+            junk = junkp.tile([P, LATENT], BF16, name="junk")
+            nc.scalar.activation(out=junk[:], in_=c_ps[:], func=ACT.Square, accum_out=ss_t[G][:, i : i + 1])
+            if i == 1:
+                ms = small.tile([P, 2], F32, name="ms")
+                nc.gpsimd.tensor_scalar(out=ms[:], in0=ss_t[G][:], scalar1=1.0 / LATENT, scalar2=RMS_EPS, op0=ALU.mult, op1=ALU.add)
+                rstd = small.tile([P, 2], F32, name="rstd")
+                sd_t[G] = rstd
+                nc.gpsimd.tensor_tensor(out=rstd[:], in0=ms[:], in1=mhalf[:], op=ALU.pow)
+
+        def norm(G):
+            rstd = sd_t[G]
+            n_sb = nsp.tile([P, 2, LATENT], BF16, name="n_sb")
+            n_t[G] = n_sb
+            for i in range(2):
+                nc.vector.scalar_tensor_tensor(
+                    out=n_sb[:, i, :],
+                    in0=c_t[(G, i)][:],
+                    scalar=rstd[:, i : i + 1],
+                    in1=g_bf[:],
+                    op0=ALU.mult,
+                    op1=ALU.mult,
+                )
+
+        def n_transpose(G):
+            nt = ps_nt.tile([P, 2, 4, P], BF16, name="nt")
+            nt_t[G] = nt
+            for i in range(2):
+                for t in range(4):
+                    nc.tensor.transpose(nt[:, i, t, :], n_t[G][:, i, 128 * t : 128 * t + 128], ident_b[:])
+
+        def n_copy(G):
+            ng = ngp.tile([P, 2, P, 4], BF16, name="ng", align_bytes=64)
+            ng_t[G] = ng
+            if G in S_NCOPY:
+                nc.scalar.copy(out=ng[:], in_=nt_t[G][:].rearrange("p i t m -> p i m t"))
+            else:
+                nc.vector.tensor_copy(out=ng[:], in_=nt_t[G][:].rearrange("p i t m -> p i m t"))
+
+        def n_quant(G):
+            ncd = ncp.tile([P, 256], U32, name="ncd", align_bytes=64)
+            nsc = ncp.tile([P, 256], U8, name="nsc", align_bytes=64)
+            nc_t[G] = ncd
+            ns_t[G] = nsc
+            nc.vector.quantize_mx(out=ncd[:].bitcast(FP8X4), scales=nsc[:], in_=ng_t[G][:].rearrange("p i m t -> p (i m t)"))
+
+        def stage2(G, i):
+            c = G // 2
+            if i == 0:
+                o_new = osp.tile([P, 2, 2, 256], F32, name="o_sb")
+                o_sb_t[G] = o_new
+            o_sb = o_sb_t[G]
+            o_ps = ps_o.tile([P, KV_OUT], F32, name="o_ps")
+            sl = slice(128 * i, 128 * i + 128)
+            nc.tensor.matmul_mx(
+                out=o_ps[:],
+                lhsT=nc_t[G][:, sl].bitcast(FP8X4),
+                lhsT_scale=ns_t[G][:, sl],
+                rhs=wbc[:].bitcast(FP8X4),
+                rhs_scale=wbs[:],
+                start=True,
+                stop=True,
+            )
+            nc.scalar.copy(out=o_sb[:, :, i, :], in_=o_ps[:].rearrange("p (kv n) -> p kv n", kv=2))
+            j0 = 2 * (G % 2)
+            if G == PAIRS - 1:
+                nc.sync.dma_start(out=o0v[c][:, j0 + i, :], in_=o_sb[:, 0, i, :])
+                nc.sync.dma_start(out=o1v[c][:, j0 + i, :], in_=o_sb[:, 1, i, :])
+            elif i == 1:
+                nc.sync.dma_start(out=o0v[c][:, j0 : j0 + 2, :], in_=o_sb[:, 0, :, :])
+                nc.sync.dma_start(out=o1v[c][:, j0 : j0 + 2, :], in_=o_sb[:, 1, :, :])
+
+        def rope_mm(c):
+            r_ps = ps_r.tile([P, 4, ROPE], F32, name="r_ps")
+            r_t[c] = r_ps
+            for j in range(4):
+                G = 2 * c + j // 2
+                i = j % 2
+                for g in range(2):
+                    sl = slice(256 * i + 128 * g, 256 * i + 128 * g + 128)
+                    nc.tensor.matmul_mx(
+                        out=r_ps[:, j, :],
+                        lhsT=xc_t[G][:, sl].bitcast(FP8X4),
+                        lhsT_scale=xs_t[G][:, sl],
+                        rhs=war[:, g, :].bitcast(FP8X4),
+                        rhs_scale=wars[:, g, :],
+                        start=(g == 0),
+                        stop=(g == 1),
+                    )
+
+        def rope_ew(c):
+            cm = c % 4
+            rv = r_t[c][:].rearrange("p j (i two) -> p (j i) two", two=2)
+            cosv = cos_t[:, 256 * cm : 256 * cm + 256]
+            sinv = sin_t[:, 256 * cm : 256 * cm + 256]
+            m1 = rop.tile([P, 256, 2], F32, name="m1")
+            m2 = rop.tile([P, 2, 256], F32, name="m2")
+            kr = rop.tile([P, 256, 2], F32, name="kr")
+            nc.vector.tensor_tensor(out=m1[:], in0=rv, in1=cosv.unsqueeze(2).to_broadcast([P, 256, 2]), op=ALU.mult)
+            nc.vector.scalar_tensor_tensor(out=m2[:, 0, :], in0=rv[:, :, 1], scalar=-1.0, in1=sinv, op0=ALU.mult, op1=ALU.mult)
+            nc.vector.tensor_tensor(out=m2[:, 1, :], in0=rv[:, :, 0], in1=sinv, op=ALU.mult)
+            nc.gpsimd.tensor_tensor(out=kr[:], in0=m1[:], in1=m2[:].rearrange("p two n -> p n two"), op=ALU.add)
+            nc.sync.dma_start(out=o2v[c], in_=kr[:].rearrange("p n two -> p (n two)"))
+
+        x_next = [0]
+
+        def x_pe():
+            if x_next[0] < PAIRS:
+                x_transpose(x_next[0])
+
+        def x_v():
+            if x_next[0] < PAIRS:
+                x_quant(x_next[0])
+                x_next[0] += 1
+
+        wa_regroup(0)
+        wa_quant(0)
+        x_pe()
+        wa_regroup(1)
+        x_v()
+        wa_quant(1)
+        for r in range(0, PAIRS + 4):
+            x_pe()
+            if 0 <= r - 2 < PAIRS:
+                n_transpose(r - 2)
+            if 0 <= r - 1 < PAIRS:
+                norm(r - 1)
+            if 0 <= r - 2 < PAIRS:
+                n_copy(r - 2)
+            for i in range(2):
+                if 0 <= r - 3 < PAIRS:
+                    stage2(r - 3, i)
+                if 0 <= r < PAIRS:
+                    stage1(r, i)
+            x_v()
+            if 0 <= r - 2 < PAIRS:
+                n_quant(r - 2)
+            cr = r - 1 - ROPE_LAG
+            if cr >= 0 and cr % 2 == 1 and cr // 2 < CHUNKS:
+                rope_ew(cr // 2)
+            if cr >= 0 and cr % 2 == 0 and cr // 2 < CHUNKS:
+                rope_mm(cr // 2)
+            if r < X_EXTRA:
+                x_pe()
+                x_v()
+            if r == 0:
+                tables_b()
+                war_regroup()
+            if r == 1:
+                wb_regroup()
+                war_quant()
+                rope_tables()
+            if r == 2:
+                wb_quant()

@@ -26,10 +26,10 @@ RMS_EPS = 1.1920928955078125e-07
 ROPE_BASE = 10000.0
 
 CHUNKS = 8
-PAIRS = 16
-X_EXTRA = 2
-ROPE_LAG = 2
-S_NCOPY = (5, 11)
+TILES = 32
+X_LEAD = 2
+X_EXTRA = 4
+S_NCOPY = ()
 
 FLOPS = 2 * TOKENS * D_MODEL * (LATENT + ROPE) + 2 * TOKENS * LATENT * KV_OUT
 
@@ -45,12 +45,12 @@ def tile_multiheadlatentattention_pa_t_kernel(tc, x, Wkv_a, kv_norm_w, Wkv_b, ou
 
     with ExitStack() as ctx:
         const = ctx.enter_context(tc.tile_pool(name="const", bufs=1))
-        xgp = ctx.enter_context(tc.tile_pool(name="xgp", bufs=3))
-        small = ctx.enter_context(tc.tile_pool(name="small", bufs=4))
+        xgp = ctx.enter_context(tc.tile_pool(name="xgp", bufs=4))
+        small = ctx.enter_context(tc.tile_pool(name="small", bufs=6))
         junkp = ctx.enter_context(tc.tile_pool(name="junkp", bufs=2))
-        nsp = ctx.enter_context(tc.tile_pool(name="nsp", bufs=3))
-        ngp = ctx.enter_context(tc.tile_pool(name="ngp", bufs=2))
-        ncp = ctx.enter_context(tc.tile_pool(name="ncp", bufs=3))
+        nsp = ctx.enter_context(tc.tile_pool(name="nsp", bufs=4))
+        ngp = ctx.enter_context(tc.tile_pool(name="ngp", bufs=3))
+        ncp = ctx.enter_context(tc.tile_pool(name="ncp", bufs=4))
         osp = ctx.enter_context(tc.tile_pool(name="osp", bufs=4))
         rop = ctx.enter_context(tc.tile_pool(name="rop", bufs=2))
         ps_xt = ctx.enter_context(tc.psum_pool(name="ps_xt", bufs=2))
@@ -74,8 +74,8 @@ def tile_multiheadlatentattention_pa_t_kernel(tc, x, Wkv_a, kv_norm_w, Wkv_b, ou
             )
 
         nc.scalar.dma_start(out=g_bf[:], in_=kv_norm_w.partition_broadcast(P))
-        load_wa(0)
         nc.sync.dma_start(out=x_sb[0][:, 0:2048], in_=xv[0][:, 0:2048])
+        load_wa(0)
         load_wa(1)
         nc.sync.dma_start(out=x_sb[0][:, 2048:4096], in_=xv[0][:, 2048:4096])
         nc.sync.dma_start(out=x_sb[1][:], in_=xv[1])
@@ -93,7 +93,7 @@ def tile_multiheadlatentattention_pa_t_kernel(tc, x, Wkv_a, kv_norm_w, Wkv_b, ou
         nc.vector.memset(eps_t[:], RMS_EPS)
         warm = const.tile([P, 1], F32, name="warm")
         nc.scalar.activation(out=warm[:], in_=eps_t[:], func=ACT.Sin)
-        mhalf = const.tile([P, 2], F32, name="mhalf")
+        mhalf = const.tile([P, 1], F32, name="mhalf")
         nc.vector.memset(mhalf[:], -0.5)
 
         pos_f = const.tile([P, 16], F32, name="pos_f")
@@ -115,18 +115,18 @@ def tile_multiheadlatentattention_pa_t_kernel(tc, x, Wkv_a, kv_norm_w, Wkv_b, ou
         )
         whole = const.tile([P, 16, 64], I32, name="whole")
         nc.vector.tensor_copy(out=whole[:], in_=turns[:])
-        sin_t = turns[:].rearrange("p a i -> p (a i)")
-        nc.vector.tensor_tensor(out=sin_t, in0=sin_t, in1=whole[:].rearrange("p a i -> p (a i)"), op=ALU.subtract)
+        frac = turns[:].rearrange("p a i -> p (a i)")
+        nc.vector.tensor_tensor(out=frac, in0=frac, in1=whole[:].rearrange("p a i -> p (a i)"), op=ALU.subtract)
+        sin_t = const.tile([P, 1024], F32, name="sin_t")
         cos_t = const.tile([P, 1024], F32, name="cos_t")
 
-        def tables_b():
-            nc.vector.tensor_scalar(out=cos_t[:], in0=sin_t, scalar1=0.25, scalar2=None, op0=ALU.add)
-            nc.vector.scalar_tensor_tensor(out=sin_t, in0=sin_t, scalar=0.5, in1=sin_t, op0=ALU.is_gt, op1=ALU.subtract)
-            nc.vector.scalar_tensor_tensor(out=cos_t[:], in0=cos_t[:], scalar=0.5, in1=cos_t[:], op0=ALU.is_gt, op1=ALU.subtract)
+        def rope_tables_a():
+            nc.scalar.activation(out=sin_t[:], in_=frac, func=ACT.Sin, scale=2.0 * math.pi)
+            nc.scalar.activation(out=cos_t[:], in_=frac, func=ACT.Sin, scale=math.pi)
 
-        def rope_tables():
-            nc.scalar.activation(out=sin_t, in_=sin_t, func=ACT.Sin, scale=-2.0 * math.pi)
-            nc.scalar.activation(out=cos_t[:], in_=cos_t[:], func=ACT.Sin, scale=-2.0 * math.pi)
+        def rope_tables_b():
+            nc.scalar.activation(out=cos_t[:], in_=cos_t[:], func=ACT.Square, scale=math.sqrt(2.0))
+            nc.scalar.activation(out=cos_t[:], in_=cos_t[:], func=ACT.Copy, scale=-1.0, bias=1.0)
 
         wag_c = const.tile([P, 2, 512, 4], BF16, name="wag_c", align_bytes=64)
         wag_r = const.tile([P, 2, 128, 4], BF16, name="wag_r", align_bytes=64)
@@ -148,7 +148,7 @@ def tile_multiheadlatentattention_pa_t_kernel(tc, x, Wkv_a, kv_norm_w, Wkv_b, ou
 
         def war_regroup():
             for g in range(2):
-                nc.scalar.copy(out=wag_r[:, g, :, :], in_=wa_raw[:, 4 * g : 4 * g + 4, 512:640].rearrange("q t n -> q n t"))
+                nc.vector.tensor_copy(out=wag_r[:, g, :, :], in_=wa_raw[:, 4 * g : 4 * g + 4, 512:640].rearrange("q t n -> q n t"))
 
         def war_quant():
             for g in range(2):
@@ -156,13 +156,12 @@ def tile_multiheadlatentattention_pa_t_kernel(tc, x, Wkv_a, kv_norm_w, Wkv_b, ou
                     out=war[:, g, :].bitcast(FP8X4), scales=wars[:, g, :], in_=wag_r[:, g, :, :].rearrange("q n t -> q (n t)")
                 )
 
-        def wb_regroup():
+        def wb_regroup(kv):
             src = wb_raw[:].rearrange("p t (h kv d) -> p kv h d t", h=2, kv=2, d=128)
-            for kv in range(2):
-                nc.scalar.copy(
-                    out=wbg[:, 256 * kv : 256 * kv + 256, :].rearrange("p (h d) t -> p h d t", h=2),
-                    in_=src[:, kv],
-                )
+            nc.vector.tensor_copy(
+                out=wbg[:, 256 * kv : 256 * kv + 256, :].rearrange("p (h d) t -> p h d t", h=2),
+                in_=src[:, kv],
+            )
 
         def wb_quant():
             nc.vector.quantize_mx(out=wbc[:].bitcast(FP8X4), scales=wbs[:], in_=wbg[:].rearrange("p n t -> p (n t)"))
@@ -171,8 +170,7 @@ def tile_multiheadlatentattention_pa_t_kernel(tc, x, Wkv_a, kv_norm_w, Wkv_b, ou
         xc_t = {}
         xs_t = {}
         c_t = {}
-        ss_t = {}
-        sd_t = {}
+        rstd_t = {}
         n_t = {}
         nt_t = {}
         ng_t = {}
@@ -180,104 +178,91 @@ def tile_multiheadlatentattention_pa_t_kernel(tc, x, Wkv_a, kv_norm_w, Wkv_b, ou
         ns_t = {}
         o_sb_t = {}
         r_t = {}
+        m_t = {}
 
-        def x_transpose(G):
-            x32 = x_sb[G // 2][:].bitcast(F32)
-            xg = xgp.tile([P, 2048], BF16, name="xg", align_bytes=64)
-            xg_t[G] = xg
-            xg32 = xg[:].bitcast(F32)
-            for i in range(2):
-                j = 2 * (G % 2) + i
-                xt = ps_xt.tile([P, 4, P], F32, name="xt")
-                for wd in range(4):
-                    col = 512 * j + 128 * wd
-                    nc.tensor.transpose(xt[:, wd, :], x32[:, col : col + 128], ident_f[:])
-                nc.scalar.copy(
-                    out=xg32[:, 512 * i : 512 * i + 512].rearrange("q (g m u) -> q g m u", g=2, m=P, u=2),
-                    in_=xt[:].rearrange("q (g u) m -> q g m u", g=2, u=2),
-                )
+        def x_transpose(T):
+            x32 = x_sb[T // 4][:].bitcast(F32)
+            xg = xgp.tile([P, 1024], BF16, name="xg", align_bytes=64)
+            xg_t[T] = xg
+            xt = ps_xt.tile([P, 4, P], F32, name="xt")
+            for wd in range(4):
+                col = 512 * (T % 4) + 128 * wd
+                nc.tensor.transpose(xt[:, wd, :], x32[:, col : col + 128], ident_f[:])
+            nc.scalar.copy(
+                out=xg[:].bitcast(F32).rearrange("q (g m u) -> q g m u", g=2, m=P, u=2),
+                in_=xt[:].rearrange("q (g u) m -> q g m u", g=2, u=2),
+            )
 
-        def x_quant(G):
-            xc = const.tile([P, 512], U32, name="xc%d" % G, align_bytes=64)
-            xs = const.tile([P, 512], U8, name="xs%d" % G, align_bytes=64)
-            xc_t[G] = xc
-            xs_t[G] = xs
-            nc.vector.quantize_mx(out=xc[:].bitcast(FP8X4), scales=xs[:], in_=xg_t[G][:])
+        def x_quant(T):
+            xc = const.tile([P, 256], U32, name="xc%d" % T, align_bytes=64)
+            xs = const.tile([P, 256], U8, name="xs%d" % T, align_bytes=64)
+            xc_t[T] = xc
+            xs_t[T] = xs
+            nc.vector.quantize_mx(out=xc[:].bitcast(FP8X4), scales=xs[:], in_=xg_t[T][:])
 
-        def stage1(G, i):
-            if i == 0:
-                ss_new = small.tile([P, 2], F32, name="ss")
-                ss_t[G] = ss_new
+        def stage1(T):
             c_ps = ps_c.tile([P, LATENT], F32, name="c_ps")
-            c_t[(G, i)] = c_ps
+            c_t[T] = c_ps
             for g in range(2):
-                sl = slice(256 * i + 128 * g, 256 * i + 128 * g + 128)
+                sl = slice(128 * g, 128 * g + 128)
                 nc.tensor.matmul_mx(
                     out=c_ps[:],
-                    lhsT=xc_t[G][:, sl].bitcast(FP8X4),
-                    lhsT_scale=xs_t[G][:, sl],
+                    lhsT=xc_t[T][:, sl].bitcast(FP8X4),
+                    lhsT_scale=xs_t[T][:, sl],
                     rhs=wac[:, g, :].bitcast(FP8X4),
                     rhs_scale=was[:, g, :],
                     start=(g == 0),
                     stop=(g == 1),
                 )
             junk = junkp.tile([P, LATENT], BF16, name="junk")
-            nc.scalar.activation(out=junk[:], in_=c_ps[:], func=ACT.Square, accum_out=ss_t[G][:, i : i + 1])
-            if i == 1:
-                ms = small.tile([P, 2], F32, name="ms")
-                nc.gpsimd.tensor_scalar(out=ms[:], in0=ss_t[G][:], scalar1=1.0 / LATENT, scalar2=RMS_EPS, op0=ALU.mult, op1=ALU.add)
-                rstd = small.tile([P, 2], F32, name="rstd")
-                sd_t[G] = rstd
-                nc.gpsimd.tensor_tensor(out=rstd[:], in0=ms[:], in1=mhalf[:], op=ALU.pow)
+            ss = small.tile([P, 1], F32, name="ss")
+            nc.scalar.activation(out=junk[:], in_=c_ps[:], func=ACT.Square, accum_out=ss[:])
+            ms = small.tile([P, 1], F32, name="ms")
+            nc.gpsimd.tensor_scalar(out=ms[:], in0=ss[:], scalar1=1.0 / LATENT, scalar2=RMS_EPS, op0=ALU.mult, op1=ALU.add)
+            rstd = small.tile([P, 1], F32, name="rstd")
+            rstd_t[T] = rstd
+            nc.gpsimd.tensor_tensor(out=rstd[:], in0=ms[:], in1=mhalf[:], op=ALU.pow)
 
-        def norm(G):
-            rstd = sd_t[G]
-            n_sb = nsp.tile([P, 2, LATENT], BF16, name="n_sb")
-            n_t[G] = n_sb
-            for i in range(2):
-                nc.vector.scalar_tensor_tensor(
-                    out=n_sb[:, i, :],
-                    in0=c_t[(G, i)][:],
-                    scalar=rstd[:, i : i + 1],
-                    in1=g_bf[:],
-                    op0=ALU.mult,
-                    op1=ALU.mult,
-                )
+        def norm(T):
+            n_sb = nsp.tile([P, LATENT], BF16, name="n_sb")
+            n_t[T] = n_sb
+            nc.vector.scalar_tensor_tensor(
+                out=n_sb[:], in0=c_t[T][:], scalar=rstd_t[T][:], in1=g_bf[:], op0=ALU.mult, op1=ALU.mult
+            )
 
-        def n_transpose(G):
-            nt = ps_nt.tile([P, 2, 4, P], BF16, name="nt")
-            nt_t[G] = nt
-            for i in range(2):
-                for t in range(4):
-                    nc.tensor.transpose(nt[:, i, t, :], n_t[G][:, i, 128 * t : 128 * t + 128], ident_b[:])
+        def n_transpose(T):
+            nt = ps_nt.tile([P, 4, P], BF16, name="nt")
+            nt_t[T] = nt
+            for t in range(4):
+                nc.tensor.transpose(nt[:, t, :], n_t[T][:, 128 * t : 128 * t + 128], ident_b[:])
 
-        def n_copy(G):
-            ng = ngp.tile([P, 2, P, 4], BF16, name="ng", align_bytes=64)
-            ng_t[G] = ng
-            if G in S_NCOPY:
-                nc.scalar.copy(out=ng[:], in_=nt_t[G][:].rearrange("p i t m -> p i m t"))
+        def n_copy(T):
+            ng = ngp.tile([P, P, 4], BF16, name="ng", align_bytes=64)
+            ng_t[T] = ng
+            if T in S_NCOPY:
+                nc.scalar.copy(out=ng[:], in_=nt_t[T][:].rearrange("p t m -> p m t"))
             else:
-                nc.vector.tensor_copy(out=ng[:], in_=nt_t[G][:].rearrange("p i t m -> p i m t"))
+                nc.vector.tensor_copy(out=ng[:], in_=nt_t[T][:].rearrange("p t m -> p m t"))
 
-        def n_quant(G):
-            ncd = ncp.tile([P, 256], U32, name="ncd", align_bytes=64)
-            nsc = ncp.tile([P, 256], U8, name="nsc", align_bytes=64)
-            nc_t[G] = ncd
-            ns_t[G] = nsc
-            nc.vector.quantize_mx(out=ncd[:].bitcast(FP8X4), scales=nsc[:], in_=ng_t[G][:].rearrange("p i m t -> p (i m t)"))
+        def n_quant(T):
+            ncd = ncp.tile([P, P], U32, name="ncd", align_bytes=64)
+            nsc = ncp.tile([P, P], U8, name="nsc", align_bytes=64)
+            nc_t[T] = ncd
+            ns_t[T] = nsc
+            nc.vector.quantize_mx(out=ncd[:].bitcast(FP8X4), scales=nsc[:], in_=ng_t[T][:].rearrange("p m t -> p (m t)"))
 
-        def stage2(G, i):
-            c = G // 2
+        def stage2(T):
+            G, i = T // 2, T % 2
+            c = T // 4
             if i == 0:
                 o_new = osp.tile([P, 2, 2, 256], F32, name="o_sb")
                 o_sb_t[G] = o_new
             o_sb = o_sb_t[G]
             o_ps = ps_o.tile([P, KV_OUT], F32, name="o_ps")
-            sl = slice(128 * i, 128 * i + 128)
             nc.tensor.matmul_mx(
                 out=o_ps[:],
-                lhsT=nc_t[G][:, sl].bitcast(FP8X4),
-                lhsT_scale=ns_t[G][:, sl],
+                lhsT=nc_t[T][:].bitcast(FP8X4),
+                lhsT_scale=ns_t[T][:],
                 rhs=wbc[:].bitcast(FP8X4),
                 rhs_scale=wbs[:],
                 start=True,
@@ -285,7 +270,7 @@ def tile_multiheadlatentattention_pa_t_kernel(tc, x, Wkv_a, kv_norm_w, Wkv_b, ou
             )
             nc.scalar.copy(out=o_sb[:, :, i, :], in_=o_ps[:].rearrange("p (kv n) -> p kv n", kv=2))
             j0 = 2 * (G % 2)
-            if G == PAIRS - 1:
+            if T >= TILES - 2:
                 nc.sync.dma_start(out=o0v[c][:, j0 + i, :], in_=o_sb[:, 0, i, :])
                 nc.sync.dma_start(out=o1v[c][:, j0 + i, :], in_=o_sb[:, 1, i, :])
             elif i == 1:
@@ -296,81 +281,90 @@ def tile_multiheadlatentattention_pa_t_kernel(tc, x, Wkv_a, kv_norm_w, Wkv_b, ou
             r_ps = ps_r.tile([P, 4, ROPE], F32, name="r_ps")
             r_t[c] = r_ps
             for j in range(4):
-                G = 2 * c + j // 2
-                i = j % 2
+                T = 4 * c + j
                 for g in range(2):
-                    sl = slice(256 * i + 128 * g, 256 * i + 128 * g + 128)
+                    sl = slice(128 * g, 128 * g + 128)
                     nc.tensor.matmul_mx(
                         out=r_ps[:, j, :],
-                        lhsT=xc_t[G][:, sl].bitcast(FP8X4),
-                        lhsT_scale=xs_t[G][:, sl],
+                        lhsT=xc_t[T][:, sl].bitcast(FP8X4),
+                        lhsT_scale=xs_t[T][:, sl],
                         rhs=war[:, g, :].bitcast(FP8X4),
                         rhs_scale=wars[:, g, :],
                         start=(g == 0),
                         stop=(g == 1),
                     )
 
-        def rope_ew(c):
+        def rope_ew_a(c):
             cm = c % 4
             rv = r_t[c][:].rearrange("p j (i two) -> p (j i) two", two=2)
             cosv = cos_t[:, 256 * cm : 256 * cm + 256]
-            sinv = sin_t[:, 256 * cm : 256 * cm + 256]
             m1 = rop.tile([P, 256, 2], F32, name="m1")
+            m_t[c] = m1
+            nc.vector.tensor_tensor(out=m1[:], in0=rv, in1=cosv.unsqueeze(2).to_broadcast([P, 256, 2]), op=ALU.mult)
+
+        def rope_ew_b(c):
+            cm = c % 4
+            rv = r_t[c][:].rearrange("p j (i two) -> p (j i) two", two=2)
+            sinv = sin_t[:, 256 * cm : 256 * cm + 256]
             m2 = rop.tile([P, 2, 256], F32, name="m2")
             kr = rop.tile([P, 256, 2], F32, name="kr")
-            nc.vector.tensor_tensor(out=m1[:], in0=rv, in1=cosv.unsqueeze(2).to_broadcast([P, 256, 2]), op=ALU.mult)
             nc.vector.scalar_tensor_tensor(out=m2[:, 0, :], in0=rv[:, :, 1], scalar=-1.0, in1=sinv, op0=ALU.mult, op1=ALU.mult)
             nc.vector.tensor_tensor(out=m2[:, 1, :], in0=rv[:, :, 0], in1=sinv, op=ALU.mult)
-            nc.gpsimd.tensor_tensor(out=kr[:], in0=m1[:], in1=m2[:].rearrange("p two n -> p n two"), op=ALU.add)
+            adder = nc.vector if c == CHUNKS - 1 else nc.gpsimd
+            adder.tensor_tensor(out=kr[:], in0=m_t[c][:], in1=m2[:].rearrange("p two n -> p n two"), op=ALU.add)
             nc.sync.dma_start(out=o2v[c], in_=kr[:].rearrange("p n two -> p (n two)"))
 
         x_next = [0]
 
         def x_pe():
-            if x_next[0] < PAIRS:
+            if x_next[0] < TILES:
                 x_transpose(x_next[0])
 
         def x_v():
-            if x_next[0] < PAIRS:
+            if x_next[0] < TILES:
                 x_quant(x_next[0])
                 x_next[0] += 1
 
-        wa_regroup(0)
-        wa_quant(0)
         x_pe()
+        wa_regroup(0)
+        x_v()
+        x_pe()
+        rope_tables_a()
         wa_regroup(1)
         x_v()
+        wa_quant(0)
         wa_quant(1)
-        for r in range(0, PAIRS + 4):
+        for t in range(0, TILES + 5):
             x_pe()
-            if 0 <= r - 2 < PAIRS:
-                n_transpose(r - 2)
-            if 0 <= r - 1 < PAIRS:
-                norm(r - 1)
-            if 0 <= r - 2 < PAIRS:
-                n_copy(r - 2)
-            for i in range(2):
-                if 0 <= r - 3 < PAIRS:
-                    stage2(r - 3, i)
-                if 0 <= r < PAIRS:
-                    stage1(r, i)
+            if 0 <= t - 3 < TILES:
+                n_transpose(t - 3)
+                n_copy(t - 3)
+            if 0 <= t - 4 < TILES:
+                stage2(t - 4)
+            if 0 <= t < TILES:
+                stage1(t)
             x_v()
-            if 0 <= r - 2 < PAIRS:
-                n_quant(r - 2)
-            cr = r - 1 - ROPE_LAG
-            if cr >= 0 and cr % 2 == 1 and cr // 2 < CHUNKS:
-                rope_ew(cr // 2)
-            if cr >= 0 and cr % 2 == 0 and cr // 2 < CHUNKS:
-                rope_mm(cr // 2)
-            if r < X_EXTRA:
+            if 0 <= t - 3 < TILES:
+                n_quant(t - 3)
+            if 0 <= t - 1 < TILES:
+                norm(t - 1)
+            cr = t - 4
+            if cr >= 0 and cr % 4 == 0 and cr // 4 < CHUNKS:
+                rope_mm(cr // 4)
+            if cr >= 0 and cr % 4 == 1 and cr // 4 < CHUNKS:
+                rope_ew_a(cr // 4)
+            if cr >= 0 and cr % 4 == 2 and cr // 4 < CHUNKS:
+                rope_ew_b(cr // 4)
+            if t < X_EXTRA:
                 x_pe()
                 x_v()
-            if r == 0:
-                tables_b()
+            if t == 0:
                 war_regroup()
-            if r == 1:
-                wb_regroup()
                 war_quant()
-                rope_tables()
-            if r == 2:
+            if t == 1:
+                rope_tables_b()
+                wb_regroup(0)
+            if t == 2:
+                wb_regroup(1)
+            if t == 3:
                 wb_quant()

@@ -93,8 +93,6 @@ def tile_multiheadlatentattention_pa_t_kernel(tc, x, Wkv_a, kv_norm_w, Wkv_b, ou
         nc.vector.memset(eps_t[:], RMS_EPS)
         warm = const.tile([P, 1], F32, name="warm")
         nc.scalar.activation(out=warm[:], in_=eps_t[:], func=ACT.Sin)
-        mhalf = const.tile([P, 1], F32, name="mhalf")
-        nc.vector.memset(mhalf[:], -0.5)
 
         pos_f = const.tile([P, 16], F32, name="pos_f")
         nc.vector.tensor_copy(out=pos_f[:], in_=pos_i[:])
@@ -123,6 +121,7 @@ def tile_multiheadlatentattention_pa_t_kernel(tc, x, Wkv_a, kv_norm_w, Wkv_b, ou
         def rope_tables_a():
             nc.scalar.activation(out=sin_t[:], in_=frac, func=ACT.Sin, scale=2.0 * math.pi)
             nc.scalar.activation(out=cos_t[:], in_=frac, func=ACT.Sin, scale=math.pi)
+            nc.scalar.activation(out=warm[:], in_=eps_t[:], func=ACT.Sqrt)
 
         def rope_tables_b():
             nc.scalar.activation(out=cos_t[:], in_=cos_t[:], func=ACT.Square, scale=math.sqrt(2.0))
@@ -217,17 +216,17 @@ def tile_multiheadlatentattention_pa_t_kernel(tc, x, Wkv_a, kv_norm_w, Wkv_b, ou
             junk = junkp.tile([P, LATENT], BF16, name="junk")
             ss = small.tile([P, 1], F32, name="ss")
             nc.scalar.activation(out=junk[:], in_=c_ps[:], func=ACT.Square, accum_out=ss[:])
-            ms = small.tile([P, 1], F32, name="ms")
-            nc.gpsimd.tensor_scalar(out=ms[:], in0=ss[:], scalar1=1.0 / LATENT, scalar2=RMS_EPS, op0=ALU.mult, op1=ALU.add)
-            rstd = small.tile([P, 1], F32, name="rstd")
-            rstd_t[T] = rstd
-            nc.gpsimd.tensor_tensor(out=rstd[:], in0=ms[:], in1=mhalf[:], op=ALU.pow)
+            sd = small.tile([P, 1], F32, name="sd")
+            rstd_t[T] = sd
+            nc.scalar.activation(out=sd[:], in_=ss[:], func=ACT.Sqrt, scale=1.0 / LATENT, bias=eps_t[:])
 
         def norm(T):
+            rstd = small.tile([P, 1], F32, name="rstd")
+            nc.vector.reciprocal(out=rstd[:], in_=rstd_t[T][:])
             n_sb = nsp.tile([P, LATENT], BF16, name="n_sb")
             n_t[T] = n_sb
             nc.vector.scalar_tensor_tensor(
-                out=n_sb[:], in0=c_t[T][:], scalar=rstd_t[T][:], in1=g_bf[:], op0=ALU.mult, op1=ALU.mult
+                out=n_sb[:], in0=c_t[T][:], scalar=rstd[:], in1=g_bf[:], op0=ALU.mult, op1=ALU.mult
             )
 
         def n_transpose(T):

@@ -26,10 +26,10 @@ RMS_EPS = 1.1920928955078125e-07
 ROPE_BASE = 10000.0
 
 CHUNKS = 8
-TILES = 32
-X_LEAD = 2
-X_EXTRA = 4
-S_NCOPY = ()
+GROUPS = (8, 8, 8, 8)
+X_ON_V = (3, 7)
+N_ON_V = (3,)
+O_ON_V = (3, 7)
 
 FLOPS = 2 * TOKENS * D_MODEL * (LATENT + ROPE) + 2 * TOKENS * LATENT * KV_OUT
 
@@ -46,18 +46,14 @@ def tile_multiheadlatentattention_pa_t_kernel(tc, x, Wkv_a, kv_norm_w, Wkv_b, ou
     with ExitStack() as ctx:
         const = ctx.enter_context(tc.tile_pool(name="const", bufs=1))
         xgp = ctx.enter_context(tc.tile_pool(name="xgp", bufs=4))
-        small = ctx.enter_context(tc.tile_pool(name="small", bufs=6))
+        small = ctx.enter_context(tc.tile_pool(name="small", bufs=8))
         junkp = ctx.enter_context(tc.tile_pool(name="junkp", bufs=2))
-        nsp = ctx.enter_context(tc.tile_pool(name="nsp", bufs=4))
-        ngp = ctx.enter_context(tc.tile_pool(name="ngp", bufs=3))
-        ncp = ctx.enter_context(tc.tile_pool(name="ncp", bufs=4))
+        nsp = ctx.enter_context(tc.tile_pool(name="nsp", bufs=6))
+        ngp = ctx.enter_context(tc.tile_pool(name="ngp", bufs=4))
+        ncp = ctx.enter_context(tc.tile_pool(name="ncp", bufs=6))
         osp = ctx.enter_context(tc.tile_pool(name="osp", bufs=4))
         rop = ctx.enter_context(tc.tile_pool(name="rop", bufs=2))
-        ps_xt = ctx.enter_context(tc.psum_pool(name="ps_xt", bufs=2))
-        ps_c = ctx.enter_context(tc.psum_pool(name="ps_c", bufs=3))
-        ps_nt = ctx.enter_context(tc.psum_pool(name="ps_nt", bufs=1))
-        ps_o = ctx.enter_context(tc.psum_pool(name="ps_o", bufs=1))
-        ps_r = ctx.enter_context(tc.psum_pool(name="ps_r", bufs=1))
+        ps = ctx.enter_context(tc.psum_pool(name="ps", bufs=8))
         ctx.enter_context(tc.manual_schedule())
 
         x_sb = []
@@ -93,6 +89,8 @@ def tile_multiheadlatentattention_pa_t_kernel(tc, x, Wkv_a, kv_norm_w, Wkv_b, ou
         nc.vector.memset(eps_t[:], RMS_EPS)
         warm = const.tile([P, 1], F32, name="warm")
         nc.scalar.activation(out=warm[:], in_=eps_t[:], func=ACT.Sin)
+        mhalf = const.tile([P, 2], F32, name="mhalf")
+        nc.vector.memset(mhalf[:], -0.5)
 
         pos_f = const.tile([P, 16], F32, name="pos_f")
         nc.vector.tensor_copy(out=pos_f[:], in_=pos_i[:])
@@ -121,7 +119,6 @@ def tile_multiheadlatentattention_pa_t_kernel(tc, x, Wkv_a, kv_norm_w, Wkv_b, ou
         def rope_tables_a():
             nc.scalar.activation(out=sin_t[:], in_=frac, func=ACT.Sin, scale=2.0 * math.pi)
             nc.scalar.activation(out=cos_t[:], in_=frac, func=ACT.Sin, scale=math.pi)
-            nc.scalar.activation(out=warm[:], in_=eps_t[:], func=ACT.Sqrt)
 
         def rope_tables_b():
             nc.scalar.activation(out=cos_t[:], in_=cos_t[:], func=ACT.Square, scale=math.sqrt(2.0))
@@ -155,12 +152,13 @@ def tile_multiheadlatentattention_pa_t_kernel(tc, x, Wkv_a, kv_norm_w, Wkv_b, ou
                     out=war[:, g, :].bitcast(FP8X4), scales=wars[:, g, :], in_=wag_r[:, g, :, :].rearrange("q n t -> q (n t)")
                 )
 
-        def wb_regroup(kv):
+        def wb_regroup():
             src = wb_raw[:].rearrange("p t (h kv d) -> p kv h d t", h=2, kv=2, d=128)
-            nc.vector.tensor_copy(
-                out=wbg[:, 256 * kv : 256 * kv + 256, :].rearrange("p (h d) t -> p h d t", h=2),
-                in_=src[:, kv],
-            )
+            for kv in range(2):
+                nc.vector.tensor_copy(
+                    out=wbg[:, 256 * kv : 256 * kv + 256, :].rearrange("p (h d) t -> p h d t", h=2),
+                    in_=src[:, kv],
+                )
 
         def wb_quant():
             nc.vector.quantize_mx(out=wbc[:].bitcast(FP8X4), scales=wbs[:], in_=wbg[:].rearrange("p n t -> p (n t)"))
@@ -169,6 +167,7 @@ def tile_multiheadlatentattention_pa_t_kernel(tc, x, Wkv_a, kv_norm_w, Wkv_b, ou
         xc_t = {}
         xs_t = {}
         c_t = {}
+        ss_t = {}
         rstd_t = {}
         n_t = {}
         nt_t = {}
@@ -177,99 +176,114 @@ def tile_multiheadlatentattention_pa_t_kernel(tc, x, Wkv_a, kv_norm_w, Wkv_b, ou
         ns_t = {}
         o_sb_t = {}
         r_t = {}
-        m_t = {}
 
-        def x_transpose(T):
+        def copy_on(on_vector, out, in_):
+            if on_vector:
+                nc.vector.tensor_copy(out=out, in_=in_)
+            else:
+                nc.scalar.copy(out=out, in_=in_)
+
+        def x_transpose(T, on_vector):
+            G, i = T // 2, T % 2
             x32 = x_sb[T // 4][:].bitcast(F32)
-            xg = xgp.tile([P, 1024], BF16, name="xg", align_bytes=64)
-            xg_t[T] = xg
-            xt = ps_xt.tile([P, 4, P], F32, name="xt")
+            if i == 0:
+                xg_new = xgp.tile([P, 2048], BF16, name="xg", align_bytes=64)
+                xg_t[G] = xg_new
+            xg32 = xg_t[G][:].bitcast(F32)
+            xt = ps.tile([P, 4, P], F32, name="xt", tag="bank")
             for wd in range(4):
                 col = 512 * (T % 4) + 128 * wd
                 nc.tensor.transpose(xt[:, wd, :], x32[:, col : col + 128], ident_f[:])
-            nc.scalar.copy(
-                out=xg[:].bitcast(F32).rearrange("q (g m u) -> q g m u", g=2, m=P, u=2),
-                in_=xt[:].rearrange("q (g u) m -> q g m u", g=2, u=2),
+            copy_on(
+                on_vector,
+                xg32[:, 512 * i : 512 * i + 512].rearrange("q (g m u) -> q g m u", g=2, m=P, u=2),
+                xt[:].rearrange("q (g u) m -> q g m u", g=2, u=2),
             )
 
-        def x_quant(T):
-            xc = const.tile([P, 256], U32, name="xc%d" % T, align_bytes=64)
-            xs = const.tile([P, 256], U8, name="xs%d" % T, align_bytes=64)
-            xc_t[T] = xc
-            xs_t[T] = xs
-            nc.vector.quantize_mx(out=xc[:].bitcast(FP8X4), scales=xs[:], in_=xg_t[T][:])
+        def x_quant(G):
+            xc = const.tile([P, 512], U32, name="xc%d" % G, align_bytes=64)
+            xs = const.tile([P, 512], U8, name="xs%d" % G, align_bytes=64)
+            xc_t[G] = xc
+            xs_t[G] = xs
+            nc.vector.quantize_mx(out=xc[:].bitcast(FP8X4), scales=xs[:], in_=xg_t[G][:])
 
         def stage1(T):
-            c_ps = ps_c.tile([P, LATENT], F32, name="c_ps")
+            G, i = T // 2, T % 2
+            if i == 0:
+                ss_new = small.tile([P, 2], F32, name="ss")
+                ss_t[G] = ss_new
+            c_ps = ps.tile([P, LATENT], F32, name="c_ps", tag="bank")
             c_t[T] = c_ps
             for g in range(2):
-                sl = slice(128 * g, 128 * g + 128)
+                sl = slice(256 * i + 128 * g, 256 * i + 128 * g + 128)
                 nc.tensor.matmul_mx(
                     out=c_ps[:],
-                    lhsT=xc_t[T][:, sl].bitcast(FP8X4),
-                    lhsT_scale=xs_t[T][:, sl],
+                    lhsT=xc_t[G][:, sl].bitcast(FP8X4),
+                    lhsT_scale=xs_t[G][:, sl],
                     rhs=wac[:, g, :].bitcast(FP8X4),
                     rhs_scale=was[:, g, :],
                     start=(g == 0),
                     stop=(g == 1),
                 )
             junk = junkp.tile([P, LATENT], BF16, name="junk")
-            ss = small.tile([P, 1], F32, name="ss")
-            nc.scalar.activation(out=junk[:], in_=c_ps[:], func=ACT.Square, accum_out=ss[:])
-            sd = small.tile([P, 1], F32, name="sd")
-            rstd_t[T] = sd
-            nc.scalar.activation(out=sd[:], in_=ss[:], func=ACT.Sqrt, scale=1.0 / LATENT, bias=eps_t[:])
+            nc.scalar.activation(out=junk[:], in_=c_ps[:], func=ACT.Square, accum_out=ss_t[G][:, i : i + 1])
+            if i == 1:
+                ms = small.tile([P, 2], F32, name="ms")
+                nc.gpsimd.tensor_scalar(out=ms[:], in0=ss_t[G][:], scalar1=1.0 / LATENT, scalar2=RMS_EPS, op0=ALU.mult, op1=ALU.add)
+                rstd = small.tile([P, 2], F32, name="rstd")
+                rstd_t[G] = rstd
+                nc.gpsimd.tensor_tensor(out=rstd[:], in0=ms[:], in1=mhalf[:], op=ALU.pow)
 
-        def norm(T):
-            rstd = small.tile([P, 1], F32, name="rstd")
-            nc.vector.reciprocal(out=rstd[:], in_=rstd_t[T][:])
-            n_sb = nsp.tile([P, LATENT], BF16, name="n_sb")
-            n_t[T] = n_sb
-            nc.vector.scalar_tensor_tensor(
-                out=n_sb[:], in0=c_t[T][:], scalar=rstd[:], in1=g_bf[:], op0=ALU.mult, op1=ALU.mult
-            )
+        def norm(G):
+            n_sb = nsp.tile([P, 2, LATENT], BF16, name="n_sb")
+            n_t[G] = n_sb
+            for i in range(2):
+                nc.vector.scalar_tensor_tensor(
+                    out=n_sb[:, i, :],
+                    in0=c_t[2 * G + i][:],
+                    scalar=rstd_t[G][:, i : i + 1],
+                    in1=g_bf[:],
+                    op0=ALU.mult,
+                    op1=ALU.mult,
+                )
 
-        def n_transpose(T):
-            nt = ps_nt.tile([P, 4, P], BF16, name="nt")
-            nt_t[T] = nt
-            for t in range(4):
-                nc.tensor.transpose(nt[:, t, :], n_t[T][:, 128 * t : 128 * t + 128], ident_b[:])
+        def n_transpose(G, on_vector):
+            nt = ps.tile([P, 2, 4, P], BF16, name="nt", tag="bank")
+            for i in range(2):
+                for t in range(4):
+                    nc.tensor.transpose(nt[:, i, t, :], n_t[G][:, i, 128 * t : 128 * t + 128], ident_b[:])
+            ng = ngp.tile([P, 2, P, 4], BF16, name="ng", align_bytes=64)
+            ng_t[G] = ng
+            copy_on(on_vector, ng[:], nt[:].rearrange("p i t m -> p i m t"))
 
-        def n_copy(T):
-            ng = ngp.tile([P, P, 4], BF16, name="ng", align_bytes=64)
-            ng_t[T] = ng
-            if T in S_NCOPY:
-                nc.scalar.copy(out=ng[:], in_=nt_t[T][:].rearrange("p t m -> p m t"))
-            else:
-                nc.vector.tensor_copy(out=ng[:], in_=nt_t[T][:].rearrange("p t m -> p m t"))
+        def n_quant(G):
+            ncd = ncp.tile([P, 256], U32, name="ncd", align_bytes=64)
+            nsc = ncp.tile([P, 256], U8, name="nsc", align_bytes=64)
+            nc_t[G] = ncd
+            ns_t[G] = nsc
+            nc.vector.quantize_mx(out=ncd[:].bitcast(FP8X4), scales=nsc[:], in_=ng_t[G][:].rearrange("p i m t -> p (i m t)"))
 
-        def n_quant(T):
-            ncd = ncp.tile([P, P], U32, name="ncd", align_bytes=64)
-            nsc = ncp.tile([P, P], U8, name="nsc", align_bytes=64)
-            nc_t[T] = ncd
-            ns_t[T] = nsc
-            nc.vector.quantize_mx(out=ncd[:].bitcast(FP8X4), scales=nsc[:], in_=ng_t[T][:].rearrange("p m t -> p (m t)"))
-
-        def stage2(T):
+        def stage2(T, on_vector, fine):
             G, i = T // 2, T % 2
             c = T // 4
             if i == 0:
                 o_new = osp.tile([P, 2, 2, 256], F32, name="o_sb")
                 o_sb_t[G] = o_new
             o_sb = o_sb_t[G]
-            o_ps = ps_o.tile([P, KV_OUT], F32, name="o_ps")
+            o_ps = ps.tile([P, KV_OUT], F32, name="o_ps", tag="bank")
+            sl = slice(128 * i, 128 * i + 128)
             nc.tensor.matmul_mx(
                 out=o_ps[:],
-                lhsT=nc_t[T][:].bitcast(FP8X4),
-                lhsT_scale=ns_t[T][:],
+                lhsT=nc_t[G][:, sl].bitcast(FP8X4),
+                lhsT_scale=ns_t[G][:, sl],
                 rhs=wbc[:].bitcast(FP8X4),
                 rhs_scale=wbs[:],
                 start=True,
                 stop=True,
             )
-            nc.scalar.copy(out=o_sb[:, :, i, :], in_=o_ps[:].rearrange("p (kv n) -> p kv n", kv=2))
+            copy_on(on_vector, o_sb[:, :, i, :], o_ps[:].rearrange("p (kv n) -> p kv n", kv=2))
             j0 = 2 * (G % 2)
-            if T >= TILES - 2:
+            if fine:
                 nc.sync.dma_start(out=o0v[c][:, j0 + i, :], in_=o_sb[:, 0, i, :])
                 nc.sync.dma_start(out=o1v[c][:, j0 + i, :], in_=o_sb[:, 1, i, :])
             elif i == 1:
@@ -277,93 +291,73 @@ def tile_multiheadlatentattention_pa_t_kernel(tc, x, Wkv_a, kv_norm_w, Wkv_b, ou
                 nc.sync.dma_start(out=o1v[c][:, j0 : j0 + 2, :], in_=o_sb[:, 1, :, :])
 
         def rope_mm(c):
-            r_ps = ps_r.tile([P, 4, ROPE], F32, name="r_ps")
+            r_ps = ps.tile([P, 4, ROPE], F32, name="r_ps", tag="bank")
             r_t[c] = r_ps
             for j in range(4):
-                T = 4 * c + j
+                G = 2 * c + j // 2
+                i = j % 2
                 for g in range(2):
-                    sl = slice(128 * g, 128 * g + 128)
+                    sl = slice(256 * i + 128 * g, 256 * i + 128 * g + 128)
                     nc.tensor.matmul_mx(
                         out=r_ps[:, j, :],
-                        lhsT=xc_t[T][:, sl].bitcast(FP8X4),
-                        lhsT_scale=xs_t[T][:, sl],
+                        lhsT=xc_t[G][:, sl].bitcast(FP8X4),
+                        lhsT_scale=xs_t[G][:, sl],
                         rhs=war[:, g, :].bitcast(FP8X4),
                         rhs_scale=wars[:, g, :],
                         start=(g == 0),
                         stop=(g == 1),
                     )
 
-        def rope_ew_a(c):
+        def rope_ew(c):
             cm = c % 4
             rv = r_t[c][:].rearrange("p j (i two) -> p (j i) two", two=2)
             cosv = cos_t[:, 256 * cm : 256 * cm + 256]
-            m1 = rop.tile([P, 256, 2], F32, name="m1")
-            m_t[c] = m1
-            nc.vector.tensor_tensor(out=m1[:], in0=rv, in1=cosv.unsqueeze(2).to_broadcast([P, 256, 2]), op=ALU.mult)
-
-        def rope_ew_b(c):
-            cm = c % 4
-            rv = r_t[c][:].rearrange("p j (i two) -> p (j i) two", two=2)
             sinv = sin_t[:, 256 * cm : 256 * cm + 256]
+            m1 = rop.tile([P, 256, 2], F32, name="m1")
             m2 = rop.tile([P, 2, 256], F32, name="m2")
             kr = rop.tile([P, 256, 2], F32, name="kr")
+            nc.vector.tensor_tensor(out=m1[:], in0=rv, in1=cosv.unsqueeze(2).to_broadcast([P, 256, 2]), op=ALU.mult)
             nc.vector.scalar_tensor_tensor(out=m2[:, 0, :], in0=rv[:, :, 1], scalar=-1.0, in1=sinv, op0=ALU.mult, op1=ALU.mult)
             nc.vector.tensor_tensor(out=m2[:, 1, :], in0=rv[:, :, 0], in1=sinv, op=ALU.mult)
-            adder = nc.vector if c == CHUNKS - 1 else nc.gpsimd
-            adder.tensor_tensor(out=kr[:], in0=m_t[c][:], in1=m2[:].rearrange("p two n -> p n two"), op=ALU.add)
+            nc.gpsimd.tensor_tensor(out=kr[:], in0=m1[:], in1=m2[:].rearrange("p two n -> p n two"), op=ALU.add)
             nc.sync.dma_start(out=o2v[c], in_=kr[:].rearrange("p n two -> p (n two)"))
 
-        x_next = [0]
-
-        def x_pe():
-            if x_next[0] < TILES:
-                x_transpose(x_next[0])
-
-        def x_v():
-            if x_next[0] < TILES:
-                x_quant(x_next[0])
-                x_next[0] += 1
-
-        x_pe()
-        wa_regroup(0)
-        x_v()
-        x_pe()
-        rope_tables_a()
-        wa_regroup(1)
-        x_v()
-        wa_quant(0)
-        wa_quant(1)
-        for t in range(0, TILES + 5):
-            x_pe()
-            if 0 <= t - 3 < TILES:
-                n_transpose(t - 3)
-                n_copy(t - 3)
-            if 0 <= t - 4 < TILES:
-                stage2(t - 4)
-            if 0 <= t < TILES:
-                stage1(t)
-            x_v()
-            if 0 <= t - 3 < TILES:
-                n_quant(t - 3)
-            if 0 <= t - 1 < TILES:
-                norm(t - 1)
-            cr = t - 4
-            if cr >= 0 and cr % 4 == 0 and cr // 4 < CHUNKS:
-                rope_mm(cr // 4)
-            if cr >= 0 and cr % 4 == 1 and cr // 4 < CHUNKS:
-                rope_ew_a(cr // 4)
-            if cr >= 0 and cr % 4 == 2 and cr // 4 < CHUNKS:
-                rope_ew_b(cr // 4)
-            if t < X_EXTRA:
-                x_pe()
-                x_v()
-            if t == 0:
+        first = 0
+        for k in range(len(GROUPS)):
+            tiles = list(range(first, first + GROUPS[k]))
+            first += GROUPS[k]
+            pairs = [T // 2 for T in tiles[0::2]]
+            last_group = k == len(GROUPS) - 1
+            for idx in range(len(tiles)):
+                x_transpose(tiles[idx], idx in X_ON_V)
+                if k == 0 and idx == 1:
+                    rope_tables_a()
+                    wa_regroup(0)
+                if k == 0 and idx == 3:
+                    wa_regroup(1)
+                    wa_quant(0)
+                    wa_quant(1)
+                if idx % 2 == 1 and idx >= 3:
+                    x_quant(pairs[idx // 2 - 1])
+            x_quant(pairs[-1])
+            if k == 0:
+                rope_tables_b()
                 war_regroup()
                 war_quant()
-            if t == 1:
-                rope_tables_b()
-                wb_regroup(0)
-            if t == 2:
-                wb_regroup(1)
-            if t == 3:
+            for idx in range(len(tiles)):
+                stage1(tiles[idx])
+                if idx % 4 == 1:
+                    rope_mm(tiles[idx] // 4)
+                    rope_ew(tiles[idx] // 4)
+                if idx % 2 == 1:
+                    norm(pairs[idx // 2])
+            if k == 0:
+                wb_regroup()
                 wb_quant()
+            for q in range(len(pairs)):
+                n_transpose(pairs[q], q in N_ON_V)
+                if q >= 1:
+                    n_quant(pairs[q - 1])
+            n_quant(pairs[-1])
+            for idx in range(len(tiles)):
+                stage2(tiles[idx], idx in O_ON_V, last_group and idx >= len(tiles) - 2)

@@ -26,10 +26,10 @@ RMS_EPS = 1.1920928955078125e-07
 ROPE_BASE = 10000.0
 
 CHUNKS = 8
-GROUPS = (8, 8, 8, 8)
-X_ON_V = (3, 7)
-N_ON_V = (3,)
-O_ON_V = (3, 7)
+PAIRS = 16
+X_EXTRA = 2
+ROPE_LAG = 2
+S_NCOPY = (5, 11)
 
 FLOPS = 2 * TOKENS * D_MODEL * (LATENT + ROPE) + 2 * TOKENS * LATENT * KV_OUT
 
@@ -45,15 +45,19 @@ def tile_multiheadlatentattention_pa_t_kernel(tc, x, Wkv_a, kv_norm_w, Wkv_b, ou
 
     with ExitStack() as ctx:
         const = ctx.enter_context(tc.tile_pool(name="const", bufs=1))
-        xgp = ctx.enter_context(tc.tile_pool(name="xgp", bufs=4))
-        small = ctx.enter_context(tc.tile_pool(name="small", bufs=8))
+        xgp = ctx.enter_context(tc.tile_pool(name="xgp", bufs=3))
+        small = ctx.enter_context(tc.tile_pool(name="small", bufs=4))
         junkp = ctx.enter_context(tc.tile_pool(name="junkp", bufs=2))
-        nsp = ctx.enter_context(tc.tile_pool(name="nsp", bufs=6))
-        ngp = ctx.enter_context(tc.tile_pool(name="ngp", bufs=4))
-        ncp = ctx.enter_context(tc.tile_pool(name="ncp", bufs=6))
+        nsp = ctx.enter_context(tc.tile_pool(name="nsp", bufs=3))
+        ngp = ctx.enter_context(tc.tile_pool(name="ngp", bufs=2))
+        ncp = ctx.enter_context(tc.tile_pool(name="ncp", bufs=3))
         osp = ctx.enter_context(tc.tile_pool(name="osp", bufs=4))
         rop = ctx.enter_context(tc.tile_pool(name="rop", bufs=2))
-        ps = ctx.enter_context(tc.psum_pool(name="ps", bufs=8))
+        ps_xt = ctx.enter_context(tc.psum_pool(name="ps_xt", bufs=2))
+        ps_c = ctx.enter_context(tc.psum_pool(name="ps_c", bufs=3))
+        ps_nt = ctx.enter_context(tc.psum_pool(name="ps_nt", bufs=1))
+        ps_o = ctx.enter_context(tc.psum_pool(name="ps_o", bufs=1))
+        ps_r = ctx.enter_context(tc.psum_pool(name="ps_r", bufs=1))
         ctx.enter_context(tc.manual_schedule())
 
         x_sb = []
@@ -70,8 +74,8 @@ def tile_multiheadlatentattention_pa_t_kernel(tc, x, Wkv_a, kv_norm_w, Wkv_b, ou
             )
 
         nc.scalar.dma_start(out=g_bf[:], in_=kv_norm_w.partition_broadcast(P))
-        nc.sync.dma_start(out=x_sb[0][:, 0:2048], in_=xv[0][:, 0:2048])
         load_wa(0)
+        nc.sync.dma_start(out=x_sb[0][:, 0:2048], in_=xv[0][:, 0:2048])
         load_wa(1)
         nc.sync.dma_start(out=x_sb[0][:, 2048:4096], in_=xv[0][:, 2048:4096])
         nc.sync.dma_start(out=x_sb[1][:], in_=xv[1])
@@ -111,18 +115,18 @@ def tile_multiheadlatentattention_pa_t_kernel(tc, x, Wkv_a, kv_norm_w, Wkv_b, ou
         )
         whole = const.tile([P, 16, 64], I32, name="whole")
         nc.vector.tensor_copy(out=whole[:], in_=turns[:])
-        frac = turns[:].rearrange("p a i -> p (a i)")
-        nc.vector.tensor_tensor(out=frac, in0=frac, in1=whole[:].rearrange("p a i -> p (a i)"), op=ALU.subtract)
-        sin_t = const.tile([P, 1024], F32, name="sin_t")
+        sin_t = turns[:].rearrange("p a i -> p (a i)")
+        nc.vector.tensor_tensor(out=sin_t, in0=sin_t, in1=whole[:].rearrange("p a i -> p (a i)"), op=ALU.subtract)
         cos_t = const.tile([P, 1024], F32, name="cos_t")
 
-        def rope_tables_a():
-            nc.scalar.activation(out=sin_t[:], in_=frac, func=ACT.Sin, scale=2.0 * math.pi)
-            nc.scalar.activation(out=cos_t[:], in_=frac, func=ACT.Sin, scale=math.pi)
+        def tables_b():
+            nc.vector.tensor_scalar(out=cos_t[:], in0=sin_t, scalar1=0.25, scalar2=None, op0=ALU.add)
+            nc.vector.scalar_tensor_tensor(out=sin_t, in0=sin_t, scalar=0.5, in1=sin_t, op0=ALU.is_gt, op1=ALU.subtract)
+            nc.vector.scalar_tensor_tensor(out=cos_t[:], in0=cos_t[:], scalar=0.5, in1=cos_t[:], op0=ALU.is_gt, op1=ALU.subtract)
 
-        def rope_tables_b():
-            nc.scalar.activation(out=cos_t[:], in_=cos_t[:], func=ACT.Square, scale=math.sqrt(2.0))
-            nc.scalar.activation(out=cos_t[:], in_=cos_t[:], func=ACT.Copy, scale=-1.0, bias=1.0)
+        def rope_tables():
+            nc.scalar.activation(out=sin_t, in_=sin_t, func=ACT.Sin, scale=-2.0 * math.pi)
+            nc.scalar.activation(out=cos_t[:], in_=cos_t[:], func=ACT.Sin, scale=-2.0 * math.pi)
 
         wag_c = const.tile([P, 2, 512, 4], BF16, name="wag_c", align_bytes=64)
         wag_r = const.tile([P, 2, 128, 4], BF16, name="wag_r", align_bytes=64)
@@ -144,7 +148,7 @@ def tile_multiheadlatentattention_pa_t_kernel(tc, x, Wkv_a, kv_norm_w, Wkv_b, ou
 
         def war_regroup():
             for g in range(2):
-                nc.vector.tensor_copy(out=wag_r[:, g, :, :], in_=wa_raw[:, 4 * g : 4 * g + 4, 512:640].rearrange("q t n -> q n t"))
+                nc.scalar.copy(out=wag_r[:, g, :, :], in_=wa_raw[:, 4 * g : 4 * g + 4, 512:640].rearrange("q t n -> q n t"))
 
         def war_quant():
             for g in range(2):
@@ -155,7 +159,7 @@ def tile_multiheadlatentattention_pa_t_kernel(tc, x, Wkv_a, kv_norm_w, Wkv_b, ou
         def wb_regroup():
             src = wb_raw[:].rearrange("p t (h kv d) -> p kv h d t", h=2, kv=2, d=128)
             for kv in range(2):
-                nc.vector.tensor_copy(
+                nc.scalar.copy(
                     out=wbg[:, 256 * kv : 256 * kv + 256, :].rearrange("p (h d) t -> p h d t", h=2),
                     in_=src[:, kv],
                 )
@@ -168,7 +172,7 @@ def tile_multiheadlatentattention_pa_t_kernel(tc, x, Wkv_a, kv_norm_w, Wkv_b, ou
         xs_t = {}
         c_t = {}
         ss_t = {}
-        rstd_t = {}
+        sd_t = {}
         n_t = {}
         nt_t = {}
         ng_t = {}
@@ -177,28 +181,21 @@ def tile_multiheadlatentattention_pa_t_kernel(tc, x, Wkv_a, kv_norm_w, Wkv_b, ou
         o_sb_t = {}
         r_t = {}
 
-        def copy_on(on_vector, out, in_):
-            if on_vector:
-                nc.vector.tensor_copy(out=out, in_=in_)
-            else:
-                nc.scalar.copy(out=out, in_=in_)
-
-        def x_transpose(T, on_vector):
-            G, i = T // 2, T % 2
-            x32 = x_sb[T // 4][:].bitcast(F32)
-            if i == 0:
-                xg_new = xgp.tile([P, 2048], BF16, name="xg", align_bytes=64)
-                xg_t[G] = xg_new
-            xg32 = xg_t[G][:].bitcast(F32)
-            xt = ps.tile([P, 4, P], F32, name="xt", tag="bank")
-            for wd in range(4):
-                col = 512 * (T % 4) + 128 * wd
-                nc.tensor.transpose(xt[:, wd, :], x32[:, col : col + 128], ident_f[:])
-            copy_on(
-                on_vector,
-                xg32[:, 512 * i : 512 * i + 512].rearrange("q (g m u) -> q g m u", g=2, m=P, u=2),
-                xt[:].rearrange("q (g u) m -> q g m u", g=2, u=2),
-            )
+        def x_transpose(G):
+            x32 = x_sb[G // 2][:].bitcast(F32)
+            xg = xgp.tile([P, 2048], BF16, name="xg", align_bytes=64)
+            xg_t[G] = xg
+            xg32 = xg[:].bitcast(F32)
+            for i in range(2):
+                j = 2 * (G % 2) + i
+                xt = ps_xt.tile([P, 4, P], F32, name="xt")
+                for wd in range(4):
+                    col = 512 * j + 128 * wd
+                    nc.tensor.transpose(xt[:, wd, :], x32[:, col : col + 128], ident_f[:])
+                nc.scalar.copy(
+                    out=xg32[:, 512 * i : 512 * i + 512].rearrange("q (g m u) -> q g m u", g=2, m=P, u=2),
+                    in_=xt[:].rearrange("q (g u) m -> q g m u", g=2, u=2),
+                )
 
         def x_quant(G):
             xc = const.tile([P, 512], U32, name="xc%d" % G, align_bytes=64)
@@ -207,13 +204,12 @@ def tile_multiheadlatentattention_pa_t_kernel(tc, x, Wkv_a, kv_norm_w, Wkv_b, ou
             xs_t[G] = xs
             nc.vector.quantize_mx(out=xc[:].bitcast(FP8X4), scales=xs[:], in_=xg_t[G][:])
 
-        def stage1(T):
-            G, i = T // 2, T % 2
+        def stage1(G, i):
             if i == 0:
                 ss_new = small.tile([P, 2], F32, name="ss")
                 ss_t[G] = ss_new
-            c_ps = ps.tile([P, LATENT], F32, name="c_ps", tag="bank")
-            c_t[T] = c_ps
+            c_ps = ps_c.tile([P, LATENT], F32, name="c_ps")
+            c_t[(G, i)] = c_ps
             for g in range(2):
                 sl = slice(256 * i + 128 * g, 256 * i + 128 * g + 128)
                 nc.tensor.matmul_mx(
@@ -231,30 +227,39 @@ def tile_multiheadlatentattention_pa_t_kernel(tc, x, Wkv_a, kv_norm_w, Wkv_b, ou
                 ms = small.tile([P, 2], F32, name="ms")
                 nc.gpsimd.tensor_scalar(out=ms[:], in0=ss_t[G][:], scalar1=1.0 / LATENT, scalar2=RMS_EPS, op0=ALU.mult, op1=ALU.add)
                 rstd = small.tile([P, 2], F32, name="rstd")
-                rstd_t[G] = rstd
+                sd_t[G] = rstd
                 nc.gpsimd.tensor_tensor(out=rstd[:], in0=ms[:], in1=mhalf[:], op=ALU.pow)
 
         def norm(G):
+            rstd = sd_t[G]
             n_sb = nsp.tile([P, 2, LATENT], BF16, name="n_sb")
             n_t[G] = n_sb
             for i in range(2):
                 nc.vector.scalar_tensor_tensor(
                     out=n_sb[:, i, :],
-                    in0=c_t[2 * G + i][:],
-                    scalar=rstd_t[G][:, i : i + 1],
+                    in0=c_t[(G, i)][:],
+                    scalar=rstd[:, i : i + 1],
                     in1=g_bf[:],
                     op0=ALU.mult,
                     op1=ALU.mult,
                 )
 
-        def n_transpose(G, on_vector):
-            nt = ps.tile([P, 2, 4, P], BF16, name="nt", tag="bank")
+        def n_transpose(G):
+            nt = ps_nt.tile([P, 2, 4, P], BF16, name="nt")
+            nt_t[G] = nt
             for i in range(2):
                 for t in range(4):
-                    nc.tensor.transpose(nt[:, i, t, :], n_t[G][:, i, 128 * t : 128 * t + 128], ident_b[:])
+                    nc.tensor.matmul(
+                        out=nt[:, i, t, :], lhsT=n_t[G][:, i, 128 * t : 128 * t + 128], rhs=ident_b[:], start=True, stop=True
+                    )
+
+        def n_copy(G):
             ng = ngp.tile([P, 2, P, 4], BF16, name="ng", align_bytes=64)
             ng_t[G] = ng
-            copy_on(on_vector, ng[:], nt[:].rearrange("p i t m -> p i m t"))
+            if G in S_NCOPY:
+                nc.scalar.copy(out=ng[:], in_=nt_t[G][:].rearrange("p i t m -> p i m t"))
+            else:
+                nc.vector.tensor_copy(out=ng[:], in_=nt_t[G][:].rearrange("p i t m -> p i m t"))
 
         def n_quant(G):
             ncd = ncp.tile([P, 256], U32, name="ncd", align_bytes=64)
@@ -263,14 +268,13 @@ def tile_multiheadlatentattention_pa_t_kernel(tc, x, Wkv_a, kv_norm_w, Wkv_b, ou
             ns_t[G] = nsc
             nc.vector.quantize_mx(out=ncd[:].bitcast(FP8X4), scales=nsc[:], in_=ng_t[G][:].rearrange("p i m t -> p (i m t)"))
 
-        def stage2(T, on_vector, fine):
-            G, i = T // 2, T % 2
-            c = T // 4
+        def stage2(G, i):
+            c = G // 2
             if i == 0:
                 o_new = osp.tile([P, 2, 2, 256], F32, name="o_sb")
                 o_sb_t[G] = o_new
             o_sb = o_sb_t[G]
-            o_ps = ps.tile([P, KV_OUT], F32, name="o_ps", tag="bank")
+            o_ps = ps_o.tile([P, KV_OUT], F32, name="o_ps")
             sl = slice(128 * i, 128 * i + 128)
             nc.tensor.matmul_mx(
                 out=o_ps[:],
@@ -281,9 +285,9 @@ def tile_multiheadlatentattention_pa_t_kernel(tc, x, Wkv_a, kv_norm_w, Wkv_b, ou
                 start=True,
                 stop=True,
             )
-            copy_on(on_vector, o_sb[:, :, i, :], o_ps[:].rearrange("p (kv n) -> p kv n", kv=2))
+            nc.scalar.copy(out=o_sb[:, :, i, :], in_=o_ps[:].rearrange("p (kv n) -> p kv n", kv=2))
             j0 = 2 * (G % 2)
-            if fine:
+            if G == PAIRS - 1:
                 nc.sync.dma_start(out=o0v[c][:, j0 + i, :], in_=o_sb[:, 0, i, :])
                 nc.sync.dma_start(out=o1v[c][:, j0 + i, :], in_=o_sb[:, 1, i, :])
             elif i == 1:
@@ -291,7 +295,7 @@ def tile_multiheadlatentattention_pa_t_kernel(tc, x, Wkv_a, kv_norm_w, Wkv_b, ou
                 nc.sync.dma_start(out=o1v[c][:, j0 : j0 + 2, :], in_=o_sb[:, 1, :, :])
 
         def rope_mm(c):
-            r_ps = ps.tile([P, 4, ROPE], F32, name="r_ps", tag="bank")
+            r_ps = ps_r.tile([P, 4, ROPE], F32, name="r_ps")
             r_t[c] = r_ps
             for j in range(4):
                 G = 2 * c + j // 2
@@ -322,42 +326,53 @@ def tile_multiheadlatentattention_pa_t_kernel(tc, x, Wkv_a, kv_norm_w, Wkv_b, ou
             nc.gpsimd.tensor_tensor(out=kr[:], in0=m1[:], in1=m2[:].rearrange("p two n -> p n two"), op=ALU.add)
             nc.sync.dma_start(out=o2v[c], in_=kr[:].rearrange("p n two -> p (n two)"))
 
-        first = 0
-        for k in range(len(GROUPS)):
-            tiles = list(range(first, first + GROUPS[k]))
-            first += GROUPS[k]
-            pairs = [T // 2 for T in tiles[0::2]]
-            last_group = k == len(GROUPS) - 1
-            for idx in range(len(tiles)):
-                x_transpose(tiles[idx], idx in X_ON_V)
-                if k == 0 and idx == 1:
-                    rope_tables_a()
-                    wa_regroup(0)
-                if k == 0 and idx == 3:
-                    wa_regroup(1)
-                    wa_quant(0)
-                    wa_quant(1)
-                if idx % 2 == 1 and idx >= 3:
-                    x_quant(pairs[idx // 2 - 1])
-            x_quant(pairs[-1])
-            if k == 0:
-                rope_tables_b()
+        x_next = [0]
+
+        def x_pe():
+            if x_next[0] < PAIRS:
+                x_transpose(x_next[0])
+
+        def x_v():
+            if x_next[0] < PAIRS:
+                x_quant(x_next[0])
+                x_next[0] += 1
+
+        wa_regroup(0)
+        wa_quant(0)
+        x_pe()
+        wa_regroup(1)
+        x_v()
+        wa_quant(1)
+        for r in range(0, PAIRS + 4):
+            x_pe()
+            if 0 <= r - 2 < PAIRS:
+                n_transpose(r - 2)
+            if 0 <= r - 1 < PAIRS:
+                norm(r - 1)
+            if 0 <= r - 2 < PAIRS:
+                n_copy(r - 2)
+            for i in range(2):
+                if 0 <= r - 3 < PAIRS:
+                    stage2(r - 3, i)
+                if 0 <= r < PAIRS:
+                    stage1(r, i)
+            x_v()
+            if 0 <= r - 2 < PAIRS:
+                n_quant(r - 2)
+            cr = r - 1 - ROPE_LAG
+            if cr >= 0 and cr % 2 == 1 and cr // 2 < CHUNKS:
+                rope_ew(cr // 2)
+            if cr >= 0 and cr % 2 == 0 and cr // 2 < CHUNKS:
+                rope_mm(cr // 2)
+            if r < X_EXTRA:
+                x_pe()
+                x_v()
+            if r == 0:
+                tables_b()
                 war_regroup()
-                war_quant()
-            for idx in range(len(tiles)):
-                stage1(tiles[idx])
-                if idx % 4 == 1:
-                    rope_mm(tiles[idx] // 4)
-                    rope_ew(tiles[idx] // 4)
-                if idx % 2 == 1:
-                    norm(pairs[idx // 2])
-            if k == 0:
+            if r == 1:
                 wb_regroup()
+                war_quant()
+                rope_tables()
+            if r == 2:
                 wb_quant()
-            for q in range(len(pairs)):
-                n_transpose(pairs[q], q in N_ON_V)
-                if q >= 1:
-                    n_quant(pairs[q - 1])
-            n_quant(pairs[-1])
-            for idx in range(len(tiles)):
-                stage2(tiles[idx], idx in O_ON_V, last_group and idx >= len(tiles) - 2)

@@ -27,9 +27,8 @@ ROPE_BASE = 10000.0
 
 CHUNKS = 8
 PAIRS = 16
-X_EXTRA = 2
 ROPE_LAG = 2
-S_NCOPY = (5, 11)
+S_NCOPY = ()
 
 FLOPS = 2 * TOKENS * D_MODEL * (LATENT + ROPE) + 2 * TOKENS * LATENT * KV_OUT
 
@@ -73,11 +72,11 @@ def tile_multiheadlatentattention_pa_t_kernel(tc, x, Wkv_a, kv_norm_w, Wkv_b, ou
                 in_=wav[:, 2 * g : 2 * g + 2, :],
             )
 
-        nc.scalar.dma_start(out=g_bf[:], in_=kv_norm_w.partition_broadcast(P))
         load_wa(0)
         nc.sync.dma_start(out=x_sb[0][:, 0:2048], in_=xv[0][:, 0:2048])
         load_wa(1)
         nc.sync.dma_start(out=x_sb[0][:, 2048:4096], in_=xv[0][:, 2048:4096])
+        nc.sync.dma_start(out=g_bf[:], in_=kv_norm_w.partition_broadcast(P))
         nc.sync.dma_start(out=x_sb[1][:], in_=xv[1])
         nc.sync.dma_start(out=wb_raw[:], in_=wbv)
         for c in range(2, CHUNKS):
@@ -118,15 +117,17 @@ def tile_multiheadlatentattention_pa_t_kernel(tc, x, Wkv_a, kv_norm_w, Wkv_b, ou
         sin_t = turns[:].rearrange("p a i -> p (a i)")
         nc.vector.tensor_tensor(out=sin_t, in0=sin_t, in1=whole[:].rearrange("p a i -> p (a i)"), op=ALU.subtract)
         cos_t = const.tile([P, 1024], F32, name="cos_t")
+        sin_v = const.tile([P, 1024], F32, name="sin_v")
 
         def tables_b():
-            nc.vector.tensor_scalar(out=cos_t[:], in0=sin_t, scalar1=0.25, scalar2=None, op0=ALU.add)
-            nc.vector.scalar_tensor_tensor(out=sin_t, in0=sin_t, scalar=0.5, in1=sin_t, op0=ALU.is_gt, op1=ALU.subtract)
-            nc.vector.scalar_tensor_tensor(out=cos_t[:], in0=cos_t[:], scalar=0.5, in1=cos_t[:], op0=ALU.is_gt, op1=ALU.subtract)
+            nc.vector.scalar_tensor_tensor(out=cos_t[:], in0=sin_t, scalar=-1.0, in1=sin_t, op0=ALU.mult, op1=ALU.min)
+            nc.vector.tensor_scalar(out=cos_t[:], in0=cos_t[:], scalar1=0.25, scalar2=None, op0=ALU.add)
 
-        def rope_tables():
-            nc.scalar.activation(out=sin_t, in_=sin_t, func=ACT.Sin, scale=-2.0 * math.pi)
-            nc.scalar.activation(out=cos_t[:], in_=cos_t[:], func=ACT.Sin, scale=-2.0 * math.pi)
+        def rope_table_sin():
+            nc.scalar.activation(out=sin_v[:], in_=sin_t, func=ACT.Sin, scale=2.0 * math.pi)
+
+        def rope_table_cos():
+            nc.scalar.activation(out=cos_t[:], in_=cos_t[:], func=ACT.Sin, scale=2.0 * math.pi)
 
         wag_c = const.tile([P, 2, 512, 4], BF16, name="wag_c", align_bytes=64)
         wag_r = const.tile([P, 2, 128, 4], BF16, name="wag_r", align_bytes=64)
@@ -148,7 +149,7 @@ def tile_multiheadlatentattention_pa_t_kernel(tc, x, Wkv_a, kv_norm_w, Wkv_b, ou
 
         def war_regroup():
             for g in range(2):
-                nc.scalar.copy(out=wag_r[:, g, :, :], in_=wa_raw[:, 4 * g : 4 * g + 4, 512:640].rearrange("q t n -> q n t"))
+                nc.vector.tensor_copy(out=wag_r[:, g, :, :], in_=wa_raw[:, 4 * g : 4 * g + 4, 512:640].rearrange("q t n -> q n t"))
 
         def war_quant():
             for g in range(2):
@@ -159,7 +160,7 @@ def tile_multiheadlatentattention_pa_t_kernel(tc, x, Wkv_a, kv_norm_w, Wkv_b, ou
         def wb_regroup():
             src = wb_raw[:].rearrange("p t (h kv d) -> p kv h d t", h=2, kv=2, d=128)
             for kv in range(2):
-                nc.scalar.copy(
+                nc.vector.tensor_copy(
                     out=wbg[:, 256 * kv : 256 * kv + 256, :].rearrange("p (h d) t -> p h d t", h=2),
                     in_=src[:, kv],
                 )
@@ -316,14 +317,15 @@ def tile_multiheadlatentattention_pa_t_kernel(tc, x, Wkv_a, kv_norm_w, Wkv_b, ou
             cm = c % 4
             rv = r_t[c][:].rearrange("p j (i two) -> p (j i) two", two=2)
             cosv = cos_t[:, 256 * cm : 256 * cm + 256]
-            sinv = sin_t[:, 256 * cm : 256 * cm + 256]
+            sinv = sin_v[:, 256 * cm : 256 * cm + 256]
             m1 = rop.tile([P, 256, 2], F32, name="m1")
             m2 = rop.tile([P, 2, 256], F32, name="m2")
             kr = rop.tile([P, 256, 2], F32, name="kr")
             nc.vector.tensor_tensor(out=m1[:], in0=rv, in1=cosv.unsqueeze(2).to_broadcast([P, 256, 2]), op=ALU.mult)
             nc.vector.scalar_tensor_tensor(out=m2[:, 0, :], in0=rv[:, :, 1], scalar=-1.0, in1=sinv, op0=ALU.mult, op1=ALU.mult)
             nc.vector.tensor_tensor(out=m2[:, 1, :], in0=rv[:, :, 0], in1=sinv, op=ALU.mult)
-            nc.gpsimd.tensor_tensor(out=kr[:], in0=m1[:], in1=m2[:].rearrange("p two n -> p n two"), op=ALU.add)
+            adder = nc.vector if c == CHUNKS - 1 else nc.gpsimd
+            adder.tensor_tensor(out=kr[:], in0=m1[:], in1=m2[:].rearrange("p two n -> p n two"), op=ALU.add)
             nc.sync.dma_start(out=o2v[c], in_=kr[:].rearrange("p n two -> p (n two)"))
 
         x_next = [0]
@@ -340,6 +342,7 @@ def tile_multiheadlatentattention_pa_t_kernel(tc, x, Wkv_a, kv_norm_w, Wkv_b, ou
         wa_regroup(0)
         wa_quant(0)
         x_pe()
+        rope_table_sin()
         wa_regroup(1)
         x_v()
         wa_quant(1)
@@ -349,30 +352,30 @@ def tile_multiheadlatentattention_pa_t_kernel(tc, x, Wkv_a, kv_norm_w, Wkv_b, ou
                 n_transpose(r - 2)
             if 0 <= r - 1 < PAIRS:
                 norm(r - 1)
+            if r == 1:
+                war_regroup()
             if 0 <= r - 2 < PAIRS:
                 n_copy(r - 2)
+            if r == 2:
+                wb_regroup()
             for i in range(2):
                 if 0 <= r - 3 < PAIRS:
                     stage2(r - 3, i)
                 if 0 <= r < PAIRS:
                     stage1(r, i)
             x_v()
+            if r == 1:
+                war_quant()
             if 0 <= r - 2 < PAIRS:
                 n_quant(r - 2)
+            if r == 2:
+                wb_quant()
             cr = r - 1 - ROPE_LAG
             if cr >= 0 and cr % 2 == 1 and cr // 2 < CHUNKS:
                 rope_ew(cr // 2)
             if cr >= 0 and cr % 2 == 0 and cr // 2 < CHUNKS:
                 rope_mm(cr // 2)
-            if r < X_EXTRA:
-                x_pe()
-                x_v()
             if r == 0:
                 tables_b()
-                war_regroup()
             if r == 1:
-                wb_regroup()
-                war_quant()
-                rope_tables()
-            if r == 2:
-                wb_quant()
+                rope_table_cos()

@@ -1,9 +1,7 @@
 import math
 from contextlib import ExitStack
 
-import concourse.bass as bass
 import concourse.mybir as mybir
-import concourse.tile as tile
 from concourse.masks import make_identity
 
 F32 = mybir.dt.float32
@@ -21,361 +19,397 @@ D_MODEL = 1024
 LATENT = 512
 ROPE = 128
 KV_OUT = 512
-SEQ = 2048
 RMS_EPS = 1.1920928955078125e-07
 ROPE_BASE = 10000.0
 
 CHUNKS = 8
 PAIRS = 16
-ROPE_LAG = 2
-S_NCOPY = ()
+SEQ_TILES = 16
+HALF_ROPE = ROPE // 2
+
+WA_SPLIT = 320
 
 FLOPS = 2 * TOKENS * D_MODEL * (LATENT + ROPE) + 2 * TOKENS * LATENT * KV_OUT
 
 
 def tile_multiheadlatentattention_pa_t_kernel(tc, x, Wkv_a, kv_norm_w, Wkv_b, out_0, out_1, out_2):
     nc = tc.nc
-    xv = x.rearrange("b s k -> (b s) k").rearrange("(c p j) k -> c p (j k)", p=P, j=4)
-    o0v = out_0.rearrange("b s h d -> (b s) (h d)").rearrange("(c p j) n -> c p j n", p=P, j=4)
-    o1v = out_1.rearrange("b s h d -> (b s) (h d)").rearrange("(c p j) n -> c p j n", p=P, j=4)
-    o2v = out_2.rearrange("b s h d -> (b s) (h d)").rearrange("(c p j) n -> c p (j n)", p=P, j=4)
-    wav = Wkv_a.rearrange("(a q e) n -> q a (e n)", a=4, q=P, e=2)
-    wbv = Wkv_b.rearrange("(t p) n -> p t n", t=4, p=P)
+
+    x_view = x.rearrange("b s k -> (b s) k").rearrange("(c p j) k -> c p (j k)", p=P, j=4)
+    k_nope_view = out_0.rearrange("b s h d -> (b s) (h d)").rearrange("(c p j) n -> c p j n", p=P, j=4)
+    v_view = out_1.rearrange("b s h d -> (b s) (h d)").rearrange("(c p j) n -> c p j n", p=P, j=4)
+    k_rope_view = out_2.rearrange("b s h d -> (b s) (h d)").rearrange("(c p j) n -> c p (j n)", p=P, j=4)
+    wa_view = Wkv_a.rearrange("(a q e) n -> q a (e n)", a=4, q=P, e=2)
+    wb_view = Wkv_b.rearrange("(t p) n -> p t n", t=4, p=P)
 
     with ExitStack() as ctx:
-        const = ctx.enter_context(tc.tile_pool(name="const", bufs=1))
-        xgp = ctx.enter_context(tc.tile_pool(name="xgp", bufs=3))
-        small = ctx.enter_context(tc.tile_pool(name="small", bufs=4))
-        junkp = ctx.enter_context(tc.tile_pool(name="junkp", bufs=2))
-        nsp = ctx.enter_context(tc.tile_pool(name="nsp", bufs=3))
-        ngp = ctx.enter_context(tc.tile_pool(name="ngp", bufs=2))
-        ncp = ctx.enter_context(tc.tile_pool(name="ncp", bufs=3))
-        osp = ctx.enter_context(tc.tile_pool(name="osp", bufs=4))
-        rop = ctx.enter_context(tc.tile_pool(name="rop", bufs=2))
-        ps_xt = ctx.enter_context(tc.psum_pool(name="ps_xt", bufs=2))
-        ps_c = ctx.enter_context(tc.psum_pool(name="ps_c", bufs=3))
-        ps_nt = ctx.enter_context(tc.psum_pool(name="ps_nt", bufs=1))
-        ps_o = ctx.enter_context(tc.psum_pool(name="ps_o", bufs=1))
-        ps_r = ctx.enter_context(tc.psum_pool(name="ps_r", bufs=1))
+        keep = ctx.enter_context(tc.tile_pool(name="keep", bufs=1))
+        x_grouped_pool = ctx.enter_context(tc.tile_pool(name="x_grouped_pool", bufs=3))
+        stat_pool = ctx.enter_context(tc.tile_pool(name="stat_pool", bufs=4))
+        squares_pool = ctx.enter_context(tc.tile_pool(name="squares_pool", bufs=2))
+        n_pool = ctx.enter_context(tc.tile_pool(name="n_pool", bufs=3))
+        n_grouped_pool = ctx.enter_context(tc.tile_pool(name="n_grouped_pool", bufs=2))
+        n_words_pool = ctx.enter_context(tc.tile_pool(name="n_words_pool", bufs=3))
+        kv_pool = ctx.enter_context(tc.tile_pool(name="kv_pool", bufs=4))
+        rope_pool = ctx.enter_context(tc.tile_pool(name="rope_pool", bufs=2))
+        psum_xt = ctx.enter_context(tc.psum_pool(name="psum_xt", bufs=2))
+        psum_latent = ctx.enter_context(tc.psum_pool(name="psum_latent", bufs=3))
+        psum_nt = ctx.enter_context(tc.psum_pool(name="psum_nt", bufs=1))
+        psum_kv = ctx.enter_context(tc.psum_pool(name="psum_kv", bufs=1))
+        psum_rope = ctx.enter_context(tc.psum_pool(name="psum_rope", bufs=1))
         ctx.enter_context(tc.manual_schedule())
 
-        x_sb = []
+        x_rows = []
         for c in range(CHUNKS):
-            x_sb.append(const.tile([P, 4096], BF16, name="x_sb%d" % c))
-        wa_raw = const.tile([P, 8, 640], BF16, name="wa_raw")
-        wb_raw = const.tile([P, 4, 512], BF16, name="wb_raw")
-        g_bf = const.tile([P, LATENT], BF16, name="g_bf")
+            x_rows.append(keep.tile([P, 4 * D_MODEL], BF16, name="x_rows%d" % c))
+        wa_rows = keep.tile([P, 8, LATENT + ROPE], BF16, name="wa_rows")
+        wb_rows = keep.tile([P, 4, KV_OUT], BF16, name="wb_rows")
+        gain = keep.tile([P, LATENT], BF16, name="gain")
 
         def load_wa(g):
             nc.sync.dma_start(
-                out=wa_raw[:, 4 * g : 4 * g + 4, :].rearrange("q (a e) n -> q a (e n)", a=2, e=2),
-                in_=wav[:, 2 * g : 2 * g + 2, :],
+                out=wa_rows[:, 4 * g : 4 * g + 4, :].rearrange("q (a e) n -> q a (e n)", a=2, e=2),
+                in_=wa_view[:, 2 * g : 2 * g + 2, :],
             )
 
+        half = 2 * D_MODEL
         load_wa(0)
-        nc.sync.dma_start(out=x_sb[0][:, 0:2048], in_=xv[0][:, 0:2048])
+        nc.sync.dma_start(out=x_rows[0][:, 0:half], in_=x_view[0][:, 0:half])
         load_wa(1)
-        nc.sync.dma_start(out=x_sb[0][:, 2048:4096], in_=xv[0][:, 2048:4096])
-        nc.sync.dma_start(out=g_bf[:], in_=kv_norm_w.partition_broadcast(P))
-        nc.sync.dma_start(out=x_sb[1][:], in_=xv[1])
-        nc.sync.dma_start(out=wb_raw[:], in_=wbv)
+        nc.sync.dma_start(out=x_rows[0][:, half : 2 * half], in_=x_view[0][:, half : 2 * half])
+        nc.sync.dma_start(out=gain[:], in_=kv_norm_w.partition_broadcast(P))
+        nc.sync.dma_start(out=x_rows[1][:], in_=x_view[1])
+        nc.sync.dma_start(out=wb_rows[:], in_=wb_view)
         for c in range(2, CHUNKS):
-            nc.sync.dma_start(out=x_sb[c][:], in_=xv[c])
+            nc.sync.dma_start(out=x_rows[c][:], in_=x_view[c])
 
-        pos_i = const.tile([P, 16], I32, name="pos_i")
-        nc.gpsimd.iota(pos_i[:], pattern=[[512, 4], [1, 4]], base=0, channel_multiplier=4)
-        ident_f = const.tile([P, P], F32, name="ident_f")
-        make_identity(nc, ident_f[:])
-        ident_b = const.tile([P, P], BF16, name="ident_b")
-        make_identity(nc, ident_b[:])
-        eps_t = const.tile([P, 1], F32, name="eps_t")
-        nc.vector.memset(eps_t[:], RMS_EPS)
-        warm = const.tile([P, 1], F32, name="warm")
-        nc.scalar.activation(out=warm[:], in_=eps_t[:], func=ACT.Sin)
-        mhalf = const.tile([P, 2], F32, name="mhalf")
-        nc.vector.memset(mhalf[:], -0.5)
+        position_int = keep.tile([P, SEQ_TILES], I32, name="position_int")
+        nc.gpsimd.iota(position_int[:], pattern=[[512, 4], [1, 4]], base=0, channel_multiplier=4)
+        identity_f32 = keep.tile([P, P], F32, name="identity_f32")
+        make_identity(nc, identity_f32[:])
+        identity_bf16 = keep.tile([P, P], BF16, name="identity_bf16")
+        make_identity(nc, identity_bf16[:])
+        minus_half = keep.tile([P, 2], F32, name="minus_half")
+        nc.vector.memset(minus_half[:], -0.5)
+        table_warm = keep.tile([P, 1], F32, name="table_warm")
+        nc.scalar.activation(out=table_warm[:], in_=minus_half[:, 0:1], func=ACT.Sin)
 
-        pos_f = const.tile([P, 16], F32, name="pos_f")
-        nc.vector.tensor_copy(out=pos_f[:], in_=pos_i[:])
-        frq = const.tile([P, 64], F32, name="frq")
-        nc.vector.memset(frq[:, 0:1], 1.0)
-        nc.vector.tensor_scalar(out=frq[:, 0:1], in0=frq[:, 0:1], scalar1=1.0 / (2.0 * math.pi), scalar2=None, op0=ALU.mult)
-        ratio = ROPE_BASE ** (-1.0 / 64.0)
-        w = 1
-        while w < 64:
-            nc.vector.tensor_scalar(out=frq[:, w : 2 * w], in0=frq[:, 0:w], scalar1=ratio**w, scalar2=None, op0=ALU.mult)
-            w *= 2
-        turns = const.tile([P, 16, 64], F32, name="turns")
+        position = keep.tile([P, SEQ_TILES], F32, name="position")
+        nc.vector.tensor_copy(out=position[:], in_=position_int[:])
+        frequency = keep.tile([P, HALF_ROPE], F32, name="frequency")
+        nc.vector.memset(frequency[:, 0:1], 1.0)
+        nc.vector.tensor_scalar(
+            out=frequency[:, 0:1], in0=frequency[:, 0:1], scalar1=1.0 / (2.0 * math.pi), scalar2=None, op0=ALU.mult
+        )
+        ratio = ROPE_BASE ** (-1.0 / HALF_ROPE)
+        filled = 1
+        while filled < HALF_ROPE:
+            nc.vector.tensor_scalar(
+                out=frequency[:, filled : 2 * filled],
+                in0=frequency[:, 0:filled],
+                scalar1=ratio**filled,
+                scalar2=None,
+                op0=ALU.mult,
+            )
+            filled *= 2
+        table_shape = [P, SEQ_TILES, HALF_ROPE]
+        turns = keep.tile(table_shape, F32, name="turns")
         nc.vector.tensor_tensor(
             out=turns[:],
-            in0=pos_f[:].unsqueeze(2).to_broadcast([P, 16, 64]),
-            in1=frq[:].unsqueeze(1).to_broadcast([P, 16, 64]),
+            in0=position[:].unsqueeze(2).to_broadcast(table_shape),
+            in1=frequency[:].unsqueeze(1).to_broadcast(table_shape),
             op=ALU.mult,
         )
-        whole = const.tile([P, 16, 64], I32, name="whole")
-        nc.vector.tensor_copy(out=whole[:], in_=turns[:])
-        sin_t = turns[:].rearrange("p a i -> p (a i)")
-        nc.vector.tensor_tensor(out=sin_t, in0=sin_t, in1=whole[:].rearrange("p a i -> p (a i)"), op=ALU.subtract)
-        cos_t = const.tile([P, 1024], F32, name="cos_t")
-        sin_v = const.tile([P, 1024], F32, name="sin_v")
+        whole_turns = keep.tile(table_shape, I32, name="whole_turns")
+        nc.vector.tensor_copy(out=whole_turns[:], in_=turns[:])
+        fraction = turns[:].rearrange("p a i -> p (a i)")
+        sin_table = keep.tile([P, SEQ_TILES * HALF_ROPE], F32, name="sin_table")
+        cos_table = keep.tile([P, SEQ_TILES * HALF_ROPE], F32, name="cos_table")
 
-        def tables_b():
-            nc.vector.scalar_tensor_tensor(out=cos_t[:], in0=sin_t, scalar=-1.0, in1=sin_t, op0=ALU.mult, op1=ALU.min)
-            nc.vector.tensor_scalar(out=cos_t[:], in0=cos_t[:], scalar1=0.25, scalar2=None, op0=ALU.add)
+        def table_arguments():
+            nc.vector.tensor_tensor(
+                out=fraction, in0=fraction, in1=whole_turns[:].rearrange("p a i -> p (a i)"), op=ALU.subtract
+            )
+            nc.vector.scalar_tensor_tensor(
+                out=cos_table[:], in0=fraction, scalar=-1.0, in1=fraction, op0=ALU.mult, op1=ALU.min
+            )
+            nc.vector.tensor_scalar(out=cos_table[:], in0=cos_table[:], scalar1=0.25, scalar2=None, op0=ALU.add)
 
-        def rope_table_sin():
-            nc.scalar.activation(out=sin_v[:], in_=sin_t, func=ACT.Sin, scale=2.0 * math.pi)
+        def table_sin():
+            nc.scalar.activation(out=sin_table[:], in_=fraction, func=ACT.Sin, scale=2.0 * math.pi)
 
-        def rope_table_cos():
-            nc.scalar.activation(out=cos_t[:], in_=cos_t[:], func=ACT.Sin, scale=2.0 * math.pi)
+        def table_cos():
+            nc.scalar.activation(out=cos_table[:], in_=cos_table[:], func=ACT.Sin, scale=2.0 * math.pi)
 
-        wag_c = const.tile([P, 2, 512, 4], BF16, name="wag_c", align_bytes=64)
-        wag_r = const.tile([P, 2, 128, 4], BF16, name="wag_r", align_bytes=64)
-        wac = const.tile([P, 2, 512], U32, name="wac", align_bytes=64)
-        was = const.tile([P, 2, 512], U8, name="was", align_bytes=64)
-        war = const.tile([P, 2, 128], U32, name="war", align_bytes=64)
-        wars = const.tile([P, 2, 128], U8, name="wars", align_bytes=64)
-        wbg = const.tile([P, 512, 4], BF16, name="wbg", align_bytes=64)
-        wbc = const.tile([P, 512], U32, name="wbc", align_bytes=64)
-        wbs = const.tile([P, 512], U8, name="wbs", align_bytes=64)
+        wa_latent_grouped = keep.tile([P, 2, LATENT, 4], BF16, name="wa_latent_grouped", align_bytes=64)
+        wa_rope_grouped = keep.tile([P, 2, ROPE, 4], BF16, name="wa_rope_grouped", align_bytes=64)
+        wa_latent_words = keep.tile([P, 2, LATENT], U32, name="wa_latent_words", align_bytes=64)
+        wa_latent_plane = keep.tile([P, 2, LATENT], U8, name="wa_latent_plane", align_bytes=64)
+        wa_rope_words = keep.tile([P, 2, ROPE], U32, name="wa_rope_words", align_bytes=64)
+        wa_rope_plane = keep.tile([P, 2, ROPE], U8, name="wa_rope_plane", align_bytes=64)
+        wb_grouped = keep.tile([P, KV_OUT, 4], BF16, name="wb_grouped", align_bytes=64)
+        wb_words = keep.tile([P, KV_OUT], U32, name="wb_words", align_bytes=64)
+        wb_plane = keep.tile([P, KV_OUT], U8, name="wb_plane", align_bytes=64)
 
-        def wa_regroup(g):
-            nc.vector.tensor_copy(out=wag_c[:, g, :, :], in_=wa_raw[:, 4 * g : 4 * g + 4, 0:512].rearrange("q t n -> q n t"))
+        def regroup_wa_latent(g, first, last, on_vector):
+            grouped = wa_latent_grouped[:, g, first:last, :]
+            rows = wa_rows[:, 4 * g : 4 * g + 4, first:last].rearrange("q t n -> q n t")
+            if on_vector:
+                nc.vector.tensor_copy(out=grouped, in_=rows)
+            else:
+                nc.scalar.copy(out=grouped, in_=rows)
 
-        def wa_quant(g):
+        def quantise_wa_latent(g):
             nc.vector.quantize_mx(
-                out=wac[:, g, :].bitcast(FP8X4), scales=was[:, g, :], in_=wag_c[:, g, :, :].rearrange("q n t -> q (n t)")
+                out=wa_latent_words[:, g, :].bitcast(FP8X4),
+                scales=wa_latent_plane[:, g, :],
+                in_=wa_latent_grouped[:, g, :, :].rearrange("q n t -> q (n t)"),
             )
 
-        def war_regroup():
-            for g in range(2):
-                nc.vector.tensor_copy(out=wag_r[:, g, :, :], in_=wa_raw[:, 4 * g : 4 * g + 4, 512:640].rearrange("q t n -> q n t"))
+        def copy_on_gpsimd(out, in_):
+            nc.gpsimd.tensor_scalar(out=out, in0=in_, scalar1=1.0, scalar2=0.0, op0=ALU.mult, op1=ALU.add)
 
-        def war_quant():
+        def regroup_wa_rope():
+            for g in range(2):
+                copy_on_gpsimd(
+                    wa_rope_grouped[:, g, :, :],
+                    wa_rows[:, 4 * g : 4 * g + 4, LATENT : LATENT + ROPE].rearrange("q t n -> q n t"),
+                )
+
+        def quantise_wa_rope():
             for g in range(2):
                 nc.vector.quantize_mx(
-                    out=war[:, g, :].bitcast(FP8X4), scales=wars[:, g, :], in_=wag_r[:, g, :, :].rearrange("q n t -> q (n t)")
+                    out=wa_rope_words[:, g, :].bitcast(FP8X4),
+                    scales=wa_rope_plane[:, g, :],
+                    in_=wa_rope_grouped[:, g, :, :].rearrange("q n t -> q (n t)"),
                 )
 
-        def wb_regroup():
-            src = wb_raw[:].rearrange("p t (h kv d) -> p kv h d t", h=2, kv=2, d=128)
+        def regroup_wb():
+            rows = wb_rows[:].rearrange("p t (h kv d) -> p kv h d t", h=2, kv=2, d=128)
             for kv in range(2):
-                nc.vector.tensor_copy(
-                    out=wbg[:, 256 * kv : 256 * kv + 256, :].rearrange("p (h d) t -> p h d t", h=2),
-                    in_=src[:, kv],
+                copy_on_gpsimd(
+                    wb_grouped[:, 256 * kv : 256 * kv + 256, :].rearrange("p (h d) t -> p h d t", h=2), rows[:, kv]
                 )
 
-        def wb_quant():
-            nc.vector.quantize_mx(out=wbc[:].bitcast(FP8X4), scales=wbs[:], in_=wbg[:].rearrange("p n t -> p (n t)"))
+        def quantise_wb():
+            nc.vector.quantize_mx(
+                out=wb_words[:].bitcast(FP8X4), scales=wb_plane[:], in_=wb_grouped[:].rearrange("p n t -> p (n t)")
+            )
 
-        xg_t = {}
-        xc_t = {}
-        xs_t = {}
-        c_t = {}
-        ss_t = {}
-        sd_t = {}
-        n_t = {}
-        nt_t = {}
-        ng_t = {}
-        nc_t = {}
-        ns_t = {}
-        o_sb_t = {}
-        r_t = {}
+        x_grouped = {}
+        x_words = {}
+        x_plane = {}
+        latent = {}
+        square_sum = {}
+        inv_rms = {}
+        n_rows = {}
+        n_transposed = {}
+        n_grouped = {}
+        n_words = {}
+        n_plane = {}
+        kv_rows = {}
+        rope_raw = {}
 
-        def x_transpose(G):
-            x32 = x_sb[G // 2][:].bitcast(F32)
-            xg = xgp.tile([P, 2048], BF16, name="xg", align_bytes=64)
-            xg_t[G] = xg
-            xg32 = xg[:].bitcast(F32)
+        def transpose_x(pair):
+            words = x_rows[pair // 2][:].bitcast(F32)
+            grouped = x_grouped_pool.tile([P, 2 * D_MODEL], BF16, name="x_grouped", align_bytes=64)
+            x_grouped[pair] = grouped
+            grouped_words = grouped[:].bitcast(F32)
             for i in range(2):
-                j = 2 * (G % 2) + i
-                xt = ps_xt.tile([P, 4, P], F32, name="xt")
-                for wd in range(4):
-                    col = 512 * j + 128 * wd
-                    nc.tensor.transpose(xt[:, wd, :], x32[:, col : col + 128], ident_f[:])
+                j = 2 * (pair % 2) + i
+                xt = psum_xt.tile([P, 4, P], F32, name="xt")
+                for block in range(4):
+                    first = 512 * j + P * block
+                    nc.tensor.transpose(xt[:, block, :], words[:, first : first + P], identity_f32[:])
                 nc.scalar.copy(
-                    out=xg32[:, 512 * i : 512 * i + 512].rearrange("q (g m u) -> q g m u", g=2, m=P, u=2),
+                    out=grouped_words[:, 512 * i : 512 * i + 512].rearrange("q (g m u) -> q g m u", g=2, m=P, u=2),
                     in_=xt[:].rearrange("q (g u) m -> q g m u", g=2, u=2),
                 )
 
-        def x_quant(G):
-            xc = const.tile([P, 512], U32, name="xc%d" % G, align_bytes=64)
-            xs = const.tile([P, 512], U8, name="xs%d" % G, align_bytes=64)
-            xc_t[G] = xc
-            xs_t[G] = xs
-            nc.vector.quantize_mx(out=xc[:].bitcast(FP8X4), scales=xs[:], in_=xg_t[G][:])
+        def quantise_x(pair):
+            words = keep.tile([P, 4 * P], U32, name="x_words%d" % pair, align_bytes=64)
+            plane = keep.tile([P, 4 * P], U8, name="x_plane%d" % pair, align_bytes=64)
+            x_words[pair] = words
+            x_plane[pair] = plane
+            nc.vector.quantize_mx(out=words[:].bitcast(FP8X4), scales=plane[:], in_=x_grouped[pair][:])
 
-        def stage1(G, i):
+        def x_operand(pair, i, g):
+            columns = slice(256 * i + P * g, 256 * i + P * g + P)
+            return x_words[pair][:, columns].bitcast(FP8X4), x_plane[pair][:, columns]
+
+        def stage1(pair, i):
             if i == 0:
-                ss_new = small.tile([P, 2], F32, name="ss")
-                ss_t[G] = ss_new
-            c_ps = ps_c.tile([P, LATENT], F32, name="c_ps")
-            c_t[(G, i)] = c_ps
+                sums = stat_pool.tile([P, 2], F32, name="square_sum")
+                square_sum[pair] = sums
+            bank = psum_latent.tile([P, LATENT], F32, name="latent")
+            latent[(pair, i)] = bank
             for g in range(2):
-                sl = slice(256 * i + 128 * g, 256 * i + 128 * g + 128)
+                words, plane = x_operand(pair, i, g)
                 nc.tensor.matmul_mx(
-                    out=c_ps[:],
-                    lhsT=xc_t[G][:, sl].bitcast(FP8X4),
-                    lhsT_scale=xs_t[G][:, sl],
-                    rhs=wac[:, g, :].bitcast(FP8X4),
-                    rhs_scale=was[:, g, :],
+                    out=bank[:],
+                    lhsT=words,
+                    lhsT_scale=plane,
+                    rhs=wa_latent_words[:, g, :].bitcast(FP8X4),
+                    rhs_scale=wa_latent_plane[:, g, :],
                     start=(g == 0),
                     stop=(g == 1),
                 )
-            junk = junkp.tile([P, LATENT], BF16, name="junk")
-            nc.scalar.activation(out=junk[:], in_=c_ps[:], func=ACT.Square, accum_out=ss_t[G][:, i : i + 1])
+            squares = squares_pool.tile([P, LATENT], BF16, name="squares")
+            nc.scalar.activation(out=squares[:], in_=bank[:], func=ACT.Square, accum_out=square_sum[pair][:, i : i + 1])
             if i == 1:
-                ms = small.tile([P, 2], F32, name="ms")
-                nc.gpsimd.tensor_scalar(out=ms[:], in0=ss_t[G][:], scalar1=1.0 / LATENT, scalar2=RMS_EPS, op0=ALU.mult, op1=ALU.add)
-                rstd = small.tile([P, 2], F32, name="rstd")
-                sd_t[G] = rstd
-                nc.gpsimd.tensor_tensor(out=rstd[:], in0=ms[:], in1=mhalf[:], op=ALU.pow)
+                mean_square = stat_pool.tile([P, 2], F32, name="mean_square")
+                nc.gpsimd.tensor_scalar(
+                    out=mean_square[:],
+                    in0=square_sum[pair][:],
+                    scalar1=1.0 / LATENT,
+                    scalar2=RMS_EPS,
+                    op0=ALU.mult,
+                    op1=ALU.add,
+                )
+                inverse = stat_pool.tile([P, 2], F32, name="inv_rms")
+                inv_rms[pair] = inverse
+                nc.gpsimd.tensor_tensor(out=inverse[:], in0=mean_square[:], in1=minus_half[:], op=ALU.pow)
 
-        def norm(G):
-            rstd = sd_t[G]
-            n_sb = nsp.tile([P, 2, LATENT], BF16, name="n_sb")
-            n_t[G] = n_sb
+        def norm(pair):
+            rows = n_pool.tile([P, 2, LATENT], BF16, name="n_rows")
+            n_rows[pair] = rows
             for i in range(2):
                 nc.vector.scalar_tensor_tensor(
-                    out=n_sb[:, i, :],
-                    in0=c_t[(G, i)][:],
-                    scalar=rstd[:, i : i + 1],
-                    in1=g_bf[:],
+                    out=rows[:, i, :],
+                    in0=latent[(pair, i)][:],
+                    scalar=inv_rms[pair][:, i : i + 1],
+                    in1=gain[:],
                     op0=ALU.mult,
                     op1=ALU.mult,
                 )
 
-        def n_transpose(G):
-            nt = ps_nt.tile([P, 2, 4, P], BF16, name="nt")
-            nt_t[G] = nt
+        def transpose_n(pair):
+            bank = psum_nt.tile([P, 2, 4, P], BF16, name="n_transposed")
+            n_transposed[pair] = bank
             for i in range(2):
                 for t in range(4):
                     nc.tensor.matmul(
-                        out=nt[:, i, t, :], lhsT=n_t[G][:, i, 128 * t : 128 * t + 128], rhs=ident_b[:], start=True, stop=True
+                        out=bank[:, i, t, :],
+                        lhsT=n_rows[pair][:, i, P * t : P * t + P],
+                        rhs=identity_bf16[:],
+                        start=True,
+                        stop=True,
                     )
 
-        def n_copy(G):
-            ng = ngp.tile([P, 2, P, 4], BF16, name="ng", align_bytes=64)
-            ng_t[G] = ng
-            if G in S_NCOPY:
-                nc.scalar.copy(out=ng[:], in_=nt_t[G][:].rearrange("p i t m -> p i m t"))
-            else:
-                nc.vector.tensor_copy(out=ng[:], in_=nt_t[G][:].rearrange("p i t m -> p i m t"))
+        def group_n(pair):
+            grouped = n_grouped_pool.tile([P, 2, P, 4], BF16, name="n_grouped", align_bytes=64)
+            n_grouped[pair] = grouped
+            nc.vector.tensor_copy(out=grouped[:], in_=n_transposed[pair][:].rearrange("p i t m -> p i m t"))
 
-        def n_quant(G):
-            ncd = ncp.tile([P, 256], U32, name="ncd", align_bytes=64)
-            nsc = ncp.tile([P, 256], U8, name="nsc", align_bytes=64)
-            nc_t[G] = ncd
-            ns_t[G] = nsc
-            nc.vector.quantize_mx(out=ncd[:].bitcast(FP8X4), scales=nsc[:], in_=ng_t[G][:].rearrange("p i m t -> p (i m t)"))
+        def quantise_n(pair):
+            words = n_words_pool.tile([P, 2 * P], U32, name="n_words", align_bytes=64)
+            plane = n_words_pool.tile([P, 2 * P], U8, name="n_plane", align_bytes=64)
+            n_words[pair] = words
+            n_plane[pair] = plane
+            nc.vector.quantize_mx(
+                out=words[:].bitcast(FP8X4), scales=plane[:], in_=n_grouped[pair][:].rearrange("p i m t -> p (i m t)")
+            )
 
-        def stage2(G, i):
-            c = G // 2
+        def stage2(pair, i):
+            c = pair // 2
             if i == 0:
-                o_new = osp.tile([P, 2, 2, 256], F32, name="o_sb")
-                o_sb_t[G] = o_new
-            o_sb = o_sb_t[G]
-            o_ps = ps_o.tile([P, KV_OUT], F32, name="o_ps")
-            sl = slice(128 * i, 128 * i + 128)
+                rows = kv_pool.tile([P, 2, 2, 256], F32, name="kv_rows")
+                kv_rows[pair] = rows
+            rows = kv_rows[pair]
+            bank = psum_kv.tile([P, KV_OUT], F32, name="kv")
+            columns = slice(P * i, P * i + P)
             nc.tensor.matmul_mx(
-                out=o_ps[:],
-                lhsT=nc_t[G][:, sl].bitcast(FP8X4),
-                lhsT_scale=ns_t[G][:, sl],
-                rhs=wbc[:].bitcast(FP8X4),
-                rhs_scale=wbs[:],
+                out=bank[:],
+                lhsT=n_words[pair][:, columns].bitcast(FP8X4),
+                lhsT_scale=n_plane[pair][:, columns],
+                rhs=wb_words[:].bitcast(FP8X4),
+                rhs_scale=wb_plane[:],
                 start=True,
                 stop=True,
             )
-            nc.scalar.copy(out=o_sb[:, :, i, :], in_=o_ps[:].rearrange("p (kv n) -> p kv n", kv=2))
-            j0 = 2 * (G % 2)
-            if G == PAIRS - 1:
-                nc.sync.dma_start(out=o0v[c][:, j0 + i, :], in_=o_sb[:, 0, i, :])
-                nc.sync.dma_start(out=o1v[c][:, j0 + i, :], in_=o_sb[:, 1, i, :])
+            nc.scalar.copy(out=rows[:, :, i, :], in_=bank[:].rearrange("p (kv n) -> p kv n", kv=2))
+            j = 2 * (pair % 2)
+            if pair == PAIRS - 1:
+                nc.sync.dma_start(out=k_nope_view[c][:, j + i, :], in_=rows[:, 0, i, :])
+                nc.sync.dma_start(out=v_view[c][:, j + i, :], in_=rows[:, 1, i, :])
             elif i == 1:
-                nc.sync.dma_start(out=o0v[c][:, j0 : j0 + 2, :], in_=o_sb[:, 0, :, :])
-                nc.sync.dma_start(out=o1v[c][:, j0 : j0 + 2, :], in_=o_sb[:, 1, :, :])
+                nc.sync.dma_start(out=k_nope_view[c][:, j : j + 2, :], in_=rows[:, 0, :, :])
+                nc.sync.dma_start(out=v_view[c][:, j : j + 2, :], in_=rows[:, 1, :, :])
 
-        def rope_mm(c):
-            r_ps = ps_r.tile([P, 4, ROPE], F32, name="r_ps")
-            r_t[c] = r_ps
+        def rope_product(c):
+            bank = psum_rope.tile([P, 4, ROPE], F32, name="rope_raw")
+            rope_raw[c] = bank
             for j in range(4):
-                G = 2 * c + j // 2
-                i = j % 2
                 for g in range(2):
-                    sl = slice(256 * i + 128 * g, 256 * i + 128 * g + 128)
+                    words, plane = x_operand(2 * c + j // 2, j % 2, g)
                     nc.tensor.matmul_mx(
-                        out=r_ps[:, j, :],
-                        lhsT=xc_t[G][:, sl].bitcast(FP8X4),
-                        lhsT_scale=xs_t[G][:, sl],
-                        rhs=war[:, g, :].bitcast(FP8X4),
-                        rhs_scale=wars[:, g, :],
+                        out=bank[:, j, :],
+                        lhsT=words,
+                        lhsT_scale=plane,
+                        rhs=wa_rope_words[:, g, :].bitcast(FP8X4),
+                        rhs_scale=wa_rope_plane[:, g, :],
                         start=(g == 0),
                         stop=(g == 1),
                     )
 
-        def rope_ew(c):
-            cm = c % 4
-            rv = r_t[c][:].rearrange("p j (i two) -> p (j i) two", two=2)
-            cosv = cos_t[:, 256 * cm : 256 * cm + 256]
-            sinv = sin_v[:, 256 * cm : 256 * cm + 256]
-            m1 = rop.tile([P, 256, 2], F32, name="m1")
-            m2 = rop.tile([P, 2, 256], F32, name="m2")
-            kr = rop.tile([P, 256, 2], F32, name="kr")
-            nc.vector.tensor_tensor(out=m1[:], in0=rv, in1=cosv.unsqueeze(2).to_broadcast([P, 256, 2]), op=ALU.mult)
-            nc.vector.scalar_tensor_tensor(out=m2[:, 0, :], in0=rv[:, :, 1], scalar=-1.0, in1=sinv, op0=ALU.mult, op1=ALU.mult)
-            nc.vector.tensor_tensor(out=m2[:, 1, :], in0=rv[:, :, 0], in1=sinv, op=ALU.mult)
+        def rope_rotation(c):
+            first = 4 * HALF_ROPE * (c % 4)
+            count = 4 * HALF_ROPE
+            raw = rope_raw[c][:].rearrange("p j (i two) -> p (j i) two", two=2)
+            cos = cos_table[:, first : first + count]
+            sin = sin_table[:, first : first + count]
+            with_cos = rope_pool.tile([P, count, 2], F32, name="with_cos")
+            with_sin = rope_pool.tile([P, 2, count], F32, name="with_sin")
+            rotated = rope_pool.tile([P, count, 2], F32, name="rotated")
+            nc.vector.tensor_tensor(out=with_cos[:], in0=raw, in1=cos.unsqueeze(2).to_broadcast([P, count, 2]), op=ALU.mult)
+            nc.vector.scalar_tensor_tensor(
+                out=with_sin[:, 0, :], in0=raw[:, :, 1], scalar=-1.0, in1=sin, op0=ALU.mult, op1=ALU.mult
+            )
+            nc.vector.tensor_tensor(out=with_sin[:, 1, :], in0=raw[:, :, 0], in1=sin, op=ALU.mult)
             adder = nc.vector if c == CHUNKS - 1 else nc.gpsimd
-            adder.tensor_tensor(out=kr[:], in0=m1[:], in1=m2[:].rearrange("p two n -> p n two"), op=ALU.add)
-            nc.sync.dma_start(out=o2v[c], in_=kr[:].rearrange("p n two -> p (n two)"))
+            adder.tensor_tensor(out=rotated[:], in0=with_cos[:], in1=with_sin[:].rearrange("p two n -> p n two"), op=ALU.add)
+            nc.sync.dma_start(out=k_rope_view[c], in_=rotated[:].rearrange("p n two -> p (n two)"))
 
-        x_next = [0]
+        def live(pair):
+            return 0 <= pair < PAIRS
 
-        def x_pe():
-            if x_next[0] < PAIRS:
-                x_transpose(x_next[0])
-
-        def x_v():
-            if x_next[0] < PAIRS:
-                x_quant(x_next[0])
-                x_next[0] += 1
-
-        wa_regroup(0)
-        wa_quant(0)
-        x_pe()
-        rope_table_sin()
-        wa_regroup(1)
-        x_v()
-        wa_quant(1)
-        for r in range(0, PAIRS + 4):
-            x_pe()
-            if 0 <= r - 2 < PAIRS:
-                n_transpose(r - 2)
-            if 0 <= r - 1 < PAIRS:
+        transpose_x(0)
+        regroup_wa_latent(0, 0, LATENT, True)
+        regroup_wa_latent(1, WA_SPLIT, LATENT, False)
+        quantise_wa_latent(0)
+        regroup_wa_latent(1, 0, WA_SPLIT, True)
+        quantise_x(0)
+        quantise_wa_latent(1)
+        table_arguments()
+        for r in range(PAIRS + 4):
+            if live(r + 1):
+                transpose_x(r + 1)
+            if live(r - 2):
+                transpose_n(r - 2)
+            if live(r - 1):
                 norm(r - 1)
-            if r == 1:
-                war_regroup()
-            if 0 <= r - 2 < PAIRS:
-                n_copy(r - 2)
-            if r == 2:
-                wb_regroup()
+            if live(r - 2):
+                group_n(r - 2)
             for i in range(2):
-                if 0 <= r - 3 < PAIRS:
+                if live(r - 3):
                     stage2(r - 3, i)
-                if 0 <= r < PAIRS:
+                if live(r):
                     stage1(r, i)
-            x_v()
+            if live(r + 1):
+                quantise_x(r + 1)
             if r == 1:
-                war_quant()
-            if 0 <= r - 2 < PAIRS:
-                n_quant(r - 2)
+                quantise_wa_rope()
+            if live(r - 2):
+                quantise_n(r - 2)
             if r == 2:
-                wb_quant()
-            cr = r - 1 - ROPE_LAG
-            if cr >= 0 and cr % 2 == 1 and cr // 2 < CHUNKS:
-                rope_ew(cr // 2)
-            if cr >= 0 and cr % 2 == 0 and cr // 2 < CHUNKS:
-                rope_mm(cr // 2)
+                quantise_wb()
+            if r >= 3 and r % 2 == 1 and (r - 3) // 2 < CHUNKS:
+                rope_rotation((r - 3) // 2)
+            if r >= 2 and r % 2 == 0 and (r - 2) // 2 < CHUNKS:
+                rope_product((r - 2) // 2)
             if r == 0:
-                tables_b()
+                regroup_wa_rope()
+                table_sin()
             if r == 1:
-                rope_table_cos()
+                regroup_wb()
+                table_cos()

@@ -40,7 +40,7 @@ def tile_multiheadlatentattention_pa_t_kernel(tc, x, Wkv_a, kv_norm_w, Wkv_b, ou
     v_view = out_1.rearrange("b s h d -> (b s) (h d)").rearrange("(c p j) n -> c p j n", p=P, j=4)
     k_rope_view = out_2.rearrange("b s h d -> (b s) (h d)").rearrange("(c p j) n -> c p (j n)", p=P, j=4)
     wa_view = Wkv_a.rearrange("(a q e) n -> q a (e n)", a=4, q=P, e=2)
-    wb_view = Wkv_b.rearrange("(t p) n -> p t n", t=4, p=P)
+    wb_view = Wkv_b.rearrange("(u p e) n -> p u (e n)", u=2, p=P, e=2)
 
     with ExitStack() as ctx:
         keep = ctx.enter_context(tc.tile_pool(name="keep", bufs=1))
@@ -79,7 +79,7 @@ def tile_multiheadlatentattention_pa_t_kernel(tc, x, Wkv_a, kv_norm_w, Wkv_b, ou
         nc.sync.dma_start(out=x_rows[0][:, half : 2 * half], in_=x_view[0][:, half : 2 * half])
         nc.sync.dma_start(out=gain[:], in_=kv_norm_w.partition_broadcast(P))
         nc.sync.dma_start(out=x_rows[1][:], in_=x_view[1])
-        nc.sync.dma_start(out=wb_rows[:], in_=wb_view)
+        nc.sync.dma_start(out=wb_rows[:].rearrange("p (u e) n -> p u (e n)", u=2, e=2), in_=wb_view)
         for c in range(2, CHUNKS):
             nc.sync.dma_start(out=x_rows[c][:], in_=x_view[c])
 
@@ -87,8 +87,6 @@ def tile_multiheadlatentattention_pa_t_kernel(tc, x, Wkv_a, kv_norm_w, Wkv_b, ou
         nc.gpsimd.iota(position_int[:], pattern=[[512, 4], [1, 4]], base=0, channel_multiplier=4)
         identity_f32 = keep.tile([P, P], F32, name="identity_f32")
         make_identity(nc, identity_f32[:])
-        identity_bf16 = keep.tile([P, P], BF16, name="identity_bf16")
-        make_identity(nc, identity_bf16[:])
         minus_half = keep.tile([P, 2], F32, name="minus_half")
         nc.vector.memset(minus_half[:], -0.5)
         table_warm = keep.tile([P, 1], F32, name="table_warm")
@@ -284,22 +282,21 @@ def tile_multiheadlatentattention_pa_t_kernel(tc, x, Wkv_a, kv_norm_w, Wkv_b, ou
                 )
 
         def transpose_n(pair):
-            bank = psum_nt.tile([P, 2, 4, P], BF16, name="n_transposed")
+            bank = psum_nt.tile([P, 2, 2, P], F32, name="n_transposed")
             n_transposed[pair] = bank
+            words = n_rows[pair][:].rearrange("p i n -> p (i n)").bitcast(F32)
             for i in range(2):
-                for t in range(4):
-                    nc.tensor.matmul(
-                        out=bank[:, i, t, :],
-                        lhsT=n_rows[pair][:, i, P * t : P * t + P],
-                        rhs=identity_bf16[:],
-                        start=True,
-                        stop=True,
-                    )
+                for u in range(2):
+                    first = 256 * i + P * u
+                    nc.tensor.transpose(bank[:, i, u, :], words[:, first : first + P], identity_f32[:])
 
         def group_n(pair):
-            grouped = n_grouped_pool.tile([P, 2, P, 4], BF16, name="n_grouped", align_bytes=64)
+            grouped = n_grouped_pool.tile([P, 8 * P], BF16, name="n_grouped", align_bytes=64)
             n_grouped[pair] = grouped
-            nc.vector.tensor_copy(out=grouped[:], in_=n_transposed[pair][:].rearrange("p i t m -> p i m t"))
+            nc.vector.tensor_copy(
+                out=grouped[:].bitcast(F32).rearrange("p (i m u) -> p i m u", i=2, m=P, u=2),
+                in_=n_transposed[pair][:].rearrange("p i u m -> p i m u"),
+            )
 
         def quantise_n(pair):
             words = n_words_pool.tile([P, 2 * P], U32, name="n_words", align_bytes=64)
@@ -307,7 +304,7 @@ def tile_multiheadlatentattention_pa_t_kernel(tc, x, Wkv_a, kv_norm_w, Wkv_b, ou
             n_words[pair] = words
             n_plane[pair] = plane
             nc.vector.quantize_mx(
-                out=words[:].bitcast(FP8X4), scales=plane[:], in_=n_grouped[pair][:].rearrange("p i m t -> p (i m t)")
+                out=words[:].bitcast(FP8X4), scales=plane[:], in_=n_grouped[pair][:]
             )
 
         def stage2(pair, i):

@@ -27,7 +27,7 @@ PAIRS = 16
 SEQ_TILES = 16
 HALF_ROPE = ROPE // 2
 
-WA_SPLIT = 320
+WA_SPLIT = (384, 256)
 
 FLOPS = 2 * TOKENS * D_MODEL * (LATENT + ROPE) + 2 * TOKENS * LATENT * KV_OUT
 
@@ -73,8 +73,8 @@ def tile_multiheadlatentattention_pa_t_kernel(tc, x, Wkv_a, kv_norm_w, Wkv_b, ou
             )
 
         half = 2 * D_MODEL
-        load_wa(0)
         nc.sync.dma_start(out=x_rows[0][:, 0:half], in_=x_view[0][:, 0:half])
+        load_wa(0)
         load_wa(1)
         nc.sync.dma_start(out=x_rows[0][:, half : 2 * half], in_=x_view[0][:, half : 2 * half])
         nc.sync.dma_start(out=gain[:], in_=kv_norm_w.partition_broadcast(P))
@@ -87,10 +87,10 @@ def tile_multiheadlatentattention_pa_t_kernel(tc, x, Wkv_a, kv_norm_w, Wkv_b, ou
         nc.gpsimd.iota(position_int[:], pattern=[[512, 4], [1, 4]], base=0, channel_multiplier=4)
         identity_f32 = keep.tile([P, P], F32, name="identity_f32")
         make_identity(nc, identity_f32[:])
-        minus_half = keep.tile([P, 2], F32, name="minus_half")
+        minus_half = keep.tile([P, 1], F32, name="minus_half")
         nc.vector.memset(minus_half[:], -0.5)
         table_warm = keep.tile([P, 1], F32, name="table_warm")
-        nc.scalar.activation(out=table_warm[:], in_=minus_half[:, 0:1], func=ACT.Sin)
+        nc.scalar.activation(out=table_warm[:], in_=minus_half[:], func=ACT.Sin)
 
         position = keep.tile([P, SEQ_TILES], F32, name="position")
         nc.vector.tensor_copy(out=position[:], in_=position_int[:])
@@ -124,20 +124,23 @@ def tile_multiheadlatentattention_pa_t_kernel(tc, x, Wkv_a, kv_norm_w, Wkv_b, ou
         sin_table = keep.tile([P, SEQ_TILES * HALF_ROPE], F32, name="sin_table")
         cos_table = keep.tile([P, SEQ_TILES * HALF_ROPE], F32, name="cos_table")
 
-        def table_arguments():
+        def table_fraction():
             nc.vector.tensor_tensor(
                 out=fraction, in0=fraction, in1=whole_turns[:].rearrange("p a i -> p (a i)"), op=ALU.subtract
             )
+
+        def table_fold():
             nc.vector.scalar_tensor_tensor(
                 out=cos_table[:], in0=fraction, scalar=-1.0, in1=fraction, op0=ALU.mult, op1=ALU.min
             )
-            nc.vector.tensor_scalar(out=cos_table[:], in0=cos_table[:], scalar1=0.25, scalar2=None, op0=ALU.add)
 
         def table_sin():
             nc.scalar.activation(out=sin_table[:], in_=fraction, func=ACT.Sin, scale=2.0 * math.pi)
 
         def table_cos():
-            nc.scalar.activation(out=cos_table[:], in_=cos_table[:], func=ACT.Sin, scale=2.0 * math.pi)
+            nc.scalar.activation(
+                out=cos_table[:], in_=cos_table[:], func=ACT.Sin, scale=2.0 * math.pi, bias=0.5 * math.pi
+            )
 
         wa_latent_grouped = keep.tile([P, 2, LATENT, 4], BF16, name="wa_latent_grouped", align_bytes=64)
         wa_rope_grouped = keep.tile([P, 2, ROPE, 4], BF16, name="wa_rope_grouped", align_bytes=64)
@@ -164,14 +167,11 @@ def tile_multiheadlatentattention_pa_t_kernel(tc, x, Wkv_a, kv_norm_w, Wkv_b, ou
                 in_=wa_latent_grouped[:, g, :, :].rearrange("q n t -> q (n t)"),
             )
 
-        def copy_on_gpsimd(out, in_):
-            nc.gpsimd.tensor_scalar(out=out, in0=in_, scalar1=1.0, scalar2=0.0, op0=ALU.mult, op1=ALU.add)
-
         def regroup_wa_rope():
             for g in range(2):
-                copy_on_gpsimd(
-                    wa_rope_grouped[:, g, :, :],
-                    wa_rows[:, 4 * g : 4 * g + 4, LATENT : LATENT + ROPE].rearrange("q t n -> q n t"),
+                nc.vector.tensor_copy(
+                    out=wa_rope_grouped[:, g, :, :],
+                    in_=wa_rows[:, 4 * g : 4 * g + 4, LATENT : LATENT + ROPE].rearrange("q t n -> q n t"),
                 )
 
         def quantise_wa_rope():
@@ -185,8 +185,8 @@ def tile_multiheadlatentattention_pa_t_kernel(tc, x, Wkv_a, kv_norm_w, Wkv_b, ou
         def regroup_wb():
             rows = wb_rows[:].rearrange("p t (h kv d) -> p kv h d t", h=2, kv=2, d=128)
             for kv in range(2):
-                copy_on_gpsimd(
-                    wb_grouped[:, 256 * kv : 256 * kv + 256, :].rearrange("p (h d) t -> p h d t", h=2), rows[:, kv]
+                nc.vector.tensor_copy(
+                    out=wb_grouped[:, 256 * kv : 256 * kv + 256, :].rearrange("p (h d) t -> p h d t", h=2), in_=rows[:, kv]
                 )
 
         def quantise_wb():
@@ -198,7 +198,6 @@ def tile_multiheadlatentattention_pa_t_kernel(tc, x, Wkv_a, kv_norm_w, Wkv_b, ou
         x_words = {}
         x_plane = {}
         latent = {}
-        square_sum = {}
         inv_rms = {}
         n_rows = {}
         n_transposed = {}
@@ -207,6 +206,7 @@ def tile_multiheadlatentattention_pa_t_kernel(tc, x, Wkv_a, kv_norm_w, Wkv_b, ou
         n_plane = {}
         kv_rows = {}
         rope_raw = {}
+        rope_parts = {}
 
         def transpose_x(pair):
             words = x_rows[pair // 2][:].bitcast(F32)
@@ -236,9 +236,7 @@ def tile_multiheadlatentattention_pa_t_kernel(tc, x, Wkv_a, kv_norm_w, Wkv_b, ou
             return x_words[pair][:, columns].bitcast(FP8X4), x_plane[pair][:, columns]
 
         def stage1(pair, i):
-            if i == 0:
-                sums = stat_pool.tile([P, 2], F32, name="square_sum")
-                square_sum[pair] = sums
+            square_sum = stat_pool.tile([P, 1], F32, name="square_sum")
             bank = psum_latent.tile([P, LATENT], F32, name="latent")
             latent[(pair, i)] = bank
             for g in range(2):
@@ -253,33 +251,32 @@ def tile_multiheadlatentattention_pa_t_kernel(tc, x, Wkv_a, kv_norm_w, Wkv_b, ou
                     stop=(g == 1),
                 )
             squares = squares_pool.tile([P, LATENT], BF16, name="squares")
-            nc.scalar.activation(out=squares[:], in_=bank[:], func=ACT.Square, accum_out=square_sum[pair][:, i : i + 1])
-            if i == 1:
-                mean_square = stat_pool.tile([P, 2], F32, name="mean_square")
-                nc.gpsimd.tensor_scalar(
-                    out=mean_square[:],
-                    in0=square_sum[pair][:],
-                    scalar1=1.0 / LATENT,
-                    scalar2=RMS_EPS,
-                    op0=ALU.mult,
-                    op1=ALU.add,
-                )
-                inverse = stat_pool.tile([P, 2], F32, name="inv_rms")
-                inv_rms[pair] = inverse
-                nc.gpsimd.tensor_tensor(out=inverse[:], in0=mean_square[:], in1=minus_half[:], op=ALU.pow)
+            nc.scalar.activation(out=squares[:], in_=bank[:], func=ACT.Square, accum_out=square_sum[:])
+            mean_square = stat_pool.tile([P, 1], F32, name="mean_square")
+            nc.gpsimd.tensor_scalar(
+                out=mean_square[:],
+                in0=square_sum[:],
+                scalar1=1.0 / LATENT,
+                scalar2=RMS_EPS,
+                op0=ALU.mult,
+                op1=ALU.add,
+            )
+            inverse = stat_pool.tile([P, 1], F32, name="inv_rms")
+            inv_rms[(pair, i)] = inverse
+            nc.gpsimd.tensor_tensor(out=inverse[:], in0=mean_square[:], in1=minus_half[:], op=ALU.pow)
 
-        def norm(pair):
-            rows = n_pool.tile([P, 2, LATENT], BF16, name="n_rows")
-            n_rows[pair] = rows
-            for i in range(2):
-                nc.vector.scalar_tensor_tensor(
-                    out=rows[:, i, :],
-                    in0=latent[(pair, i)][:],
-                    scalar=inv_rms[pair][:, i : i + 1],
-                    in1=gain[:],
-                    op0=ALU.mult,
-                    op1=ALU.mult,
-                )
+        def norm(pair, i):
+            if i == 0:
+                rows = n_pool.tile([P, 2, LATENT], BF16, name="n_rows")
+                n_rows[pair] = rows
+            nc.vector.scalar_tensor_tensor(
+                out=n_rows[pair][:, i, :],
+                in0=latent[(pair, i)][:],
+                scalar=inv_rms[(pair, i)][:],
+                in1=gain[:],
+                op0=ALU.mult,
+                op1=ALU.mult,
+            )
 
         def transpose_n(pair):
             bank = psum_nt.tile([P, 2, 2, P], F32, name="n_transposed")
@@ -333,14 +330,14 @@ def tile_multiheadlatentattention_pa_t_kernel(tc, x, Wkv_a, kv_norm_w, Wkv_b, ou
                 nc.sync.dma_start(out=k_nope_view[c][:, j : j + 2, :], in_=rows[:, 0, :, :])
                 nc.sync.dma_start(out=v_view[c][:, j : j + 2, :], in_=rows[:, 1, :, :])
 
-        def rope_product(c):
-            bank = psum_rope.tile([P, 4, ROPE], F32, name="rope_raw")
-            rope_raw[c] = bank
-            for j in range(4):
+        def rope_product(pair):
+            bank = psum_rope.tile([P, 2, ROPE], F32, name="rope_raw")
+            rope_raw[pair] = bank
+            for i in range(2):
                 for g in range(2):
-                    words, plane = x_operand(2 * c + j // 2, j % 2, g)
+                    words, plane = x_operand(pair, i, g)
                     nc.tensor.matmul_mx(
-                        out=bank[:, j, :],
+                        out=bank[:, i, :],
                         lhsT=words,
                         lhsT_scale=plane,
                         rhs=wa_rope_words[:, g, :].bitcast(FP8X4),
@@ -349,63 +346,81 @@ def tile_multiheadlatentattention_pa_t_kernel(tc, x, Wkv_a, kv_norm_w, Wkv_b, ou
                         stop=(g == 1),
                     )
 
-        def rope_rotation(c):
-            first = 4 * HALF_ROPE * (c % 4)
-            count = 4 * HALF_ROPE
-            raw = rope_raw[c][:].rearrange("p j (i two) -> p (j i) two", two=2)
+        def rope_rotation(pair):
+            count = 2 * HALF_ROPE
+            first = count * (pair % 8)
+            raw = rope_raw[pair][:].rearrange("p i (f two) -> p (i f) two", two=2)
             cos = cos_table[:, first : first + count]
             sin = sin_table[:, first : first + count]
             with_cos = rope_pool.tile([P, count, 2], F32, name="with_cos")
             with_sin = rope_pool.tile([P, 2, count], F32, name="with_sin")
-            rotated = rope_pool.tile([P, count, 2], F32, name="rotated")
+            rope_parts[pair] = (with_cos, with_sin)
             nc.vector.tensor_tensor(out=with_cos[:], in0=raw, in1=cos.unsqueeze(2).to_broadcast([P, count, 2]), op=ALU.mult)
             nc.vector.scalar_tensor_tensor(
                 out=with_sin[:, 0, :], in0=raw[:, :, 1], scalar=-1.0, in1=sin, op0=ALU.mult, op1=ALU.mult
             )
             nc.vector.tensor_tensor(out=with_sin[:, 1, :], in0=raw[:, :, 0], in1=sin, op=ALU.mult)
-            adder = nc.vector if c == CHUNKS - 1 else nc.gpsimd
-            adder.tensor_tensor(out=rotated[:], in0=with_cos[:], in1=with_sin[:].rearrange("p two n -> p n two"), op=ALU.add)
-            nc.sync.dma_start(out=k_rope_view[c], in_=rotated[:].rearrange("p n two -> p (n two)"))
+
+        def rope_sum(pair):
+            count = 2 * HALF_ROPE
+            with_cos, with_sin = rope_parts[pair]
+            rotated = rope_pool.tile([P, count, 2], F32, name="rotated")
+            nc.vector.tensor_tensor(
+                out=rotated[:], in0=with_cos[:], in1=with_sin[:].rearrange("p two n -> p n two"), op=ALU.add
+            )
+            first = 2 * ROPE * (pair % 2)
+            nc.sync.dma_start(
+                out=k_rope_view[pair // 2][:, first : first + 2 * ROPE], in_=rotated[:].rearrange("p n two -> p (n two)")
+            )
 
         def live(pair):
             return 0 <= pair < PAIRS
 
         transpose_x(0)
-        regroup_wa_latent(0, 0, LATENT, True)
-        regroup_wa_latent(1, WA_SPLIT, LATENT, False)
-        quantise_wa_latent(0)
-        regroup_wa_latent(1, 0, WA_SPLIT, True)
+        regroup_wa_latent(0, WA_SPLIT[0], LATENT, False)
+        regroup_wa_latent(0, 0, WA_SPLIT[0], True)
         quantise_x(0)
+        quantise_wa_latent(0)
+        regroup_wa_latent(1, WA_SPLIT[1], LATENT, False)
+        regroup_wa_latent(1, 0, WA_SPLIT[1], True)
+        transpose_x(1)
+        table_fraction()
         quantise_wa_latent(1)
-        table_arguments()
-        for r in range(PAIRS + 4):
-            if live(r + 1):
+        quantise_x(1)
+        for r in range(PAIRS + 3):
+            if r > 0 and live(r + 1):
                 transpose_x(r + 1)
             if live(r - 2):
                 transpose_n(r - 2)
+            if r == 0:
+                table_fold()
+                regroup_wa_rope()
+                quantise_wa_rope()
+            if live(r - 3):
+                stage2(r - 3, 0)
             if live(r - 1):
-                norm(r - 1)
+                norm(r - 1, 0)
+            if live(r):
+                stage1(r, 0)
             if live(r - 2):
                 group_n(r - 2)
-            for i in range(2):
-                if live(r - 3):
-                    stage2(r - 3, i)
-                if live(r):
-                    stage1(r, i)
-            if live(r + 1):
-                quantise_x(r + 1)
-            if r == 1:
-                quantise_wa_rope()
-            if live(r - 2):
-                quantise_n(r - 2)
+            if live(r - 1):
+                norm(r - 1, 1)
+            if live(r):
+                stage1(r, 1)
             if r == 2:
                 quantise_wb()
-            if r >= 3 and r % 2 == 1 and (r - 3) // 2 < CHUNKS:
-                rope_rotation((r - 3) // 2)
-            if r >= 2 and r % 2 == 0 and (r - 2) // 2 < CHUNKS:
-                rope_product((r - 2) // 2)
+            if live(r - 2):
+                quantise_n(r - 2)
+                rope_product(r - 2)
+                rope_rotation(r - 2)
+            if live(r - 3):
+                stage2(r - 3, 1)
+            if r > 0 and live(r + 1):
+                quantise_x(r + 1)
+            if live(r - 2):
+                rope_sum(r - 2)
             if r == 0:
-                regroup_wa_rope()
                 table_sin()
             if r == 1:
                 regroup_wb()

@@ -29,6 +29,8 @@ HALF_ROPE = ROPE // 2
 
 WA_SPLIT = (384, 256)
 
+TAIL_PAIRS = 3
+
 FLOPS = 2 * TOKENS * D_MODEL * (LATENT + ROPE) + 2 * TOKENS * LATENT * KV_OUT
 
 
@@ -290,10 +292,12 @@ def tile_multiheadlatentattention_pa_t_kernel(tc, x, Wkv_a, kv_norm_w, Wkv_b, ou
         def group_n(pair):
             grouped = n_grouped_pool.tile([P, 8 * P], BF16, name="n_grouped", align_bytes=64)
             n_grouped[pair] = grouped
-            nc.vector.tensor_copy(
-                out=grouped[:].bitcast(F32).rearrange("p (i m u) -> p i m u", i=2, m=P, u=2),
-                in_=n_transposed[pair][:].rearrange("p i u m -> p i m u"),
-            )
+            grouped_words = grouped[:].bitcast(F32).rearrange("p (i m u) -> p i m u", i=2, m=P, u=2)
+            words = n_transposed[pair][:].rearrange("p i u m -> p i m u")
+            if pair == PAIRS - 2:
+                nc.scalar.copy(out=grouped_words, in_=words)
+            else:
+                nc.vector.tensor_copy(out=grouped_words, in_=words)
 
         def quantise_n(pair):
             words = n_words_pool.tile([P, 2 * P], U32, name="n_words", align_bytes=64)
@@ -310,7 +314,10 @@ def tile_multiheadlatentattention_pa_t_kernel(tc, x, Wkv_a, kv_norm_w, Wkv_b, ou
                 rows = kv_pool.tile([P, 2, 2, 256], F32, name="kv_rows")
                 kv_rows[pair] = rows
             rows = kv_rows[pair]
-            bank = psum_kv.tile([P, KV_OUT], F32, name="kv")
+            if pair >= PAIRS - TAIL_PAIRS and i == 1:
+                bank = psum_xt.tile([P, KV_OUT], F32, name="xt")
+            else:
+                bank = psum_kv.tile([P, KV_OUT], F32, name="kv")
             columns = slice(P * i, P * i + P)
             nc.tensor.matmul_mx(
                 out=bank[:],
@@ -321,7 +328,8 @@ def tile_multiheadlatentattention_pa_t_kernel(tc, x, Wkv_a, kv_norm_w, Wkv_b, ou
                 start=True,
                 stop=True,
             )
-            nc.scalar.copy(out=rows[:, :, i, :], in_=bank[:].rearrange("p (kv n) -> p kv n", kv=2))
+            empty = nc.vector.tensor_copy if pair == PAIRS - 1 and i == 1 else nc.scalar.copy
+            empty(out=rows[:, :, i, :], in_=bank[:].rearrange("p (kv n) -> p kv n", kv=2))
             j = 2 * (pair % 2)
             if pair == PAIRS - 1:
                 nc.sync.dma_start(out=k_nope_view[c][:, j + i, :], in_=rows[:, 0, i, :])

@@ -373,7 +373,7 @@ def tile_multiheadlatentattention_pa_t_kernel(tc, x, Wkv_a, kv_norm_w, Wkv_b, ou
             count = 2 * HALF_ROPE
             with_cos, with_sin = rope_parts[pair]
             rotated = rope_pool.tile([P, count, 2], F32, name="rotated")
-            nc.vector.tensor_tensor(
+            nc.gpsimd.tensor_tensor(
                 out=rotated[:], in0=with_cos[:], in1=with_sin[:].rearrange("p two n -> p n two"), op=ALU.add
             )
             first = 2 * ROPE * (pair % 2)

@@ -29,7 +29,6 @@ HALF_ROPE = ROPE // 2
 
 WA_SPLIT = (384, 256)
 
-TAIL_PAIRS = 3
 
 FLOPS = 2 * TOKENS * D_MODEL * (LATENT + ROPE) + 2 * TOKENS * LATENT * KV_OUT
 
@@ -54,11 +53,8 @@ def tile_multiheadlatentattention_pa_t_kernel(tc, x, Wkv_a, kv_norm_w, Wkv_b, ou
         n_words_pool = ctx.enter_context(tc.tile_pool(name="n_words_pool", bufs=3))
         kv_pool = ctx.enter_context(tc.tile_pool(name="kv_pool", bufs=4))
         rope_pool = ctx.enter_context(tc.tile_pool(name="rope_pool", bufs=2))
-        psum_xt = ctx.enter_context(tc.psum_pool(name="psum_xt", bufs=2))
+        psum_turn = ctx.enter_context(tc.psum_pool(name="psum_turn", bufs=5))
         psum_latent = ctx.enter_context(tc.psum_pool(name="psum_latent", bufs=3))
-        psum_nt = ctx.enter_context(tc.psum_pool(name="psum_nt", bufs=1))
-        psum_kv = ctx.enter_context(tc.psum_pool(name="psum_kv", bufs=1))
-        psum_rope = ctx.enter_context(tc.psum_pool(name="psum_rope", bufs=1))
         ctx.enter_context(tc.manual_schedule())
 
         x_rows = []
@@ -197,6 +193,8 @@ def tile_multiheadlatentattention_pa_t_kernel(tc, x, Wkv_a, kv_norm_w, Wkv_b, ou
             )
 
         x_grouped = {}
+        x_transposed = {}
+        kv_bank = {}
         x_words = {}
         x_plane = {}
         latent = {}
@@ -211,20 +209,28 @@ def tile_multiheadlatentattention_pa_t_kernel(tc, x, Wkv_a, kv_norm_w, Wkv_b, ou
         rope_parts = {}
 
         def transpose_x(pair):
+            transpose_x_tensor(pair)
+            empty_xt(pair, 0)
+            empty_xt(pair, 1)
+
+        def transpose_x_tensor(pair):
             words = x_rows[pair // 2][:].bitcast(F32)
             grouped = x_grouped_pool.tile([P, 2 * D_MODEL], BF16, name="x_grouped", align_bytes=64)
             x_grouped[pair] = grouped
-            grouped_words = grouped[:].bitcast(F32)
             for i in range(2):
                 j = 2 * (pair % 2) + i
-                xt = psum_xt.tile([P, 4, P], F32, name="xt")
+                xt = psum_turn.tile([P, 4, P], F32, name="turn")
+                x_transposed[(pair, i)] = xt
                 for block in range(4):
                     first = 512 * j + P * block
                     nc.tensor.transpose(xt[:, block, :], words[:, first : first + P], identity_f32[:])
-                nc.scalar.copy(
-                    out=grouped_words[:, 512 * i : 512 * i + 512].rearrange("q (g m u) -> q g m u", g=2, m=P, u=2),
-                    in_=xt[:].rearrange("q (g u) m -> q g m u", g=2, u=2),
-                )
+
+        def empty_xt(pair, i):
+            words = x_grouped[pair][:].bitcast(F32)[:, 512 * i : 512 * i + 512]
+            nc.scalar.copy(
+                out=words.rearrange("q (g m u) -> q g m u", g=2, m=P, u=2),
+                in_=x_transposed[(pair, i)][:].rearrange("q (g u) m -> q g m u", g=2, u=2),
+            )
 
         def quantise_x(pair):
             words = keep.tile([P, 4 * P], U32, name="x_words%d" % pair, align_bytes=64)
@@ -238,7 +244,6 @@ def tile_multiheadlatentattention_pa_t_kernel(tc, x, Wkv_a, kv_norm_w, Wkv_b, ou
             return x_words[pair][:, columns].bitcast(FP8X4), x_plane[pair][:, columns]
 
         def stage1(pair, i):
-            square_sum = stat_pool.tile([P, 1], F32, name="square_sum")
             bank = psum_latent.tile([P, LATENT], F32, name="latent")
             latent[(pair, i)] = bank
             for g in range(2):
@@ -252,6 +257,10 @@ def tile_multiheadlatentattention_pa_t_kernel(tc, x, Wkv_a, kv_norm_w, Wkv_b, ou
                     start=(g == 0),
                     stop=(g == 1),
                 )
+
+        def rms(pair, i):
+            bank = latent[(pair, i)]
+            square_sum = stat_pool.tile([P, 1], F32, name="square_sum")
             squares = squares_pool.tile([P, LATENT], BF16, name="squares")
             nc.scalar.activation(out=squares[:], in_=bank[:], func=ACT.Square, accum_out=square_sum[:])
             mean_square = stat_pool.tile([P, 1], F32, name="mean_square")
@@ -281,7 +290,7 @@ def tile_multiheadlatentattention_pa_t_kernel(tc, x, Wkv_a, kv_norm_w, Wkv_b, ou
             )
 
         def transpose_n(pair):
-            bank = psum_nt.tile([P, 2, 2, P], F32, name="n_transposed")
+            bank = psum_turn.tile([P, 2, 2, P], F32, name="turn")
             n_transposed[pair] = bank
             words = n_rows[pair][:].rearrange("p i n -> p (i n)").bitcast(F32)
             for i in range(2):
@@ -309,15 +318,10 @@ def tile_multiheadlatentattention_pa_t_kernel(tc, x, Wkv_a, kv_norm_w, Wkv_b, ou
             )
 
         def stage2(pair, i):
-            c = pair // 2
             if i == 0:
                 rows = kv_pool.tile([P, 2, 2, 256], F32, name="kv_rows")
                 kv_rows[pair] = rows
-            rows = kv_rows[pair]
-            if pair >= PAIRS - TAIL_PAIRS and i == 1:
-                bank = psum_xt.tile([P, KV_OUT], F32, name="xt")
-            else:
-                bank = psum_kv.tile([P, KV_OUT], F32, name="kv")
+            bank = psum_turn.tile([P, KV_OUT], F32, name="turn")
             columns = slice(P * i, P * i + P)
             nc.tensor.matmul_mx(
                 out=bank[:],
@@ -328,6 +332,12 @@ def tile_multiheadlatentattention_pa_t_kernel(tc, x, Wkv_a, kv_norm_w, Wkv_b, ou
                 start=True,
                 stop=True,
             )
+            kv_bank[(pair, i)] = bank
+
+        def store_kv(pair, i):
+            c = pair // 2
+            rows = kv_rows[pair]
+            bank = kv_bank[(pair, i)]
             empty = nc.vector.tensor_copy if pair == PAIRS - 1 and i == 1 else nc.scalar.copy
             empty(out=rows[:, :, i, :], in_=bank[:].rearrange("p (kv n) -> p kv n", kv=2))
             j = 2 * (pair % 2)
@@ -339,7 +349,7 @@ def tile_multiheadlatentattention_pa_t_kernel(tc, x, Wkv_a, kv_norm_w, Wkv_b, ou
                 nc.sync.dma_start(out=v_view[c][:, j : j + 2, :], in_=rows[:, 1, :, :])
 
         def rope_product(pair):
-            bank = psum_rope.tile([P, 2, ROPE], F32, name="rope_raw")
+            bank = psum_turn.tile([P, 2, ROPE], F32, name="turn")
             rope_raw[pair] = bank
             for i in range(2):
                 for g in range(2):
@@ -397,35 +407,43 @@ def tile_multiheadlatentattention_pa_t_kernel(tc, x, Wkv_a, kv_norm_w, Wkv_b, ou
         quantise_x(1)
         for r in range(PAIRS + 3):
             if r > 0 and live(r + 1):
-                transpose_x(r + 1)
+                transpose_x_tensor(r + 1)
+                empty_xt(r + 1, 0)
             if live(r - 2):
                 transpose_n(r - 2)
+            if r > 0 and live(r + 1):
+                empty_xt(r + 1, 1)
             if r == 0:
                 table_fold()
                 regroup_wa_rope()
                 quantise_wa_rope()
-            if live(r - 3):
-                stage2(r - 3, 0)
             if live(r - 1):
                 norm(r - 1, 0)
             if live(r):
                 stage1(r, 0)
+                rms(r, 0)
+            if live(r - 3):
+                stage2(r - 3, 0)
+                stage2(r - 3, 1)
             if live(r - 2):
                 group_n(r - 2)
-            if live(r - 1):
-                norm(r - 1, 1)
-            if live(r):
-                stage1(r, 1)
             if r == 2:
                 quantise_wb()
+            if live(r - 3):
+                store_kv(r - 3, 0)
+            if r > 0 and live(r + 1):
+                quantise_x(r + 1)
+            if live(r):
+                stage1(r, 1)
+                rms(r, 1)
+            if live(r - 1):
+                norm(r - 1, 1)
             if live(r - 2):
                 quantise_n(r - 2)
                 rope_product(r - 2)
                 rope_rotation(r - 2)
             if live(r - 3):
-                stage2(r - 3, 1)
-            if r > 0 and live(r + 1):
-                quantise_x(r + 1)
+                store_kv(r - 3, 1)
             if live(r - 2):
                 rope_sum(r - 2)
             if r == 0:

@@ -180,12 +180,11 @@ def tile_multiheadlatentattention_pa_t_kernel(tc, x, Wkv_a, kv_norm_w, Wkv_b, ou
                     in_=wa_rope_grouped[:, g, :, :].rearrange("q n t -> q (n t)"),
                 )
 
-        def regroup_wb():
+        def regroup_wb(kv):
             rows = wb_rows[:].rearrange("p t (h kv d) -> p kv h d t", h=2, kv=2, d=128)
-            for kv in range(2):
-                nc.vector.tensor_copy(
-                    out=wb_grouped[:, 256 * kv : 256 * kv + 256, :].rearrange("p (h d) t -> p h d t", h=2), in_=rows[:, kv]
-                )
+            nc.vector.tensor_copy(
+                out=wb_grouped[:, 256 * kv : 256 * kv + 256, :].rearrange("p (h d) t -> p h d t", h=2), in_=rows[:, kv]
+            )
 
         def quantise_wb():
             nc.vector.quantize_mx(
@@ -402,8 +401,8 @@ def tile_multiheadlatentattention_pa_t_kernel(tc, x, Wkv_a, kv_norm_w, Wkv_b, ou
         regroup_wa_latent(1, WA_SPLIT[1], LATENT, False)
         regroup_wa_latent(1, 0, WA_SPLIT[1], True)
         transpose_x(1)
-        table_fraction()
         quantise_wa_latent(1)
+        table_fraction()
         quantise_x(1)
         for r in range(PAIRS + 3):
             if r > 0 and live(r + 1):
@@ -422,6 +421,8 @@ def tile_multiheadlatentattention_pa_t_kernel(tc, x, Wkv_a, kv_norm_w, Wkv_b, ou
             if live(r):
                 stage1(r, 0)
                 rms(r, 0)
+            if r == 1:
+                table_sin()
             if live(r - 3):
                 stage2(r - 3, 0)
                 stage2(r - 3, 1)
@@ -438,6 +439,10 @@ def tile_multiheadlatentattention_pa_t_kernel(tc, x, Wkv_a, kv_norm_w, Wkv_b, ou
                 rms(r, 1)
             if live(r - 1):
                 norm(r - 1, 1)
+            if r == 1:
+                table_cos()
+                regroup_wb(0)
+                regroup_wb(1)
             if live(r - 2):
                 quantise_n(r - 2)
                 rope_product(r - 2)
@@ -446,8 +451,3 @@ def tile_multiheadlatentattention_pa_t_kernel(tc, x, Wkv_a, kv_norm_w, Wkv_b, ou
                 store_kv(r - 3, 1)
             if live(r - 2):
                 rope_sum(r - 2)
-            if r == 0:
-                table_sin()
-            if r == 1:
-                regroup_wb()
-                table_cos()

@@ -64,6 +64,12 @@ def tile_multiheadlatentattention_pa_t_kernel(tc, x, Wkv_a, kv_norm_w, Wkv_b, ou
         wb_rows = keep.tile([P, 4, KV_OUT], BF16, name="wb_rows")
         gain = keep.tile([P, LATENT], BF16, name="gain")
 
+        gain_row = keep.tile([P, LATENT], BF16, name="gain_row")
+        nc.vector.memset(gain_row[:], 0.0)
+        nc.scalar.dma_start(out=gain_row[0:1, :], in_=kv_norm_w.rearrange("(o n) -> o n", o=1))
+        ones = keep.tile([P, P], BF16, name="ones")
+        nc.vector.memset(ones[:], 1.0)
+
         def load_wa(g):
             nc.sync.dma_start(
                 out=wa_rows[:, 4 * g : 4 * g + 4, :].rearrange("q (a e) n -> q a (e n)", a=2, e=2),
@@ -75,7 +81,6 @@ def tile_multiheadlatentattention_pa_t_kernel(tc, x, Wkv_a, kv_norm_w, Wkv_b, ou
         load_wa(0)
         load_wa(1)
         nc.sync.dma_start(out=x_rows[0][:, half : 2 * half], in_=x_view[0][:, half : 2 * half])
-        nc.sync.dma_start(out=gain[:], in_=kv_norm_w.partition_broadcast(P))
         nc.sync.dma_start(out=x_rows[1][:], in_=x_view[1])
         nc.sync.dma_start(out=wb_rows[:].rearrange("p (u e) n -> p u (e n)", u=2, e=2), in_=wb_view)
         for c in range(2, CHUNKS):
@@ -190,6 +195,11 @@ def tile_multiheadlatentattention_pa_t_kernel(tc, x, Wkv_a, kv_norm_w, Wkv_b, ou
             nc.vector.quantize_mx(
                 out=wb_words[:].bitcast(FP8X4), scales=wb_plane[:], in_=wb_grouped[:].rearrange("p n t -> p (n t)")
             )
+
+        def spread_gain():
+            bank = psum_turn.tile([P, LATENT], F32, name="turn")
+            nc.tensor.matmul(out=bank[:], lhsT=ones[:], rhs=gain_row[:], start=True, stop=True)
+            nc.scalar.copy(out=gain[:], in_=bank[:])
 
         x_grouped = {}
         x_transposed = {}
@@ -400,6 +410,7 @@ def tile_multiheadlatentattention_pa_t_kernel(tc, x, Wkv_a, kv_norm_w, Wkv_b, ou
         quantise_wa_latent(0)
         regroup_wa_latent(1, WA_SPLIT[1], LATENT, False)
         regroup_wa_latent(1, 0, WA_SPLIT[1], True)
+        spread_gain()
         transpose_x(1)
         quantise_wa_latent(1)
         table_fraction()

@@ -30,6 +30,8 @@ HALF_ROPE = ROPE // 2
 WA_SPLIT = (384, 256)
 
 
+WARM_UP = 4
+
 FLOPS = 2 * TOKENS * D_MODEL * (LATENT + ROPE) + 2 * TOKENS * LATENT * KV_OUT
 
 
@@ -65,9 +67,9 @@ def tile_multiheadlatentattention_pa_t_kernel(tc, x, Wkv_a, kv_norm_w, Wkv_b, ou
         gain = keep.tile([P, LATENT], BF16, name="gain")
 
         gain_row = keep.tile([P, LATENT], BF16, name="gain_row")
-        nc.vector.memset(gain_row[:], 0.0)
+        nc.vector.memset(gain_row[:].bitcast(I32), 0)
         nc.scalar.dma_start(out=gain_row[0:1, :], in_=kv_norm_w.rearrange("(o n) -> o n", o=1))
-        ones = keep.tile([P, P], BF16, name="ones")
+        ones = keep.tile([P, LATENT], BF16, name="ones")
         nc.vector.memset(ones[:], 1.0)
 
         def load_wa(g):
@@ -198,8 +200,13 @@ def tile_multiheadlatentattention_pa_t_kernel(tc, x, Wkv_a, kv_norm_w, Wkv_b, ou
 
         def spread_gain():
             bank = psum_turn.tile([P, LATENT], F32, name="turn")
-            nc.tensor.matmul(out=bank[:], lhsT=ones[:], rhs=gain_row[:], start=True, stop=True)
+            nc.tensor.matmul(out=bank[:], lhsT=ones[:, 0:P], rhs=gain_row[:], start=True, stop=True)
             nc.scalar.copy(out=gain[:], in_=bank[:])
+
+        def warm_up():
+            bank = psum_turn.tile([P, LATENT], F32, name="turn")
+            for k in range(WARM_UP):
+                nc.tensor.matmul(out=bank[:], lhsT=ones[:, 0:P], rhs=ones[:], start=True, stop=True)
 
         x_grouped = {}
         x_transposed = {}
@@ -253,7 +260,10 @@ def tile_multiheadlatentattention_pa_t_kernel(tc, x, Wkv_a, kv_norm_w, Wkv_b, ou
             return x_words[pair][:, columns].bitcast(FP8X4), x_plane[pair][:, columns]
 
         def stage1(pair, i):
-            bank = psum_latent.tile([P, LATENT], F32, name="latent")
+            if pair in (0, PAIRS - 1):
+                bank = psum_turn.tile([P, LATENT], F32, name="turn")
+            else:
+                bank = psum_latent.tile([P, LATENT], F32, name="latent")
             latent[(pair, i)] = bank
             for g in range(2):
                 words, plane = x_operand(pair, i, g)
@@ -392,7 +402,8 @@ def tile_multiheadlatentattention_pa_t_kernel(tc, x, Wkv_a, kv_norm_w, Wkv_b, ou
             count = 2 * HALF_ROPE
             with_cos, with_sin = rope_parts[pair]
             rotated = rope_pool.tile([P, count, 2], F32, name="rotated")
-            nc.gpsimd.tensor_tensor(
+            adder = nc.vector if pair >= PAIRS - 2 else nc.gpsimd
+            adder.tensor_tensor(
                 out=rotated[:], in0=with_cos[:], in1=with_sin[:].rearrange("p two n -> p n two"), op=ALU.add
             )
             first = 2 * ROPE * (pair % 2)
@@ -404,14 +415,15 @@ def tile_multiheadlatentattention_pa_t_kernel(tc, x, Wkv_a, kv_norm_w, Wkv_b, ou
             return 0 <= pair < PAIRS
 
         transpose_x(0)
+        warm_up()
         regroup_wa_latent(0, WA_SPLIT[0], LATENT, False)
         regroup_wa_latent(0, 0, WA_SPLIT[0], True)
         quantise_x(0)
         quantise_wa_latent(0)
         regroup_wa_latent(1, WA_SPLIT[1], LATENT, False)
         regroup_wa_latent(1, 0, WA_SPLIT[1], True)
-        spread_gain()
         transpose_x(1)
+        spread_gain()
         quantise_wa_latent(1)
         table_fraction()
         quantise_x(1)
@@ -419,6 +431,10 @@ def tile_multiheadlatentattention_pa_t_kernel(tc, x, Wkv_a, kv_norm_w, Wkv_b, ou
             if r > 0 and live(r + 1):
                 transpose_x_tensor(r + 1)
                 empty_xt(r + 1, 0)
+            if r == PAIRS - 1:
+                for i in range(2):
+                    stage1(r, i)
+                    rms(r, i)
             if live(r - 2):
                 transpose_n(r - 2)
             if r > 0 and live(r + 1):
@@ -429,7 +445,7 @@ def tile_multiheadlatentattention_pa_t_kernel(tc, x, Wkv_a, kv_norm_w, Wkv_b, ou
                 quantise_wa_rope()
             if live(r - 1):
                 norm(r - 1, 0)
-            if live(r):
+            if r < PAIRS - 1:
                 stage1(r, 0)
                 rms(r, 0)
             if r == 1:
@@ -445,7 +461,7 @@ def tile_multiheadlatentattention_pa_t_kernel(tc, x, Wkv_a, kv_norm_w, Wkv_b, ou
                 store_kv(r - 3, 0)
             if r > 0 and live(r + 1):
                 quantise_x(r + 1)
-            if live(r):
+            if r < PAIRS - 1:
                 stage1(r, 1)
                 rms(r, 1)
             if live(r - 1):

@@ -158,8 +158,8 @@ def tile_multiheadlatentattention_pa_t_kernel(tc, x, Wkv_a, kv_norm_w, Wkv_b, ou
         wb_plane = keep.tile([P, KV_OUT], U8, name="wb_plane", align_bytes=64)
 
         def regroup_wa_latent(g, first, last, on_vector):
-            grouped = wa_latent_grouped[:, g, first:last, :]
-            rows = wa_rows[:, 4 * g : 4 * g + 4, first:last].rearrange("q t n -> q n t")
+            grouped = wa_latent_grouped[:, g, first:last, :].rearrange("q (c i) t -> q c t i", i=4)
+            rows = wa_rows[:, 4 * g : 4 * g + 4, first:last].rearrange("q t (c i) -> q c t i", i=4)
             if on_vector:
                 nc.vector.tensor_copy(out=grouped, in_=rows)
             else:
@@ -175,8 +175,8 @@ def tile_multiheadlatentattention_pa_t_kernel(tc, x, Wkv_a, kv_norm_w, Wkv_b, ou
         def regroup_wa_rope():
             for g in range(2):
                 nc.vector.tensor_copy(
-                    out=wa_rope_grouped[:, g, :, :],
-                    in_=wa_rows[:, 4 * g : 4 * g + 4, LATENT : LATENT + ROPE].rearrange("q t n -> q n t"),
+                    out=wa_rope_grouped[:, g, :, :].rearrange("q (c i) t -> q c t i", i=4),
+                    in_=wa_rows[:, 4 * g : 4 * g + 4, LATENT : LATENT + ROPE].rearrange("q t (c i) -> q c t i", i=4),
                 )
 
         def quantise_wa_rope():
@@ -188,10 +188,13 @@ def tile_multiheadlatentattention_pa_t_kernel(tc, x, Wkv_a, kv_norm_w, Wkv_b, ou
                 )
 
         def regroup_wb(kv):
-            rows = wb_rows[:].rearrange("p t (h kv d) -> p kv h d t", h=2, kv=2, d=128)
-            nc.vector.tensor_copy(
-                out=wb_grouped[:, 256 * kv : 256 * kv + 256, :].rearrange("p (h d) t -> p h d t", h=2), in_=rows[:, kv]
-            )
+            for h in range(2):
+                first = 256 * kv + 128 * h
+                rows = wb_rows[:, :, 256 * h + 128 * kv : 256 * h + 128 * kv + 128]
+                nc.vector.tensor_copy(
+                    out=wb_grouped[:, first : first + 128, :].rearrange("p (c i) t -> p c t i", i=4),
+                    in_=rows.rearrange("p t (c i) -> p c t i", i=4),
+                )
 
         def quantise_wb():
             nc.vector.quantize_mx(

@@ -26,11 +26,15 @@ CHUNKS = 8
 PAIRS = 16
 SEQ_TILES = 16
 HALF_ROPE = ROPE // 2
+SEEDS = 8
+HALF_TABLE = SEQ_TILES * HALF_ROPE // 2
 
 WA_SPLIT = (384, 256)
 
 
 WARM_UP = 4
+
+KV_SPLIT = 192
 
 FLOPS = 2 * TOKENS * D_MODEL * (LATENT + ROPE) + 2 * TOKENS * LATENT * KV_OUT
 
@@ -67,10 +71,8 @@ def tile_multiheadlatentattention_pa_t_kernel(tc, x, Wkv_a, kv_norm_w, Wkv_b, ou
         gain = keep.tile([P, LATENT], BF16, name="gain")
 
         gain_row = keep.tile([P, LATENT], BF16, name="gain_row")
-        nc.vector.memset(gain_row[:].bitcast(I32), 0)
+        nc.gpsimd.memset(gain_row[:].bitcast(I32), 0)
         nc.scalar.dma_start(out=gain_row[0:1, :], in_=kv_norm_w.rearrange("(o n) -> o n", o=1))
-        ones = keep.tile([P, LATENT], BF16, name="ones")
-        nc.vector.memset(ones[:], 1.0)
 
         def load_wa(g):
             nc.sync.dma_start(
@@ -78,11 +80,11 @@ def tile_multiheadlatentattention_pa_t_kernel(tc, x, Wkv_a, kv_norm_w, Wkv_b, ou
                 in_=wa_view[:, 2 * g : 2 * g + 2, :],
             )
 
-        half = 2 * D_MODEL
-        nc.sync.dma_start(out=x_rows[0][:, 0:half], in_=x_view[0][:, 0:half])
+        middle = 2 * D_MODEL
+        nc.sync.dma_start(out=x_rows[0][:, 0:middle], in_=x_view[0][:, 0:middle])
         load_wa(0)
         load_wa(1)
-        nc.sync.dma_start(out=x_rows[0][:, half : 2 * half], in_=x_view[0][:, half : 2 * half])
+        nc.sync.dma_start(out=x_rows[0][:, middle : 2 * middle], in_=x_view[0][:, middle : 2 * middle])
         nc.sync.dma_start(out=x_rows[1][:], in_=x_view[1])
         nc.sync.dma_start(out=wb_rows[:].rearrange("p (u e) n -> p u (e n)", u=2, e=2), in_=wb_view)
         for c in range(2, CHUNKS):
@@ -92,51 +94,46 @@ def tile_multiheadlatentattention_pa_t_kernel(tc, x, Wkv_a, kv_norm_w, Wkv_b, ou
         nc.gpsimd.iota(position_int[:], pattern=[[512, 4], [1, 4]], base=0, channel_multiplier=4)
         identity_f32 = keep.tile([P, P], F32, name="identity_f32")
         make_identity(nc, identity_f32[:])
+        ones = keep.tile([P, LATENT], BF16, name="ones")
+        nc.gpsimd.memset(ones[:], 1.0)
         minus_half = keep.tile([P, 1], F32, name="minus_half")
         nc.vector.memset(minus_half[:], -0.5)
         table_warm = keep.tile([P, 1], F32, name="table_warm")
         nc.scalar.activation(out=table_warm[:], in_=minus_half[:], func=ACT.Sin)
 
-        position = keep.tile([P, SEQ_TILES], F32, name="position")
-        nc.vector.tensor_copy(out=position[:], in_=position_int[:])
-        frequency = keep.tile([P, HALF_ROPE], F32, name="frequency")
-        nc.vector.memset(frequency[:, 0:1], 1.0)
-        nc.vector.tensor_scalar(
-            out=frequency[:, 0:1], in0=frequency[:, 0:1], scalar1=1.0 / (2.0 * math.pi), scalar2=None, op0=ALU.mult
-        )
+        turns = keep.tile([P, SEQ_TILES, HALF_ROPE], F32, name="turns")
+        whole_turns = keep.tile([P, SEQ_TILES, HALF_ROPE], I32, name="whole_turns")
+        position_halves = (slice(0, SEQ_TILES // 2), slice(SEQ_TILES // 2, SEQ_TILES))
         ratio = ROPE_BASE ** (-1.0 / HALF_ROPE)
-        filled = 1
-        while filled < HALF_ROPE:
+        for i in range(SEEDS):
             nc.vector.tensor_scalar(
-                out=frequency[:, filled : 2 * filled],
-                in0=frequency[:, 0:filled],
-                scalar1=ratio**filled,
-                scalar2=None,
-                op0=ALU.mult,
+                out=turns[:, :, i], in0=position_int[:], scalar1=ratio**i / (2.0 * math.pi), scalar2=None, op0=ALU.mult
             )
+        filled = SEEDS
+        while filled < HALF_ROPE:
+            for half in position_halves:
+                nc.vector.tensor_scalar(
+                    out=turns[:, half, filled : 2 * filled],
+                    in0=turns[:, half, 0:filled],
+                    scalar1=ratio**filled,
+                    scalar2=None,
+                    op0=ALU.mult,
+                )
             filled *= 2
-        table_shape = [P, SEQ_TILES, HALF_ROPE]
-        turns = keep.tile(table_shape, F32, name="turns")
-        nc.vector.tensor_tensor(
-            out=turns[:],
-            in0=position[:].unsqueeze(2).to_broadcast(table_shape),
-            in1=frequency[:].unsqueeze(1).to_broadcast(table_shape),
-            op=ALU.mult,
-        )
-        whole_turns = keep.tile(table_shape, I32, name="whole_turns")
-        nc.vector.tensor_copy(out=whole_turns[:], in_=turns[:])
+        for half in position_halves:
+            nc.vector.tensor_copy(out=whole_turns[:, half, :], in_=turns[:, half, :])
+        for half in position_halves:
+            nc.vector.tensor_tensor(
+                out=turns[:, half, :], in0=turns[:, half, :], in1=whole_turns[:, half, :], op=ALU.subtract
+            )
         fraction = turns[:].rearrange("p a i -> p (a i)")
         sin_table = keep.tile([P, SEQ_TILES * HALF_ROPE], F32, name="sin_table")
         cos_table = keep.tile([P, SEQ_TILES * HALF_ROPE], F32, name="cos_table")
 
-        def table_fraction():
-            nc.vector.tensor_tensor(
-                out=fraction, in0=fraction, in1=whole_turns[:].rearrange("p a i -> p (a i)"), op=ALU.subtract
-            )
-
-        def table_fold():
+        def table_fold(half):
+            columns = slice(half * HALF_TABLE, half * HALF_TABLE + HALF_TABLE)
             nc.vector.scalar_tensor_tensor(
-                out=cos_table[:], in0=fraction, scalar=-1.0, in1=fraction, op0=ALU.mult, op1=ALU.min
+                out=cos_table[:, columns], in0=fraction[:, columns], scalar=-1.0, in1=fraction[:, columns], op0=ALU.mult, op1=ALU.min
             )
 
         def table_sin():
@@ -325,7 +322,7 @@ def tile_multiheadlatentattention_pa_t_kernel(tc, x, Wkv_a, kv_norm_w, Wkv_b, ou
             n_grouped[pair] = grouped
             grouped_words = grouped[:].bitcast(F32).rearrange("p (i m u) -> p i m u", i=2, m=P, u=2)
             words = n_transposed[pair][:].rearrange("p i u m -> p i m u")
-            if pair == PAIRS - 2:
+            if pair >= PAIRS - 2:
                 nc.scalar.copy(out=grouped_words, in_=words)
             else:
                 nc.vector.tensor_copy(out=grouped_words, in_=words)
@@ -356,12 +353,21 @@ def tile_multiheadlatentattention_pa_t_kernel(tc, x, Wkv_a, kv_norm_w, Wkv_b, ou
             )
             kv_bank[(pair, i)] = bank
 
+        def empty_kv_part(pair):
+            values = kv_bank[(pair, 1)][:].rearrange("p (kv n) -> p kv n", kv=2)
+            nc.vector.tensor_copy(out=kv_rows[pair][:, :, 1, KV_SPLIT:256], in_=values[:, :, KV_SPLIT:256])
+
         def store_kv(pair, i):
             c = pair // 2
             rows = kv_rows[pair]
             bank = kv_bank[(pair, i)]
-            empty = nc.vector.tensor_copy if pair == PAIRS - 1 and i == 1 else nc.scalar.copy
-            empty(out=rows[:, :, i, :], in_=bank[:].rearrange("p (kv n) -> p kv n", kv=2))
+            values = bank[:].rearrange("p (kv n) -> p kv n", kv=2)
+            if pair == PAIRS - 1 and i == 1:
+                nc.vector.tensor_copy(out=rows[:, :, i, :], in_=values)
+            elif i == 1:
+                nc.scalar.copy(out=rows[:, :, i, 0:KV_SPLIT], in_=values[:, :, 0:KV_SPLIT])
+            else:
+                nc.scalar.copy(out=rows[:, :, i, :], in_=values)
             j = 2 * (pair % 2)
             if pair == PAIRS - 1:
                 nc.sync.dma_start(out=k_nope_view[c][:, j + i, :], in_=rows[:, 0, i, :])
@@ -428,7 +434,7 @@ def tile_multiheadlatentattention_pa_t_kernel(tc, x, Wkv_a, kv_norm_w, Wkv_b, ou
         transpose_x(1)
         spread_gain()
         quantise_wa_latent(1)
-        table_fraction()
+        table_fold(0)
         quantise_x(1)
         for r in range(PAIRS + 3):
             if r > 0 and live(r + 1):
@@ -443,7 +449,7 @@ def tile_multiheadlatentattention_pa_t_kernel(tc, x, Wkv_a, kv_norm_w, Wkv_b, ou
             if r > 0 and live(r + 1):
                 empty_xt(r + 1, 1)
             if r == 0:
-                table_fold()
+                table_fold(1)
                 regroup_wa_rope()
                 quantise_wa_rope()
             if live(r - 1):
@@ -464,6 +470,8 @@ def tile_multiheadlatentattention_pa_t_kernel(tc, x, Wkv_a, kv_norm_w, Wkv_b, ou
                 store_kv(r - 3, 0)
             if r > 0 and live(r + 1):
                 quantise_x(r + 1)
+            if live(r - 3) and r < PAIRS + 2:
+                empty_kv_part(r - 3)
             if r < PAIRS - 1:
                 stage1(r, 1)
                 rms(r, 1)

import math
from contextlib import ExitStack

import concourse.mybir as mybir
from concourse.masks import make_identity

F32 = mybir.dt.float32
BF16 = mybir.dt.bfloat16
I32 = mybir.dt.int32
U32 = mybir.dt.uint32
U8 = mybir.dt.uint8
FP8X4 = mybir.dt.float8_e4m3fn_x4
ALU = mybir.AluOpType
ACT = mybir.ActivationFunctionType

P = 128
TOKENS = 4096
D_MODEL = 1024
LATENT = 512
ROPE = 128
KV_OUT = 512
RMS_EPS = 1.1920928955078125e-07
ROPE_BASE = 10000.0

CHUNKS = 8
PAIRS = 16
SEQ_TILES = 16
HALF_ROPE = ROPE // 2
SEEDS = 8
HALF_TABLE = SEQ_TILES * HALF_ROPE // 2

WA_SPLIT = (384, 256)


WARM_UP = 4

KV_SPLIT = 192

FLOPS = 2 * TOKENS * D_MODEL * (LATENT + ROPE) + 2 * TOKENS * LATENT * KV_OUT


def tile_multiheadlatentattention_pa_t_kernel(tc, x, Wkv_a, kv_norm_w, Wkv_b, out_0, out_1, out_2):
    nc = tc.nc

    x_view = x.rearrange("b s k -> (b s) k").rearrange("(c p j) k -> c p (j k)", p=P, j=4)
    k_nope_view = out_0.rearrange("b s h d -> (b s) (h d)").rearrange("(c p j) n -> c p j n", p=P, j=4)
    v_view = out_1.rearrange("b s h d -> (b s) (h d)").rearrange("(c p j) n -> c p j n", p=P, j=4)
    k_rope_view = out_2.rearrange("b s h d -> (b s) (h d)").rearrange("(c p j) n -> c p (j n)", p=P, j=4)
    wa_view = Wkv_a.rearrange("(a q e) n -> q a (e n)", a=4, q=P, e=2)
    wb_view = Wkv_b.rearrange("(u p e) n -> p u (e n)", u=2, p=P, e=2)

    with ExitStack() as ctx:
        keep = ctx.enter_context(tc.tile_pool(name="keep", bufs=1))
        x_grouped_pool = ctx.enter_context(tc.tile_pool(name="x_grouped_pool", bufs=3))
        stat_pool = ctx.enter_context(tc.tile_pool(name="stat_pool", bufs=4))
        squares_pool = ctx.enter_context(tc.tile_pool(name="squares_pool", bufs=2))
        n_pool = ctx.enter_context(tc.tile_pool(name="n_pool", bufs=3))
        n_grouped_pool = ctx.enter_context(tc.tile_pool(name="n_grouped_pool", bufs=2))
        n_words_pool = ctx.enter_context(tc.tile_pool(name="n_words_pool", bufs=3))
        kv_pool = ctx.enter_context(tc.tile_pool(name="kv_pool", bufs=4))
        rope_pool = ctx.enter_context(tc.tile_pool(name="rope_pool", bufs=2))
        psum_turn = ctx.enter_context(tc.psum_pool(name="psum_turn", bufs=5))
        psum_latent = ctx.enter_context(tc.psum_pool(name="psum_latent", bufs=3))
        ctx.enter_context(tc.manual_schedule())

        x_rows = []
        for c in range(CHUNKS):
            x_rows.append(keep.tile([P, 4 * D_MODEL], BF16, name="x_rows%d" % c))
        wa_rows = keep.tile([P, 8, LATENT + ROPE], BF16, name="wa_rows")
        wb_rows = keep.tile([P, 4, KV_OUT], BF16, name="wb_rows")
        gain = keep.tile([P, LATENT], BF16, name="gain")

        gain_row = keep.tile([P, LATENT], BF16, name="gain_row")
        nc.gpsimd.memset(gain_row[:].bitcast(I32), 0)
        nc.scalar.dma_start(out=gain_row[0:1, :], in_=kv_norm_w.rearrange("(o n) -> o n", o=1))

        def load_wa(g):
            nc.sync.dma_start(
                out=wa_rows[:, 4 * g : 4 * g + 4, :].rearrange("q (a e) n -> q a (e n)", a=2, e=2),
                in_=wa_view[:, 2 * g : 2 * g + 2, :],
            )

        middle = 2 * D_MODEL
        nc.sync.dma_start(out=x_rows[0][:, 0:middle], in_=x_view[0][:, 0:middle])
        load_wa(0)
        load_wa(1)
        nc.sync.dma_start(out=x_rows[0][:, middle : 2 * middle], in_=x_view[0][:, middle : 2 * middle])
        nc.sync.dma_start(out=x_rows[1][:], in_=x_view[1])
        nc.sync.dma_start(out=wb_rows[:].rearrange("p (u e) n -> p u (e n)", u=2, e=2), in_=wb_view)
        for c in range(2, CHUNKS):
            nc.sync.dma_start(out=x_rows[c][:], in_=x_view[c])

        position_int = keep.tile([P, SEQ_TILES], I32, name="position_int")
        nc.gpsimd.iota(position_int[:], pattern=[[512, 4], [1, 4]], base=0, channel_multiplier=4)
        identity_f32 = keep.tile([P, P], F32, name="identity_f32")
        make_identity(nc, identity_f32[:])
        ones = keep.tile([P, LATENT], BF16, name="ones")
        nc.gpsimd.memset(ones[:], 1.0)
        minus_half = keep.tile([P, 1], F32, name="minus_half")
        nc.vector.memset(minus_half[:], -0.5)
        table_warm = keep.tile([P, 1], F32, name="table_warm")
        nc.scalar.activation(out=table_warm[:], in_=minus_half[:], func=ACT.Sin)

        turns = keep.tile([P, SEQ_TILES, HALF_ROPE], F32, name="turns")
        whole_turns = keep.tile([P, SEQ_TILES, HALF_ROPE], I32, name="whole_turns")
        position_halves = (slice(0, SEQ_TILES // 2), slice(SEQ_TILES // 2, SEQ_TILES))
        ratio = ROPE_BASE ** (-1.0 / HALF_ROPE)
        for i in range(SEEDS):
            nc.vector.tensor_scalar(
                out=turns[:, :, i], in0=position_int[:], scalar1=ratio**i / (2.0 * math.pi), scalar2=None, op0=ALU.mult
            )
        filled = SEEDS
        while filled < HALF_ROPE:
            for half in position_halves:
                nc.vector.tensor_scalar(
                    out=turns[:, half, filled : 2 * filled],
                    in0=turns[:, half, 0:filled],
                    scalar1=ratio**filled,
                    scalar2=None,
                    op0=ALU.mult,
                )
            filled *= 2
        for half in position_halves:
            nc.vector.tensor_copy(out=whole_turns[:, half, :], in_=turns[:, half, :])
        for half in position_halves:
            nc.vector.tensor_tensor(
                out=turns[:, half, :], in0=turns[:, half, :], in1=whole_turns[:, half, :], op=ALU.subtract
            )
        fraction = turns[:].rearrange("p a i -> p (a i)")
        sin_table = keep.tile([P, SEQ_TILES * HALF_ROPE], F32, name="sin_table")
        cos_table = keep.tile([P, SEQ_TILES * HALF_ROPE], F32, name="cos_table")

        def table_fold(half):
            columns = slice(half * HALF_TABLE, half * HALF_TABLE + HALF_TABLE)
            nc.vector.scalar_tensor_tensor(
                out=cos_table[:, columns], in0=fraction[:, columns], scalar=-1.0, in1=fraction[:, columns], op0=ALU.mult, op1=ALU.min
            )

        def table_sin():
            nc.scalar.activation(out=sin_table[:], in_=fraction, func=ACT.Sin, scale=2.0 * math.pi)

        def table_cos():
            nc.scalar.activation(
                out=cos_table[:], in_=cos_table[:], func=ACT.Sin, scale=2.0 * math.pi, bias=0.5 * math.pi
            )

        wa_latent_grouped = keep.tile([P, 2, LATENT, 4], BF16, name="wa_latent_grouped", align_bytes=64)
        wa_rope_grouped = keep.tile([P, 2, ROPE, 4], BF16, name="wa_rope_grouped", align_bytes=64)
        wa_latent_words = keep.tile([P, 2, LATENT], U32, name="wa_latent_words", align_bytes=64)
        wa_latent_plane = keep.tile([P, 2, LATENT], U8, name="wa_latent_plane", align_bytes=64)
        wa_rope_words = keep.tile([P, 2, ROPE], U32, name="wa_rope_words", align_bytes=64)
        wa_rope_plane = keep.tile([P, 2, ROPE], U8, name="wa_rope_plane", align_bytes=64)
        wb_grouped = keep.tile([P, KV_OUT, 4], BF16, name="wb_grouped", align_bytes=64)
        wb_words = keep.tile([P, KV_OUT], U32, name="wb_words", align_bytes=64)
        wb_plane = keep.tile([P, KV_OUT], U8, name="wb_plane", align_bytes=64)

        def regroup_wa_latent(g, first, last, on_vector):
            grouped = wa_latent_grouped[:, g, first:last, :].rearrange("q (c i) t -> q c t i", i=4)
            rows = wa_rows[:, 4 * g : 4 * g + 4, first:last].rearrange("q t (c i) -> q c t i", i=4)
            if on_vector:
                nc.vector.tensor_copy(out=grouped, in_=rows)
            else:
                nc.scalar.copy(out=grouped, in_=rows)

        def quantise_wa_latent(g):
            nc.vector.quantize_mx(
                out=wa_latent_words[:, g, :].bitcast(FP8X4),
                scales=wa_latent_plane[:, g, :],
                in_=wa_latent_grouped[:, g, :, :].rearrange("q n t -> q (n t)"),
            )

        def regroup_wa_rope():
            for g in range(2):
                nc.vector.tensor_copy(
                    out=wa_rope_grouped[:, g, :, :].rearrange("q (c i) t -> q c t i", i=4),
                    in_=wa_rows[:, 4 * g : 4 * g + 4, LATENT : LATENT + ROPE].rearrange("q t (c i) -> q c t i", i=4),
                )

        def quantise_wa_rope():
            for g in range(2):
                nc.vector.quantize_mx(
                    out=wa_rope_words[:, g, :].bitcast(FP8X4),
                    scales=wa_rope_plane[:, g, :],
                    in_=wa_rope_grouped[:, g, :, :].rearrange("q n t -> q (n t)"),
                )

        def regroup_wb(kv):
            for h in range(2):
                first = 256 * kv + 128 * h
                rows = wb_rows[:, :, 256 * h + 128 * kv : 256 * h + 128 * kv + 128]
                nc.vector.tensor_copy(
                    out=wb_grouped[:, first : first + 128, :].rearrange("p (c i) t -> p c t i", i=4),
                    in_=rows.rearrange("p t (c i) -> p c t i", i=4),
                )

        def quantise_wb():
            nc.vector.quantize_mx(
                out=wb_words[:].bitcast(FP8X4), scales=wb_plane[:], in_=wb_grouped[:].rearrange("p n t -> p (n t)")
            )

        def spread_gain():
            bank = psum_turn.tile([P, LATENT], F32, name="turn")
            nc.tensor.matmul(out=bank[:], lhsT=ones[:, 0:P], rhs=gain_row[:], start=True, stop=True)
            nc.scalar.copy(out=gain[:], in_=bank[:])

        def warm_up():
            bank = psum_turn.tile([P, LATENT], F32, name="turn")
            for k in range(WARM_UP):
                nc.tensor.matmul(out=bank[:], lhsT=ones[:, 0:P], rhs=ones[:], start=True, stop=True)

        x_grouped = {}
        x_transposed = {}
        kv_bank = {}
        x_words = {}
        x_plane = {}
        latent = {}
        inv_rms = {}
        n_rows = {}
        n_transposed = {}
        n_grouped = {}
        n_words = {}
        n_plane = {}
        kv_rows = {}
        rope_raw = {}
        rope_parts = {}

        def transpose_x(pair):
            transpose_x_tensor(pair)
            empty_xt(pair, 0)
            empty_xt(pair, 1)

        def transpose_x_tensor(pair):
            words = x_rows[pair // 2][:].bitcast(F32)
            grouped = x_grouped_pool.tile([P, 2 * D_MODEL], BF16, name="x_grouped", align_bytes=64)
            x_grouped[pair] = grouped
            for i in range(2):
                j = 2 * (pair % 2) + i
                xt = psum_turn.tile([P, 4, P], F32, name="turn")
                x_transposed[(pair, i)] = xt
                for block in range(4):
                    first = 512 * j + P * block
                    nc.tensor.transpose(xt[:, block, :], words[:, first : first + P], identity_f32[:])

        def empty_xt(pair, i):
            words = x_grouped[pair][:].bitcast(F32)[:, 512 * i : 512 * i + 512]
            nc.scalar.copy(
                out=words.rearrange("q (g m u) -> q g m u", g=2, m=P, u=2),
                in_=x_transposed[(pair, i)][:].rearrange("q (g u) m -> q g m u", g=2, u=2),
            )

        def quantise_x(pair):
            words = keep.tile([P, 4 * P], U32, name="x_words%d" % pair, align_bytes=64)
            plane = keep.tile([P, 4 * P], U8, name="x_plane%d" % pair, align_bytes=64)
            x_words[pair] = words
            x_plane[pair] = plane
            nc.vector.quantize_mx(out=words[:].bitcast(FP8X4), scales=plane[:], in_=x_grouped[pair][:])

        def x_operand(pair, i, g):
            columns = slice(256 * i + P * g, 256 * i + P * g + P)
            return x_words[pair][:, columns].bitcast(FP8X4), x_plane[pair][:, columns]

        def stage1(pair, i):
            if pair in (0, PAIRS - 1):
                bank = psum_turn.tile([P, LATENT], F32, name="turn")
            else:
                bank = psum_latent.tile([P, LATENT], F32, name="latent")
            latent[(pair, i)] = bank
            for g in range(2):
                words, plane = x_operand(pair, i, g)
                nc.tensor.matmul_mx(
                    out=bank[:],
                    lhsT=words,
                    lhsT_scale=plane,
                    rhs=wa_latent_words[:, g, :].bitcast(FP8X4),
                    rhs_scale=wa_latent_plane[:, g, :],
                    start=(g == 0),
                    stop=(g == 1),
                )

        def rms(pair, i):
            bank = latent[(pair, i)]
            square_sum = stat_pool.tile([P, 1], F32, name="square_sum")
            squares = squares_pool.tile([P, LATENT], BF16, name="squares")
            nc.scalar.activation(out=squares[:], in_=bank[:], func=ACT.Square, accum_out=square_sum[:])
            mean_square = stat_pool.tile([P, 1], F32, name="mean_square")
            nc.gpsimd.tensor_scalar(
                out=mean_square[:],
                in0=square_sum[:],
                scalar1=1.0 / LATENT,
                scalar2=RMS_EPS,
                op0=ALU.mult,
                op1=ALU.add,
            )
            inverse = stat_pool.tile([P, 1], F32, name="inv_rms")
            inv_rms[(pair, i)] = inverse
            nc.gpsimd.tensor_tensor(out=inverse[:], in0=mean_square[:], in1=minus_half[:], op=ALU.pow)

        def norm(pair, i):
            if i == 0:
                rows = n_pool.tile([P, 2, LATENT], BF16, name="n_rows")
                n_rows[pair] = rows
            nc.vector.scalar_tensor_tensor(
                out=n_rows[pair][:, i, :],
                in0=latent[(pair, i)][:],
                scalar=inv_rms[(pair, i)][:],
                in1=gain[:],
                op0=ALU.mult,
                op1=ALU.mult,
            )

        def transpose_n(pair):
            bank = psum_turn.tile([P, 2, 2, P], F32, name="turn")
            n_transposed[pair] = bank
            words = n_rows[pair][:].rearrange("p i n -> p (i n)").bitcast(F32)
            for i in range(2):
                for u in range(2):
                    first = 256 * i + P * u
                    nc.tensor.transpose(bank[:, i, u, :], words[:, first : first + P], identity_f32[:])

        def group_n(pair):
            grouped = n_grouped_pool.tile([P, 8 * P], BF16, name="n_grouped", align_bytes=64)
            n_grouped[pair] = grouped
            grouped_words = grouped[:].bitcast(F32).rearrange("p (i m u) -> p i m u", i=2, m=P, u=2)
            words = n_transposed[pair][:].rearrange("p i u m -> p i m u")
            if pair >= PAIRS - 2:
                nc.scalar.copy(out=grouped_words, in_=words)
            else:
                nc.vector.tensor_copy(out=grouped_words, in_=words)

        def quantise_n(pair):
            words = n_words_pool.tile([P, 2 * P], U32, name="n_words", align_bytes=64)
            plane = n_words_pool.tile([P, 2 * P], U8, name="n_plane", align_bytes=64)
            n_words[pair] = words
            n_plane[pair] = plane
            nc.vector.quantize_mx(
                out=words[:].bitcast(FP8X4), scales=plane[:], in_=n_grouped[pair][:]
            )

        def stage2(pair, i):
            if i == 0:
                rows = kv_pool.tile([P, 2, 2, 256], F32, name="kv_rows")
                kv_rows[pair] = rows
            bank = psum_turn.tile([P, KV_OUT], F32, name="turn")
            columns = slice(P * i, P * i + P)
            nc.tensor.matmul_mx(
                out=bank[:],
                lhsT=n_words[pair][:, columns].bitcast(FP8X4),
                lhsT_scale=n_plane[pair][:, columns],
                rhs=wb_words[:].bitcast(FP8X4),
                rhs_scale=wb_plane[:],
                start=True,
                stop=True,
            )
            kv_bank[(pair, i)] = bank

        def empty_kv_part(pair):
            values = kv_bank[(pair, 1)][:].rearrange("p (kv n) -> p kv n", kv=2)
            nc.vector.tensor_copy(out=kv_rows[pair][:, :, 1, KV_SPLIT:256], in_=values[:, :, KV_SPLIT:256])

        def store_kv(pair, i):
            c = pair // 2
            rows = kv_rows[pair]
            bank = kv_bank[(pair, i)]
            values = bank[:].rearrange("p (kv n) -> p kv n", kv=2)
            if pair == PAIRS - 1 and i == 1:
                nc.vector.tensor_copy(out=rows[:, :, i, :], in_=values)
            elif i == 1:
                nc.scalar.copy(out=rows[:, :, i, 0:KV_SPLIT], in_=values[:, :, 0:KV_SPLIT])
            else:
                nc.scalar.copy(out=rows[:, :, i, :], in_=values)
            j = 2 * (pair % 2)
            if pair == PAIRS - 1:
                nc.sync.dma_start(out=k_nope_view[c][:, j + i, :], in_=rows[:, 0, i, :])
                nc.sync.dma_start(out=v_view[c][:, j + i, :], in_=rows[:, 1, i, :])
            elif i == 1:
                nc.sync.dma_start(out=k_nope_view[c][:, j : j + 2, :], in_=rows[:, 0, :, :])
                nc.sync.dma_start(out=v_view[c][:, j : j + 2, :], in_=rows[:, 1, :, :])

        def rope_product(pair):
            bank = psum_turn.tile([P, 2, ROPE], F32, name="turn")
            rope_raw[pair] = bank
            for i in range(2):
                for g in range(2):
                    words, plane = x_operand(pair, i, g)
                    nc.tensor.matmul_mx(
                        out=bank[:, i, :],
                        lhsT=words,
                        lhsT_scale=plane,
                        rhs=wa_rope_words[:, g, :].bitcast(FP8X4),
                        rhs_scale=wa_rope_plane[:, g, :],
                        start=(g == 0),
                        stop=(g == 1),
                    )

        def rope_rotation(pair):
            count = 2 * HALF_ROPE
            first = count * (pair % 8)
            raw = rope_raw[pair][:].rearrange("p i (f two) -> p (i f) two", two=2)
            cos = cos_table[:, first : first + count]
            sin = sin_table[:, first : first + count]
            with_cos = rope_pool.tile([P, count, 2], F32, name="with_cos")
            with_sin = rope_pool.tile([P, 2, count], F32, name="with_sin")
            rope_parts[pair] = (with_cos, with_sin)
            nc.vector.tensor_tensor(out=with_cos[:], in0=raw, in1=cos.unsqueeze(2).to_broadcast([P, count, 2]), op=ALU.mult)
            nc.vector.scalar_tensor_tensor(
                out=with_sin[:, 0, :], in0=raw[:, :, 1], scalar=-1.0, in1=sin, op0=ALU.mult, op1=ALU.mult
            )
            nc.vector.tensor_tensor(out=with_sin[:, 1, :], in0=raw[:, :, 0], in1=sin, op=ALU.mult)

        def rope_sum(pair):
            count = 2 * HALF_ROPE
            with_cos, with_sin = rope_parts[pair]
            rotated = rope_pool.tile([P, count, 2], F32, name="rotated")
            adder = nc.vector if pair >= PAIRS - 2 else nc.gpsimd
            adder.tensor_tensor(
                out=rotated[:], in0=with_cos[:], in1=with_sin[:].rearrange("p two n -> p n two"), op=ALU.add
            )
            first = 2 * ROPE * (pair % 2)
            nc.sync.dma_start(
                out=k_rope_view[pair // 2][:, first : first + 2 * ROPE], in_=rotated[:].rearrange("p n two -> p (n two)")
            )

        def live(pair):
            return 0 <= pair < PAIRS

        transpose_x(0)
        warm_up()
        regroup_wa_latent(0, WA_SPLIT[0], LATENT, False)
        regroup_wa_latent(0, 0, WA_SPLIT[0], True)
        quantise_x(0)
        quantise_wa_latent(0)
        regroup_wa_latent(1, WA_SPLIT[1], LATENT, False)
        regroup_wa_latent(1, 0, WA_SPLIT[1], True)
        transpose_x(1)
        spread_gain()
        quantise_wa_latent(1)
        table_fold(0)
        quantise_x(1)
        for r in range(PAIRS + 3):
            if r > 0 and live(r + 1):
                transpose_x_tensor(r + 1)
                empty_xt(r + 1, 0)
            if r == PAIRS - 1:
                for i in range(2):
                    stage1(r, i)
                    rms(r, i)
            if live(r - 2):
                transpose_n(r - 2)
            if r > 0 and live(r + 1):
                empty_xt(r + 1, 1)
            if r == 0:
                table_fold(1)
                regroup_wa_rope()
                quantise_wa_rope()
            if live(r - 1):
                norm(r - 1, 0)
            if r < PAIRS - 1:
                stage1(r, 0)
                rms(r, 0)
            if r == 1:
                table_sin()
            if live(r - 3):
                stage2(r - 3, 0)
                stage2(r - 3, 1)
            if live(r - 2):
                group_n(r - 2)
            if r == 2:
                quantise_wb()
            if live(r - 3):
                store_kv(r - 3, 0)
            if r > 0 and live(r + 1):
                quantise_x(r + 1)
            if live(r - 3) and r < PAIRS + 2:
                empty_kv_part(r - 3)
            if r < PAIRS - 1:
                stage1(r, 1)
                rms(r, 1)
            if live(r - 1):
                norm(r - 1, 1)
            if r == 1:
                table_cos()
                regroup_wb(0)
                regroup_wb(1)
            if live(r - 2):
                quantise_n(r - 2)
                rope_product(r - 2)
                rope_rotation(r - 2)
            if live(r - 3):
                store_kv(r - 3, 1)
            if live(r - 2):
                rope_sum(r - 2)
